import numpy as np
import ml_dtypes


def mxq(x, axis, fmt="e4m3"):
    dtype, down = {"e4m3": (ml_dtypes.float8_e4m3fn, 7), "e5m2": (ml_dtypes.float8_e5m2, 14)}[fmt]
    v = np.moveaxis(np.asarray(x, np.float32).astype(ml_dtypes.bfloat16).astype(np.float64), axis, -1)
    blocks = v.reshape(v.shape[:-1] + (-1, 32))
    amax = np.abs(blocks).max(-1, keepdims=True)
    byte = np.maximum(np.where(amax > 0, np.frexp(amax)[1] - 1 + 127, 0) - down, 1)
    scale = np.exp2(byte - 127.0)
    codes = (blocks / scale).astype(np.float32).astype(dtype).astype(np.float64)
    return np.moveaxis((codes * scale).reshape(v.shape), -1, axis)


WIDE = False


def mx_kscale(k):
    if not WIDE:
        return np.ones(k)
    levels = np.array([10, -10, 5, -5, 0])
    a = np.random.permutation(np.resize(levels, k // 512 * 4)).reshape(k // 512, 4)
    idx = np.arange(k)
    return np.exp2(a[idx // 512, idx % 128 // 32])


BF16 = ml_dtypes.bfloat16


def bf(x):
    return np.asarray(x, np.float32).astype(BF16)


def f64(x):
    return np.asarray(x).astype(np.float64)


N, K, DN, DE, DT, H, DOUT = 512, 20, 384, 512, 128, 2, 128
DH = DOUT // H
C = DN + DE + DT
CO = DOUT + DN
VS = 1.8
TS = 1.5
LN_EPS = 1e-5


def setup_inputs():
    g = np.random.standard_normal
    s = np.concatenate([mx_kscale(C)[:DN + DE], np.ones(DT)])
    u = mx_kscale(CO)
    t, sr = u[:DOUT], u[DOUT:]
    a = 1.4 * g((N, K, H))
    a = np.where(a >= 0.0, a, 0.2 * a)
    e = np.exp(a - a.max(axis=1, keepdims=True))
    return {
        "att": bf(e / e.sum(axis=1, keepdims=True)),
        "root_node_feature": bf(g((N, DN)) * sr),
        "root_ts": bf(np.random.uniform(size=N) * TS + TS),
        "neighbor_ts": bf(np.random.uniform(size=(N, K)) * TS),
        "neighbor_node_feature": bf(g((N, K, DN)) * s[:DN]),
        "neighbor_edge_feature": bf(g((N, K, DE)) * s[DN:DN + DE]),
        "time_w": bf((10.0 ** -np.linspace(0.0, 1.0, DT) * (1.0 + 0.1 * g(DT))).reshape(DT, 1)),
        "time_b": bf(0.2 * g(DT)),
        "wv_w": bf(g((DOUT, C)) * VS / np.sqrt(C) / s[None, :] * t[:, None]),
        "wv_b": bf(0.3 * g(DOUT) * t),
        "wo_w": bf(g((DOUT, CO)) / np.sqrt(CO) / u[None, :]),
        "wo_b": bf(0.3 * g(DOUT)),
        "ln_g": bf(1.0 + 0.1 * g(DOUT)),
        "ln_b": bf(0.1 * g(DOUT)),
    }


def reference(att, root_node_feature, root_ts, neighbor_ts, neighbor_node_feature, neighbor_edge_feature, time_w, time_b, wv_w, wv_b, wo_w, wo_b, ln_g, ln_b):
    n, k = neighbor_ts.shape
    tw, tb = f64(time_w)[:, 0], f64(time_b)
    dt = f64(root_ts)[:, None] - f64(neighbor_ts)
    edge_tf = np.cos(dt[..., None] * tw + tb)
    kv_in = np.concatenate([f64(neighbor_node_feature), f64(neighbor_edge_feature), edge_tf], axis=-1).reshape(n * k, C)
    h_v = (mxq(kv_in, 1, "e4m3") @ mxq(f64(wv_w), 1, "e4m3").T) + f64(wv_b)
    h_neigh = np.sum(h_v.reshape(n, k, H, DH) * f64(att)[..., None], axis=1).reshape(n, DOUT)
    cat = np.concatenate([h_neigh, f64(root_node_feature)], axis=1)
    h_out = (mxq(cat, 1, "e4m3") @ mxq(f64(wo_w), 1, "e4m3").T) + f64(wo_b)
    h_out = np.maximum(h_out, 0.0)
    mu = h_out.mean(axis=-1, keepdims=True)
    var = ((h_out - mu) ** 2).mean(axis=-1, keepdims=True)
    return (h_out - mu) / np.sqrt(var + LN_EPS) * f64(ln_g) + f64(ln_b)

@@ -1,0 +1,370 @@
+import math
+from contextlib import ExitStack
+
+import concourse.mybir as mybir
+from concourse.masks import make_identity
+
+F32 = mybir.dt.float32
+BF16 = mybir.dt.bfloat16
+I32 = mybir.dt.int32
+U32 = mybir.dt.uint32
+U8 = mybir.dt.uint8
+FP8X4 = mybir.dt.float8_e4m3fn_x4
+ALU = mybir.AluOpType
+ACT = mybir.ActivationFunctionType
+AX = mybir.AxisListType
+
+P = 128
+N_NODES, N_NEIGH, D_NODE, D_EDGE, D_TIME, HEADS, D_OUT = 512, 20, 384, 512, 128, 2, 128
+D_HEAD = D_OUT // HEADS
+K1 = D_NODE + D_EDGE + D_TIME
+D_FEAT = D_NODE + D_EDGE
+NPP = N_NODES // P
+TILES = NPP * N_NEIGH
+QUAD = 4
+GROUPS = TILES // QUAD
+GPN = N_NEIGH // QUAD
+BATCH = 4
+BATCHES = GROUPS // BATCH
+NX = 6
+LN_EPS = 1e-5
+TWO_PI = 2.0 * math.pi
+
+FLOPS = 2 * N_NODES * N_NEIGH * K1 * D_OUT + 2 * N_NODES * (D_OUT + D_NODE) * D_OUT
+
+
+def tile_transformeraggregator_pb_kernel(
+    tc, att, root_node_feature, root_ts, neighbor_ts, neighbor_node_feature, neighbor_edge_feature,
+    time_w, time_b, wv_w, wv_b, wo_w, wo_b, ln_g, ln_b, out,
+):
+    nc = tc.nc
+    with ExitStack() as ctx:
+        const = ctx.enter_context(tc.tile_pool(name="const", bufs=1))
+        xpool = ctx.enter_context(tc.tile_pool(name="xpool", bufs=1))
+        gpool = ctx.enter_context(tc.tile_pool(name="gpool", bufs=3))
+        cpool = ctx.enter_context(tc.tile_pool(name="cpool", bufs=2))
+        spool = ctx.enter_context(tc.tile_pool(name="spool", bufs=2))
+        tp_pool = ctx.enter_context(tc.psum_pool(name="tp", bufs=4))
+        mo_pool = ctx.enter_context(tc.psum_pool(name="mo", bufs=2))
+        ms_pool = ctx.enter_context(tc.psum_pool(name="ms", bufs=2))
+
+        node_v = neighbor_node_feature.rearrange("(p a) j c -> p (a j) c", a=NPP)
+        edge_v = neighbor_edge_feature.rearrange("(p a) j c -> p (a j) c", a=NPP)
+        out_v = out.rearrange("(p a) c -> p a c", a=NPP)
+
+        ident_f = const.tile([P, P], F32, name="ident_f")
+        make_identity(nc, ident_f[:])
+        ident_b = const.tile([P, P], BF16, name="ident_b")
+        make_identity(nc, ident_b[:])
+
+        xq = [xpool.tile([P, QUAD, K1], BF16, name="xq%d" % k) for k in range(NX)]
+
+        def load(g):
+            x = xq[g % NX]
+            nc.sync.dma_start(out=x[:, :, 0:D_NODE], in_=node_v[:, QUAD * g:QUAD * (g + 1), :])
+            nc.sync.dma_start(out=x[:, :, D_NODE:D_FEAT], in_=edge_v[:, QUAD * g:QUAD * (g + 1), :])
+
+        nts = const.tile([P, TILES], BF16, name="nts")
+        nc.scalar.dma_start(out=nts[:], in_=neighbor_ts.rearrange("(p a) j -> p (a j)", a=NPP))
+        rts = const.tile([P, NPP], BF16, name="rts")
+        nc.scalar.dma_start(out=rts[:], in_=root_ts.rearrange("(p a) -> p a", a=NPP))
+        tb8 = const.tile([P, P], BF16, name="tb8")
+        nc.vector.memset(tb8[:], 0.0)
+        nc.scalar.dma_start(
+            out=tb8[0:4, :].rearrange("t (r q) -> t r q", r=4),
+            in_=time_w.rearrange("(t q) o -> t o q", t=4).to_broadcast([4, 4, 32]),
+        )
+        nc.scalar.dma_start(
+            out=tb8[4:8, :].rearrange("t (r q) -> t r q", r=4),
+            in_=time_b.rearrange("(t o q) -> t o q", t=4, o=1).to_broadcast([4, 4, 32]),
+        )
+        load(0)
+        wvz = const.tile([P, K1], BF16, name="wvz")
+        nc.vector.memset(wvz[:, D_FEAT:K1], 0.0)
+        nc.scalar.dma_start(out=wvz[:, 0:D_FEAT], in_=wv_w[:, 0:D_FEAT])
+        wcos = const.tile([P, D_TIME], BF16, name="wcos")
+        nc.scalar.dma_start(out=wcos[:], in_=wv_w[:, D_FEAT:K1])
+        att_b = const.tile([P, TILES * HEADS], BF16, name="att_b")
+        nc.scalar.dma_start(out=att_b[:], in_=att.rearrange("(p a) j h -> p (a j h)", a=NPP))
+        for k in range(NX):
+            nc.gpsimd.memset(xq[k][:, :, D_FEAT:K1], 0.0)
+        for g in range(1, NX):
+            load(g)
+
+        wvb = const.tile([P, D_OUT], BF16, name="wvb")
+        nc.gpsimd.dma_start(out=wvb[:], in_=wv_b.partition_broadcast(P))
+        wo_sb = const.tile([P, D_OUT + D_NODE], BF16, name="wo_sb")
+        nc.gpsimd.dma_start(out=wo_sb[:], in_=wo_w)
+        rootf = const.tile([P, NPP, D_NODE], BF16, name="rootf")
+        nc.gpsimd.dma_start(out=rootf[:], in_=root_node_feature.rearrange("(p a) c -> p a c", a=NPP))
+        wob = const.tile([P, D_OUT], BF16, name="wob")
+        nc.gpsimd.dma_start(out=wob[:], in_=wo_b.partition_broadcast(P))
+        lng = const.tile([P, D_OUT], BF16, name="lng")
+        nc.gpsimd.dma_start(out=lng[:], in_=ln_g.partition_broadcast(P))
+        lnb = const.tile([P, D_OUT], BF16, name="lnb")
+        nc.gpsimd.dma_start(out=lnb[:], in_=ln_b.partition_broadcast(P))
+
+        def transpose_row_tile(words):
+            tp = tp_pool.tile([P, 4, P], F32, name="tp")
+            for c in range(4):
+                nc.tensor.transpose(tp[:, c, :], words[:, P * c:P * (c + 1)], ident_f[:])
+            return tp
+
+        def evacuate(dst_words, tp):
+            nc.scalar.copy(
+                out=dst_words.rearrange("p (g w u) -> p g w u", g=2, u=2),
+                in_=tp[:].rearrange("p (g u) w -> p g w u", g=2),
+            )
+
+        dt_rows = const.tile([P, TILES], F32, name="dt_rows")
+        nc.vector.tensor_tensor(
+            out=dt_rows[:].rearrange("p (a j) -> p a j", a=NPP),
+            in0=rts[:].unsqueeze(2).to_broadcast([P, NPP, N_NEIGH]),
+            in1=nts[:].rearrange("p (a j) -> p a j", a=NPP),
+            op=ALU.subtract,
+        )
+        dt_rep = const.tile([P, TILES, 32], F32, name="dt_rep")
+        dtq = const.tile([P, GROUPS * P], F32, name="dtq")
+        TB = QUAD * BATCH
+
+        def spread_dt(b):
+            nc.vector.tensor_copy(
+                out=dt_rep[:, TB * b:TB * (b + 1), :],
+                in_=dt_rows[:, TB * b:TB * (b + 1)].unsqueeze(2).to_broadcast([P, TB, 32]),
+            )
+            tpd = tp_pool.tile([P, 4, P], F32, name="tp")
+            for q in range(BATCH):
+                g = BATCH * b + q
+                nc.tensor.transpose(
+                    tpd[:, q, :], dt_rep[:, QUAD * g:QUAD * (g + 1), :].rearrange("p i c -> p (i c)"), ident_f[:]
+                )
+            nc.scalar.copy(out=dtq[:, 512 * b:512 * (b + 1)], in_=tpd[:].rearrange("p q w -> p (q w)"))
+
+        spread_dt(0)
+
+        ps8 = ms_pool.tile([P, P], BF16, name="ms")
+        nc.tensor.transpose(ps8[:], tb8[:], ident_b[:])
+        a_q = const.tile([P, 4], F32, name="a_q")
+        nc.vector.tensor_scalar(out=a_q[:], in0=ps8[:, 0:4], scalar1=1.0 / TWO_PI, scalar2=None, op0=ALU.mult)
+        b_q = const.tile([P, 4], F32, name="b_q")
+        nc.vector.tensor_scalar(out=b_q[:], in0=ps8[:, 4:8], scalar1=1.0 / TWO_PI, scalar2=0.25,
+                                op0=ALU.mult, op1=ALU.add)
+        b_2 = const.tile([P, 4], F32, name="b_2")
+        nc.vector.tensor_scalar(out=b_2[:], in0=ps8[:, 4:8], scalar1=0.5 * math.pi, scalar2=None, op0=ALU.add)
+
+        cos_state = {}
+
+        def cos_open(b):
+            turns = cpool.tile([P, 4, 512], I32, name="turns")
+            frac = cpool.tile([P, 4, 512], F32, name="frac")
+            planes = cpool.tile([P, 4, 512], BF16, name="planes")
+            cos_state[b] = (turns, frac, planes)
+
+        def cos_plane(b, t):
+            turns, frac, planes = cos_state[b]
+            d = dtq[:, 512 * b:512 * (b + 1)]
+            nc.vector.tensor_scalar(out=turns[:, t, :], in0=d, scalar1=a_q[:, t:t + 1], scalar2=b_q[:, t:t + 1],
+                                    op0=ALU.mult, op1=ALU.add)
+            nc.vector.scalar_tensor_tensor(out=frac[:, t, :], in0=d, scalar=a_q[:, t:t + 1], in1=turns[:, t, :],
+                                           op0=ALU.mult, op1=ALU.subtract)
+            nc.scalar.activation(out=planes[:, t, :], in_=frac[:, t, :], func=ACT.Sin,
+                                 bias=b_2[:, t:t + 1], scale=TWO_PI)
+
+        cos_codes = {}
+
+        def cos_close(b):
+            planes = cos_state[b][2]
+            cos_g = cpool.tile([P, 2048], BF16, name="cos_g", align_bytes=64)
+            nc.vector.tensor_copy(
+                out=cos_g[:].rearrange("p (c i t) -> p c t i", i=4, t=4),
+                in_=planes[:].rearrange("p t (c i) -> p c t i", i=4),
+            )
+            cc = cpool.tile([P, 512], U32, name="cc", align_bytes=64)
+            cs = cpool.tile([P, 512], U8, name="cs", align_bytes=64)
+            nc.vector.quantize_mx(out=cc[:].bitcast(FP8X4), scales=cs[:], in_=cos_g[:])
+            cos_codes[b] = (cc, cs)
+
+        cos_open(0)
+        for t in range(4):
+            cos_plane(0, t)
+
+        tpw = transpose_row_tile(wvz[:].bitcast(F32))
+        gw = const.tile([P, K1], BF16, name="gw", align_bytes=64)
+        evacuate(gw[:].bitcast(F32), tpw)
+        wvc = const.tile([P, 256], U32, name="wvc", align_bytes=64)
+        wvs = const.tile([P, 256], U8, name="wvs", align_bytes=64)
+        nc.vector.quantize_mx(out=wvc[:].bitcast(FP8X4), scales=wvs[:], in_=gw[:])
+
+        wcr = const.tile([P, 4, 4, 32], BF16, name="wcr")
+        nc.vector.tensor_copy(
+            out=wcr[:],
+            in_=wcos[:].rearrange("p (t q) -> p t q", t=4).unsqueeze(2).to_broadcast([P, 4, 4, 32]),
+        )
+        pw = ms_pool.tile([P, 4, P], BF16, name="ms")
+        for t in range(4):
+            nc.tensor.transpose(pw[:, t, :], wcr[:, t, :, :].rearrange("p r q -> p (r q)"), ident_b[:])
+        wcm = const.tile([P, 4, 512], BF16, name="wcm", align_bytes=64)
+        nc.vector.memset(wcm[:].bitcast(I32), 0)
+        for r in range(4):
+            nc.scalar.copy(
+                out=wcm[32 * r:32 * (r + 1), r, :].rearrange("p (c t) -> p c t", t=4),
+                in_=pw[32 * r:32 * (r + 1), :, :].rearrange("p t c -> p c t"),
+            )
+        wcc = const.tile([P, 512], U32, name="wcc", align_bytes=64)
+        wcs = const.tile([P, 512], U8, name="wcs", align_bytes=64)
+        nc.vector.quantize_mx(out=wcc[:].bitcast(FP8X4), scales=wcs[:],
+                              in_=wcm[:].rearrange("p r c -> p (r c)"))
+
+        cos_close(0)
+
+        att_f = const.tile([P, TILES * HEADS], F32, name="att_f")
+        nc.vector.tensor_copy(out=att_f[:], in_=att_b[:])
+        att_sum = const.tile([P, NPP * HEADS], F32, name="att_sum")
+        nc.vector.tensor_reduce(
+            out=att_sum[:].rearrange("p (a h) -> p a h", a=NPP),
+            in_=att_f[:].rearrange("p (a j h) -> p a h j", a=NPP, j=N_NEIGH),
+            axis=AX.X, op=ALU.add,
+        )
+        m_half = const.tile([P, 1], F32, name="m_half")
+        nc.vector.memset(m_half[:], -0.5)
+
+        pwo = ms_pool.tile([P, 4, P], BF16, name="ms")
+        for t in range(4):
+            nc.tensor.transpose(pwo[:, t, :], wo_sb[:, P * t:P * (t + 1)], ident_b[:])
+        gwo = const.tile([P, 512], BF16, name="gwo", align_bytes=64)
+        nc.scalar.copy(out=gwo[:].rearrange("p (c t) -> p c t", t=4), in_=pwo[:].rearrange("p t c -> p c t"))
+        woc = const.tile([P, P], U32, name="woc", align_bytes=64)
+        wos = const.tile([P, P], U8, name="wos", align_bytes=64)
+        nc.vector.quantize_mx(out=woc[:].bitcast(FP8X4), scales=wos[:], in_=gwo[:])
+
+        for b in range(1, BATCHES):
+            spread_dt(b)
+
+        grouped = {}
+        codes = {}
+        sums = {}
+        accs = {}
+        pb = const.tile([P, NPP, D_OUT], BF16, name="pb")
+
+        def stage_t(g):
+            xw = xq[g % NX][:].bitcast(F32)
+            gq = gpool.tile([P, QUAD * K1], BF16, name="gq", align_bytes=64)
+            gqw = gq[:].bitcast(F32)
+            for r in range(QUAD):
+                tp = transpose_row_tile(xw[:, r, :])
+                evacuate(gqw[:, 512 * r:512 * (r + 1)], tp)
+            grouped[g] = gq
+
+        def stage_q(g):
+            gq = grouped[g]
+            cq = gpool.tile([P, QUAD * 256], U32, name="cq", align_bytes=64)
+            sq = gpool.tile([P, QUAD * 256], U8, name="sq", align_bytes=64)
+            for hlf in range(2):
+                nc.vector.quantize_mx(
+                    out=cq[:, 512 * hlf:512 * (hlf + 1)].bitcast(FP8X4),
+                    scales=sq[:, 512 * hlf:512 * (hlf + 1)],
+                    in_=gq[:, 2048 * hlf:2048 * (hlf + 1)],
+                )
+            codes[g] = (cq, sq)
+
+        def stage_m(g):
+            cq, sq = codes[g]
+            cc, cs = cos_codes[g // BATCH]
+            cw = P * (g % BATCH)
+            mo = mo_pool.tile([P, QUAD, D_OUT], F32, name="mo")
+            for r in range(QUAD):
+                for ps in range(2):
+                    s = 256 * r + P * ps
+                    nc.tensor.matmul_mx(
+                        out=mo[:, r, :],
+                        lhsT=cq[:, s:s + P].bitcast(FP8X4), lhsT_scale=sq[:, s:s + P],
+                        rhs=wvc[:, P * ps:P * (ps + 1)].bitcast(FP8X4), rhs_scale=wvs[:, P * ps:P * (ps + 1)],
+                        start=(ps == 0), stop=False,
+                    )
+                nc.tensor.matmul_mx(
+                    out=mo[:, r, :],
+                    lhsT=cc[:, cw:cw + P].bitcast(FP8X4), lhsT_scale=cs[:, cw:cw + P],
+                    rhs=wcc[:, P * r:P * (r + 1)].bitcast(FP8X4), rhs_scale=wcs[:, P * r:P * (r + 1)],
+                    start=False, stop=True,
+                )
+            sums[g] = mo
+
+        def stage_p(g):
+            mo = sums[g]
+            a = g // GPN
+            if g % GPN == 0:
+                acc_new = spool.tile([P, QUAD, D_OUT], F32, name="acc")
+                accs[a] = acc_new
+            acc = accs[a]
+            for r in range(QUAD):
+                i = QUAD * g + r
+                for h in range(HEADS):
+                    cols = slice(D_HEAD * h, D_HEAD * (h + 1))
+                    w = att_f[:, HEADS * i + h:HEADS * i + h + 1]
+                    if g % GPN == 0:
+                        nc.vector.tensor_scalar(out=acc[:, r, cols], in0=mo[:, r, cols], scalar1=w, scalar2=None,
+                                                op0=ALU.mult)
+                    else:
+                        nc.vector.scalar_tensor_tensor(out=acc[:, r, cols], in0=mo[:, r, cols], scalar=w,
+                                                       in1=acc[:, r, cols], op0=ALU.mult, op1=ALU.add)
+            if g % GPN == GPN - 1:
+                output_stage(a)
+
+        def output_stage(a):
+            acc = accs[a]
+            red = spool.tile([P, D_OUT], F32, name="red")
+            nc.vector.tensor_reduce(out=red[:], in_=acc[:].rearrange("p r c -> p c r"), axis=AX.X, op=ALU.add)
+            for h in range(HEADS):
+                cols = slice(D_HEAD * h, D_HEAD * (h + 1))
+                nc.vector.scalar_tensor_tensor(
+                    out=pb[:, a, cols], in0=wvb[:, cols], scalar=att_sum[:, HEADS * a + h:HEADS * a + h + 1],
+                    in1=red[:, cols], op0=ALU.mult, op1=ALU.add,
+                )
+            ps2 = ms_pool.tile([P, 4, P], BF16, name="ms")
+            nc.tensor.transpose(ps2[:, 0, :], pb[:, a, :], ident_b[:])
+            for c in range(3):
+                nc.tensor.transpose(ps2[:, 1 + c, :], rootf[:, a, P * c:P * (c + 1)], ident_b[:])
+            g2 = spool.tile([P, 512], BF16, name="g2", align_bytes=64)
+            nc.scalar.copy(out=g2[:].rearrange("p (w t) -> p w t", t=4), in_=ps2[:].rearrange("p t w -> p w t"))
+            c2 = spool.tile([P, P], U32, name="c2", align_bytes=64)
+            s2 = spool.tile([P, P], U8, name="s2", align_bytes=64)
+            nc.vector.quantize_mx(out=c2[:].bitcast(FP8X4), scales=s2[:], in_=g2[:])
+            o2 = ms_pool.tile([P, D_OUT], F32, name="ms")
+            nc.tensor.matmul_mx(out=o2[:], lhsT=c2[:].bitcast(FP8X4), lhsT_scale=s2[:],
+                                rhs=woc[:].bitcast(FP8X4), rhs_scale=wos[:], start=True, stop=True)
+            hid = spool.tile([P, D_OUT], F32, name="hid")
+            nc.vector.tensor_tensor(out=hid[:], in0=o2[:], in1=wob[:], op=ALU.add)
+            nc.vector.tensor_scalar_max(out=hid[:], in0=hid[:], scalar1=0.0)
+            stats = spool.tile([P, 6], F32, name="stats")
+            nc.vector.bn_stats(out=stats[:], in_=hid[:])
+            mv = spool.tile([P, 2], F32, name="mv")
+            nc.vector.bn_aggr(out=mv[:], in_=stats[:])
+            ve = spool.tile([P, 1], F32, name="ve")
+            nc.vector.tensor_scalar_add(out=ve[:], in0=mv[:, 1:2], scalar1=LN_EPS)
+            rstd = spool.tile([P, 1], F32, name="rstd")
+            nc.gpsimd.tensor_tensor(out=rstd[:], in0=ve[:], in1=m_half[:], op=ALU.pow)
+            res = spool.tile([P, D_OUT], F32, name="res")
+            nc.vector.tensor_scalar(out=res[:], in0=hid[:], scalar1=mv[:, 0:1], scalar2=rstd[:],
+                                    op0=ALU.subtract, op1=ALU.mult)
+            nc.vector.tensor_tensor(out=res[:], in0=res[:], in1=lng[:], op=ALU.mult)
+            nc.vector.tensor_tensor(out=res[:], in0=res[:], in1=lnb[:], op=ALU.add)
+            nc.sync.dma_start(out=out_v[:, a, :], in_=res[:])
+
+        for s in range(GROUPS + 2):
+            if s < GROUPS:
+                stage_t(s)
+                if s + NX < GROUPS:
+                    load(s + NX)
+            if 1 <= s <= GROUPS:
+                stage_q(s - 1)
+            b_next, t_next = s // BATCH + 1, s % BATCH
+            if b_next < BATCHES:
+                if t_next == 0:
+                    cos_open(b_next)
+                cos_plane(b_next, t_next)
+            if s % BATCH == 0 and 1 <= s // BATCH < BATCHES:
+                cos_close(s // BATCH)
+            if 1 <= s <= GROUPS:
+                stage_m(s - 1)
+            if s >= 2:
+                stage_p(s - 2)

@@ -39,6 +39,7 @@ def tile_transformeraggregator_pb_kernel(
 ):
     nc = tc.nc
     with ExitStack() as ctx:
+        ctx.enter_context(tc.manual_schedule())
         const = ctx.enter_context(tc.tile_pool(name="const", bufs=1))
         xpool = ctx.enter_context(tc.tile_pool(name="xpool", bufs=1))
         gpool = ctx.enter_context(tc.tile_pool(name="gpool", bufs=3))
@@ -64,12 +65,19 @@ def tile_transformeraggregator_pb_kernel(
             nc.sync.dma_start(out=x[:, :, 0:D_NODE], in_=node_v[:, QUAD * g:QUAD * (g + 1), :])
             nc.sync.dma_start(out=x[:, :, D_NODE:D_FEAT], in_=edge_v[:, QUAD * g:QUAD * (g + 1), :])
 
+        tb8 = const.tile([P, P], BF16, name="tb8")
+        nc.vector.memset(tb8[:], 0.0)
+        wvz = const.tile([P, K1], BF16, name="wvz")
+        nc.vector.memset(wvz[:, D_FEAT:K1], 0.0)
+        wcm = const.tile([P, 4, 512], BF16, name="wcm", align_bytes=64)
+        nc.vector.memset(wcm[:].bitcast(I32), 0)
+        m_half = const.tile([P, 1], F32, name="m_half")
+        nc.vector.memset(m_half[:], -0.5)
+
         nts = const.tile([P, TILES], BF16, name="nts")
         nc.scalar.dma_start(out=nts[:], in_=neighbor_ts.rearrange("(p a) j -> p (a j)", a=NPP))
         rts = const.tile([P, NPP], BF16, name="rts")
         nc.scalar.dma_start(out=rts[:], in_=root_ts.rearrange("(p a) -> p a", a=NPP))
-        tb8 = const.tile([P, P], BF16, name="tb8")
-        nc.vector.memset(tb8[:], 0.0)
         nc.scalar.dma_start(
             out=tb8[0:4, :].rearrange("t (r q) -> t r q", r=4),
             in_=time_w.rearrange("(t q) o -> t o q", t=4).to_broadcast([4, 4, 32]),
@@ -79,8 +87,6 @@ def tile_transformeraggregator_pb_kernel(
             in_=time_b.rearrange("(t o q) -> t o q", t=4, o=1).to_broadcast([4, 4, 32]),
         )
         load(0)
-        wvz = const.tile([P, K1], BF16, name="wvz")
-        nc.vector.memset(wvz[:, D_FEAT:K1], 0.0)
         nc.scalar.dma_start(out=wvz[:, 0:D_FEAT], in_=wv_w[:, 0:D_FEAT])
         wcos = const.tile([P, D_TIME], BF16, name="wcos")
         nc.scalar.dma_start(out=wcos[:], in_=wv_w[:, D_FEAT:K1])
@@ -127,23 +133,31 @@ def tile_transformeraggregator_pb_kernel(
         dtq = const.tile([P, GROUPS * P], F32, name="dtq")
         TB = QUAD * BATCH
 
-        def spread_dt(b):
+        def repeat_dt(b):
             nc.vector.tensor_copy(
                 out=dt_rep[:, TB * b:TB * (b + 1), :],
                 in_=dt_rows[:, TB * b:TB * (b + 1)].unsqueeze(2).to_broadcast([P, TB, 32]),
             )
-            tpd = tp_pool.tile([P, 4, P], F32, name="tp")
+
+        spread = {}
+
+        def spread_dt_pe(b):
+            tpd = ms_pool.tile([P, 4, P], F32, name="ms")
             for q in range(BATCH):
                 g = BATCH * b + q
                 nc.tensor.transpose(
                     tpd[:, q, :], dt_rep[:, QUAD * g:QUAD * (g + 1), :].rearrange("p i c -> p (i c)"), ident_f[:]
                 )
-            nc.scalar.copy(out=dtq[:, 512 * b:512 * (b + 1)], in_=tpd[:].rearrange("p q w -> p (q w)"))
+            spread[b] = tpd
 
-        spread_dt(0)
+        def spread_dt_out(b):
+            nc.scalar.copy(out=dtq[:, 512 * b:512 * (b + 1)], in_=spread[b][:].rearrange("p q w -> p (q w)"))
 
+        repeat_dt(0)
         ps8 = ms_pool.tile([P, P], BF16, name="ms")
         nc.tensor.transpose(ps8[:], tb8[:], ident_b[:])
+        spread_dt_pe(0)
+        spread_dt_out(0)
         a_q = const.tile([P, 4], F32, name="a_q")
         nc.vector.tensor_scalar(out=a_q[:], in0=ps8[:, 0:4], scalar1=1.0 / TWO_PI, scalar2=None, op0=ALU.mult)
         b_q = const.tile([P, 4], F32, name="b_q")
@@ -160,13 +174,16 @@ def tile_transformeraggregator_pb_kernel(
             planes = cpool.tile([P, 4, 512], BF16, name="planes")
             cos_state[b] = (turns, frac, planes)
 
-        def cos_plane(b, t):
+        def cos_reduce(b, t):
             turns, frac, planes = cos_state[b]
             d = dtq[:, 512 * b:512 * (b + 1)]
             nc.vector.tensor_scalar(out=turns[:, t, :], in0=d, scalar1=a_q[:, t:t + 1], scalar2=b_q[:, t:t + 1],
                                     op0=ALU.mult, op1=ALU.add)
             nc.vector.scalar_tensor_tensor(out=frac[:, t, :], in0=d, scalar=a_q[:, t:t + 1], in1=turns[:, t, :],
                                            op0=ALU.mult, op1=ALU.subtract)
+
+        def cos_sin(b, t):
+            turns, frac, planes = cos_state[b]
             nc.scalar.activation(out=planes[:, t, :], in_=frac[:, t, :], func=ACT.Sin,
                                  bias=b_2[:, t:t + 1], scale=TWO_PI)
 
@@ -184,17 +201,9 @@ def tile_transformeraggregator_pb_kernel(
             nc.vector.quantize_mx(out=cc[:].bitcast(FP8X4), scales=cs[:], in_=cos_g[:])
             cos_codes[b] = (cc, cs)
 
-        cos_open(0)
-        for t in range(4):
-            cos_plane(0, t)
-
         tpw = transpose_row_tile(wvz[:].bitcast(F32))
         gw = const.tile([P, K1], BF16, name="gw", align_bytes=64)
         evacuate(gw[:].bitcast(F32), tpw)
-        wvc = const.tile([P, 256], U32, name="wvc", align_bytes=64)
-        wvs = const.tile([P, 256], U8, name="wvs", align_bytes=64)
-        nc.vector.quantize_mx(out=wvc[:].bitcast(FP8X4), scales=wvs[:], in_=gw[:])
-
         wcr = const.tile([P, 4, 4, 32], BF16, name="wcr")
         nc.vector.tensor_copy(
             out=wcr[:],
@@ -203,19 +212,28 @@ def tile_transformeraggregator_pb_kernel(
         pw = ms_pool.tile([P, 4, P], BF16, name="ms")
         for t in range(4):
             nc.tensor.transpose(pw[:, t, :], wcr[:, t, :, :].rearrange("p r q -> p (r q)"), ident_b[:])
-        wcm = const.tile([P, 4, 512], BF16, name="wcm", align_bytes=64)
-        nc.vector.memset(wcm[:].bitcast(I32), 0)
         for r in range(4):
             nc.scalar.copy(
                 out=wcm[32 * r:32 * (r + 1), r, :].rearrange("p (c t) -> p c t", t=4),
                 in_=pw[32 * r:32 * (r + 1), :, :].rearrange("p t c -> p c t"),
             )
+
+        cos_open(0)
+        for t in range(4):
+            cos_reduce(0, t)
+            cos_sin(0, t)
+
+        wvc = const.tile([P, 256], U32, name="wvc", align_bytes=64)
+        wvs = const.tile([P, 256], U8, name="wvs", align_bytes=64)
+        nc.vector.quantize_mx(out=wvc[:].bitcast(FP8X4), scales=wvs[:], in_=gw[:])
         wcc = const.tile([P, 512], U32, name="wcc", align_bytes=64)
         wcs = const.tile([P, 512], U8, name="wcs", align_bytes=64)
         nc.vector.quantize_mx(out=wcc[:].bitcast(FP8X4), scales=wcs[:],
                               in_=wcm[:].rearrange("p r c -> p (r c)"))
-
+        repeat_dt(1)
         cos_close(0)
+        spread_dt_pe(1)
+        spread_dt_out(1)
 
         att_f = const.tile([P, TILES * HEADS], F32, name="att_f")
         nc.vector.tensor_copy(out=att_f[:], in_=att_b[:])
@@ -225,25 +243,16 @@ def tile_transformeraggregator_pb_kernel(
             in_=att_f[:].rearrange("p (a j h) -> p a h j", a=NPP, j=N_NEIGH),
             axis=AX.X, op=ALU.add,
         )
-        m_half = const.tile([P, 1], F32, name="m_half")
-        nc.vector.memset(m_half[:], -0.5)
 
-        pwo = ms_pool.tile([P, 4, P], BF16, name="ms")
-        for t in range(4):
-            nc.tensor.transpose(pwo[:, t, :], wo_sb[:, P * t:P * (t + 1)], ident_b[:])
         gwo = const.tile([P, 512], BF16, name="gwo", align_bytes=64)
-        nc.scalar.copy(out=gwo[:].rearrange("p (c t) -> p c t", t=4), in_=pwo[:].rearrange("p t c -> p c t"))
         woc = const.tile([P, P], U32, name="woc", align_bytes=64)
         wos = const.tile([P, P], U8, name="wos", align_bytes=64)
-        nc.vector.quantize_mx(out=woc[:].bitcast(FP8X4), scales=wos[:], in_=gwo[:])
-
-        for b in range(1, BATCHES):
-            spread_dt(b)
 
         grouped = {}
         codes = {}
         sums = {}
         accs = {}
+        late = {}
         pb = const.tile([P, NPP, D_OUT], BF16, name="pb")
 
         def stage_t(g):
@@ -307,10 +316,8 @@ def tile_transformeraggregator_pb_kernel(
                     else:
                         nc.vector.scalar_tensor_tensor(out=acc[:, r, cols], in0=mo[:, r, cols], scalar=w,
                                                        in1=acc[:, r, cols], op0=ALU.mult, op1=ALU.add)
-            if g % GPN == GPN - 1:
-                output_stage(a)
 
-        def output_stage(a):
+        def out_pool(a):
             acc = accs[a]
             red = spool.tile([P, D_OUT], F32, name="red")
             nc.vector.tensor_reduce(out=red[:], in_=acc[:].rearrange("p r c -> p c r"), axis=AX.X, op=ALU.add)
@@ -320,18 +327,31 @@ def tile_transformeraggregator_pb_kernel(
                     out=pb[:, a, cols], in0=wvb[:, cols], scalar=att_sum[:, HEADS * a + h:HEADS * a + h + 1],
                     in1=red[:, cols], op0=ALU.mult, op1=ALU.add,
                 )
+
+        def out_transpose(a):
             ps2 = ms_pool.tile([P, 4, P], BF16, name="ms")
             nc.tensor.transpose(ps2[:, 0, :], pb[:, a, :], ident_b[:])
             for c in range(3):
                 nc.tensor.transpose(ps2[:, 1 + c, :], rootf[:, a, P * c:P * (c + 1)], ident_b[:])
             g2 = spool.tile([P, 512], BF16, name="g2", align_bytes=64)
             nc.scalar.copy(out=g2[:].rearrange("p (w t) -> p w t", t=4), in_=ps2[:].rearrange("p t w -> p w t"))
+            late[("g2", a)] = g2
+
+        def out_quantise(a):
             c2 = spool.tile([P, P], U32, name="c2", align_bytes=64)
             s2 = spool.tile([P, P], U8, name="s2", align_bytes=64)
-            nc.vector.quantize_mx(out=c2[:].bitcast(FP8X4), scales=s2[:], in_=g2[:])
+            nc.vector.quantize_mx(out=c2[:].bitcast(FP8X4), scales=s2[:], in_=late[("g2", a)][:])
+            late[("c2", a)] = (c2, s2)
+
+        def out_matmul(a):
+            c2, s2 = late[("c2", a)]
             o2 = ms_pool.tile([P, D_OUT], F32, name="ms")
             nc.tensor.matmul_mx(out=o2[:], lhsT=c2[:].bitcast(FP8X4), lhsT_scale=s2[:],
                                 rhs=woc[:].bitcast(FP8X4), rhs_scale=wos[:], start=True, stop=True)
+            late[("o2", a)] = o2
+
+        def out_stats(a):
+            o2 = late[("o2", a)]
             hid = spool.tile([P, D_OUT], F32, name="hid")
             nc.vector.tensor_tensor(out=hid[:], in0=o2[:], in1=wob[:], op=ALU.add)
             nc.vector.tensor_scalar_max(out=hid[:], in0=hid[:], scalar1=0.0)
@@ -343,6 +363,10 @@ def tile_transformeraggregator_pb_kernel(
             nc.vector.tensor_scalar_add(out=ve[:], in0=mv[:, 1:2], scalar1=LN_EPS)
             rstd = spool.tile([P, 1], F32, name="rstd")
             nc.gpsimd.tensor_tensor(out=rstd[:], in0=ve[:], in1=m_half[:], op=ALU.pow)
+            late[("st", a)] = (hid, mv, rstd)
+
+        def out_norm(a):
+            hid, mv, rstd = late[("st", a)]
             res = spool.tile([P, D_OUT], F32, name="res")
             nc.vector.tensor_scalar(out=res[:], in0=hid[:], scalar1=mv[:, 0:1], scalar2=rstd[:],
                                     op0=ALU.subtract, op1=ALU.mult)
@@ -350,21 +374,52 @@ def tile_transformeraggregator_pb_kernel(
             nc.vector.tensor_tensor(out=res[:], in0=res[:], in1=lnb[:], op=ALU.add)
             nc.sync.dma_start(out=out_v[:, a, :], in_=res[:])
 
-        for s in range(GROUPS + 2):
+        done_at = [GPN * a + GPN - 1 + 2 for a in range(NPP)]
+
+        for s in range(GROUPS + 7):
             if s < GROUPS:
                 stage_t(s)
                 if s + NX < GROUPS:
                     load(s + NX)
+            if s == 1:
+                pwo = ms_pool.tile([P, 4, P], BF16, name="ms")
+                for t in range(4):
+                    nc.tensor.transpose(pwo[:, t, :], wo_sb[:, P * t:P * (t + 1)], ident_b[:])
+                nc.scalar.copy(out=gwo[:].rearrange("p (c t) -> p c t", t=4), in_=pwo[:].rearrange("p t c -> p c t"))
+            if s % BATCH == 2 and s // BATCH + 2 < BATCHES:
+                spread_dt_pe(s // BATCH + 2)
+                spread_dt_out(s // BATCH + 2)
+            for a in range(NPP):
+                if done_at[a] + 1 == s:
+                    out_transpose(a)
             if 1 <= s <= GROUPS:
                 stage_q(s - 1)
+            for a in range(NPP):
+                if done_at[a] + 2 == s:
+                    out_quantise(a)
+            if s == 2:
+                nc.vector.quantize_mx(out=woc[:].bitcast(FP8X4), scales=wos[:], in_=gwo[:])
             b_next, t_next = s // BATCH + 1, s % BATCH
             if b_next < BATCHES:
                 if t_next == 0:
                     cos_open(b_next)
-                cos_plane(b_next, t_next)
+                cos_reduce(b_next, t_next)
+                cos_sin(b_next, t_next)
             if s % BATCH == 0 and 1 <= s // BATCH < BATCHES:
                 cos_close(s // BATCH)
+            if s % BATCH == 1 and s // BATCH + 2 < BATCHES:
+                repeat_dt(s // BATCH + 2)
             if 1 <= s <= GROUPS:
                 stage_m(s - 1)
-            if s >= 2:
+            for a in range(NPP):
+                if done_at[a] + 2 == s:
+                    out_matmul(a)
+            if 2 <= s < GROUPS + 2:
                 stage_p(s - 2)
+            for a in range(NPP):
+                if done_at[a] == s:
+                    out_pool(a)
+                if done_at[a] + 3 == s:
+                    out_stats(a)
+                if done_at[a] + 4 == s:
+                    out_norm(a)

@@ -26,6 +26,8 @@ GROUPS = TILES // QUAD
 GPN = N_NEIGH // QUAD
 BATCH = 4
 BATCHES = GROUPS // BATCH
+COS_BATCHES = [(0, 1), (1, 1), (2, 2), (4, 4), (8, 4), (12, 4), (16, 4)]
+EARLY = 3
 NX = 6
 LN_EPS = 1e-5
 TWO_PI = 2.0 * math.pi
@@ -39,10 +41,9 @@ def tile_transformeraggregator_pb_kernel(
 ):
     nc = tc.nc
     with ExitStack() as ctx:
-        ctx.enter_context(tc.manual_schedule())
         const = ctx.enter_context(tc.tile_pool(name="const", bufs=1))
         xpool = ctx.enter_context(tc.tile_pool(name="xpool", bufs=1))
-        gpool = ctx.enter_context(tc.tile_pool(name="gpool", bufs=3))
+        gpool = ctx.enter_context(tc.tile_pool(name="gpool", bufs=4))
         cpool = ctx.enter_context(tc.tile_pool(name="cpool", bufs=2))
         spool = ctx.enter_context(tc.tile_pool(name="spool", bufs=2))
         tp_pool = ctx.enter_context(tc.psum_pool(name="tp", bufs=4))
@@ -65,19 +66,12 @@ def tile_transformeraggregator_pb_kernel(
             nc.sync.dma_start(out=x[:, :, 0:D_NODE], in_=node_v[:, QUAD * g:QUAD * (g + 1), :])
             nc.sync.dma_start(out=x[:, :, D_NODE:D_FEAT], in_=edge_v[:, QUAD * g:QUAD * (g + 1), :])
 
-        tb8 = const.tile([P, P], BF16, name="tb8")
-        nc.vector.memset(tb8[:], 0.0)
-        wvz = const.tile([P, K1], BF16, name="wvz")
-        nc.vector.memset(wvz[:, D_FEAT:K1], 0.0)
-        wcm = const.tile([P, 4, 512], BF16, name="wcm", align_bytes=64)
-        nc.vector.memset(wcm[:].bitcast(I32), 0)
-        m_half = const.tile([P, 1], F32, name="m_half")
-        nc.vector.memset(m_half[:], -0.5)
-
         nts = const.tile([P, TILES], BF16, name="nts")
         nc.scalar.dma_start(out=nts[:], in_=neighbor_ts.rearrange("(p a) j -> p (a j)", a=NPP))
         rts = const.tile([P, NPP], BF16, name="rts")
         nc.scalar.dma_start(out=rts[:], in_=root_ts.rearrange("(p a) -> p a", a=NPP))
+        tb8 = const.tile([P, P], BF16, name="tb8")
+        nc.vector.memset(tb8[:], 0.0)
         nc.scalar.dma_start(
             out=tb8[0:4, :].rearrange("t (r q) -> t r q", r=4),
             in_=time_w.rearrange("(t q) o -> t o q", t=4).to_broadcast([4, 4, 32]),
@@ -86,7 +80,11 @@ def tile_transformeraggregator_pb_kernel(
             out=tb8[4:8, :].rearrange("t (r q) -> t r q", r=4),
             in_=time_b.rearrange("(t o q) -> t o q", t=4, o=1).to_broadcast([4, 4, 32]),
         )
-        load(0)
+        for r in range(QUAD):
+            nc.sync.dma_start(out=xq[0][:, r, 0:D_NODE], in_=node_v[:, r, :])
+            nc.sync.dma_start(out=xq[0][:, r, D_NODE:D_FEAT], in_=edge_v[:, r, :])
+        wvz = const.tile([P, K1], BF16, name="wvz")
+        nc.gpsimd.memset(wvz[:, D_FEAT:K1], 0.0)
         nc.scalar.dma_start(out=wvz[:, 0:D_FEAT], in_=wv_w[:, 0:D_FEAT])
         wcos = const.tile([P, D_TIME], BF16, name="wcos")
         nc.scalar.dma_start(out=wcos[:], in_=wv_w[:, D_FEAT:K1])
@@ -98,17 +96,17 @@ def tile_transformeraggregator_pb_kernel(
             load(g)
 
         wvb = const.tile([P, D_OUT], BF16, name="wvb")
-        nc.gpsimd.dma_start(out=wvb[:], in_=wv_b.partition_broadcast(P))
+        nc.sync.dma_start(out=wvb[:], in_=wv_b.partition_broadcast(P))
         wo_sb = const.tile([P, D_OUT + D_NODE], BF16, name="wo_sb")
-        nc.gpsimd.dma_start(out=wo_sb[:], in_=wo_w)
+        nc.sync.dma_start(out=wo_sb[:], in_=wo_w)
         rootf = const.tile([P, NPP, D_NODE], BF16, name="rootf")
-        nc.gpsimd.dma_start(out=rootf[:], in_=root_node_feature.rearrange("(p a) c -> p a c", a=NPP))
+        nc.sync.dma_start(out=rootf[:], in_=root_node_feature.rearrange("(p a) c -> p a c", a=NPP))
         wob = const.tile([P, D_OUT], BF16, name="wob")
-        nc.gpsimd.dma_start(out=wob[:], in_=wo_b.partition_broadcast(P))
+        nc.sync.dma_start(out=wob[:], in_=wo_b.partition_broadcast(P))
         lng = const.tile([P, D_OUT], BF16, name="lng")
-        nc.gpsimd.dma_start(out=lng[:], in_=ln_g.partition_broadcast(P))
+        nc.sync.dma_start(out=lng[:], in_=ln_g.partition_broadcast(P))
         lnb = const.tile([P, D_OUT], BF16, name="lnb")
-        nc.gpsimd.dma_start(out=lnb[:], in_=ln_b.partition_broadcast(P))
+        nc.sync.dma_start(out=lnb[:], in_=ln_b.partition_broadcast(P))
 
         def transpose_row_tile(words):
             tp = tp_pool.tile([P, 4, P], F32, name="tp")
@@ -133,31 +131,25 @@ def tile_transformeraggregator_pb_kernel(
         dtq = const.tile([P, GROUPS * P], F32, name="dtq")
         TB = QUAD * BATCH
 
-        def repeat_dt(b):
-            nc.vector.tensor_copy(
-                out=dt_rep[:, TB * b:TB * (b + 1), :],
-                in_=dt_rows[:, TB * b:TB * (b + 1)].unsqueeze(2).to_broadcast([P, TB, 32]),
-            )
-
-        spread = {}
-
-        def spread_dt_pe(b):
+        def spread_dt(b):
+            src = dt_rows[:, TB * b:TB * (b + 1)].unsqueeze(2).to_broadcast([P, TB, 32])
+            if b == 0:
+                nc.vector.tensor_copy(out=dt_rep[:, TB * b:TB * (b + 1), :], in_=src)
+            else:
+                nc.gpsimd.tensor_scalar(out=dt_rep[:, TB * b:TB * (b + 1), :], in0=src, scalar1=1.0, scalar2=0.0,
+                                        op0=ALU.mult, op1=ALU.add)
             tpd = ms_pool.tile([P, 4, P], F32, name="ms")
             for q in range(BATCH):
                 g = BATCH * b + q
                 nc.tensor.transpose(
                     tpd[:, q, :], dt_rep[:, QUAD * g:QUAD * (g + 1), :].rearrange("p i c -> p (i c)"), ident_f[:]
                 )
-            spread[b] = tpd
+            nc.scalar.copy(out=dtq[:, 512 * b:512 * (b + 1)], in_=tpd[:].rearrange("p q w -> p (q w)"))
 
-        def spread_dt_out(b):
-            nc.scalar.copy(out=dtq[:, 512 * b:512 * (b + 1)], in_=spread[b][:].rearrange("p q w -> p (q w)"))
+        spread_dt(0)
 
-        repeat_dt(0)
         ps8 = ms_pool.tile([P, P], BF16, name="ms")
         nc.tensor.transpose(ps8[:], tb8[:], ident_b[:])
-        spread_dt_pe(0)
-        spread_dt_out(0)
         a_q = const.tile([P, 4], F32, name="a_q")
         nc.vector.tensor_scalar(out=a_q[:], in0=ps8[:, 0:4], scalar1=1.0 / TWO_PI, scalar2=None, op0=ALU.mult)
         b_q = const.tile([P, 4], F32, name="b_q")
@@ -168,42 +160,62 @@ def tile_transformeraggregator_pb_kernel(
 
         cos_state = {}
 
+        turns = const.tile([P, 4, 512], I32, name="turns")
+
         def cos_open(b):
-            turns = cpool.tile([P, 4, 512], I32, name="turns")
             frac = cpool.tile([P, 4, 512], F32, name="frac")
             planes = cpool.tile([P, 4, 512], BF16, name="planes")
-            cos_state[b] = (turns, frac, planes)
+            cos_state[b] = (frac, planes)
 
-        def cos_reduce(b, t):
-            turns, frac, planes = cos_state[b]
-            d = dtq[:, 512 * b:512 * (b + 1)]
-            nc.vector.tensor_scalar(out=turns[:, t, :], in0=d, scalar1=a_q[:, t:t + 1], scalar2=b_q[:, t:t + 1],
-                                    op0=ALU.mult, op1=ALU.add)
-            nc.vector.scalar_tensor_tensor(out=frac[:, t, :], in0=d, scalar=a_q[:, t:t + 1], in1=turns[:, t, :],
+        def cos_turns(b, t):
+            g0, n = COS_BATCHES[b]
+            nc.gpsimd.tensor_scalar(out=turns[:, t, 0:P * n], in0=dtq[:, P * g0:P * (g0 + n)], scalar1=a_q[:, t:t + 1],
+                                    scalar2=b_q[:, t:t + 1], op0=ALU.mult, op1=ALU.add)
+
+        def cos_plane(b, t):
+            g0, n = COS_BATCHES[b]
+            frac, planes = cos_state[b]
+            nc.vector.scalar_tensor_tensor(out=frac[:, t, 0:P * n], in0=dtq[:, P * g0:P * (g0 + n)],
+                                           scalar=a_q[:, t:t + 1], in1=turns[:, t, 0:P * n],
                                            op0=ALU.mult, op1=ALU.subtract)
-
-        def cos_sin(b, t):
-            turns, frac, planes = cos_state[b]
-            nc.scalar.activation(out=planes[:, t, :], in_=frac[:, t, :], func=ACT.Sin,
+            nc.scalar.activation(out=planes[:, t, 0:P * n], in_=frac[:, t, 0:P * n], func=ACT.Sin,
                                  bias=b_2[:, t:t + 1], scale=TWO_PI)
+            if b + 1 < len(COS_BATCHES):
+                cos_turns(b + 1, t)
 
         cos_codes = {}
 
         def cos_close(b):
-            planes = cos_state[b][2]
+            g0, n = COS_BATCHES[b]
+            planes = cos_state[b][1]
             cos_g = cpool.tile([P, 2048], BF16, name="cos_g", align_bytes=64)
             nc.vector.tensor_copy(
-                out=cos_g[:].rearrange("p (c i t) -> p c t i", i=4, t=4),
-                in_=planes[:].rearrange("p t (c i) -> p c t i", i=4),
+                out=cos_g[:, 0:512 * n].rearrange("p (c i t) -> p c t i", i=4, t=4),
+                in_=planes[:, :, 0:P * n].rearrange("p t (c i) -> p c t i", i=4),
             )
-            cc = cpool.tile([P, 512], U32, name="cc", align_bytes=64)
-            cs = cpool.tile([P, 512], U8, name="cs", align_bytes=64)
-            nc.vector.quantize_mx(out=cc[:].bitcast(FP8X4), scales=cs[:], in_=cos_g[:])
-            cos_codes[b] = (cc, cs)
+            cc = cpool.tile([P, 512], U32, name="cc", align_bytes=64, bufs=4)
+            cs = cpool.tile([P, 512], U8, name="cs", align_bytes=64, bufs=4)
+            nc.vector.quantize_mx(out=cc[:, 0:P * n].bitcast(FP8X4), scales=cs[:, 0:P * n], in_=cos_g[:, 0:512 * n])
+            for g in range(g0, g0 + n):
+                cos_codes[g] = (cc, cs, P * (g - g0))
+
+        for t in range(4):
+            cos_turns(0, t)
+        for b in range(1, BATCHES):
+            spread_dt(b)
+        for b in range(EARLY):
+            cos_open(b)
+            for t in range(4):
+                cos_plane(b, t)
+            cos_close(b)
 
         tpw = transpose_row_tile(wvz[:].bitcast(F32))
         gw = const.tile([P, K1], BF16, name="gw", align_bytes=64)
         evacuate(gw[:].bitcast(F32), tpw)
+        wvc = const.tile([P, 256], U32, name="wvc", align_bytes=64)
+        wvs = const.tile([P, 256], U8, name="wvs", align_bytes=64)
+        nc.vector.quantize_mx(out=wvc[:].bitcast(FP8X4), scales=wvs[:], in_=gw[:])
+
         wcr = const.tile([P, 4, 4, 32], BF16, name="wcr")
         nc.vector.tensor_copy(
             out=wcr[:],
@@ -212,47 +224,41 @@ def tile_transformeraggregator_pb_kernel(
         pw = ms_pool.tile([P, 4, P], BF16, name="ms")
         for t in range(4):
             nc.tensor.transpose(pw[:, t, :], wcr[:, t, :, :].rearrange("p r q -> p (r q)"), ident_b[:])
-        for r in range(4):
-            nc.scalar.copy(
-                out=wcm[32 * r:32 * (r + 1), r, :].rearrange("p (c t) -> p c t", t=4),
-                in_=pw[32 * r:32 * (r + 1), :, :].rearrange("p t c -> p c t"),
-            )
-
-        cos_open(0)
-        for t in range(4):
-            cos_reduce(0, t)
-            cos_sin(0, t)
-
-        wvc = const.tile([P, 256], U32, name="wvc", align_bytes=64)
-        wvs = const.tile([P, 256], U8, name="wvs", align_bytes=64)
-        nc.vector.quantize_mx(out=wvc[:].bitcast(FP8X4), scales=wvs[:], in_=gw[:])
+        wcg = const.tile([P, 512], BF16, name="wcg", align_bytes=64)
+        nc.scalar.copy(out=wcg[:].rearrange("p (c t) -> p c t", t=4), in_=pw[:].rearrange("p t c -> p c t"))
+        wc1 = const.tile([P, P], U32, name="wc1", align_bytes=64)
+        wcs = const.tile([P, P], U8, name="wcs", align_bytes=64)
+        nc.vector.quantize_mx(out=wc1[:].bitcast(FP8X4), scales=wcs[:], in_=wcg[:])
         wcc = const.tile([P, 512], U32, name="wcc", align_bytes=64)
-        wcs = const.tile([P, 512], U8, name="wcs", align_bytes=64)
-        nc.vector.quantize_mx(out=wcc[:].bitcast(FP8X4), scales=wcs[:],
-                              in_=wcm[:].rearrange("p r c -> p (r c)"))
-        repeat_dt(1)
-        cos_close(0)
-        spread_dt_pe(1)
-        spread_dt_out(1)
+        nc.gpsimd.memset(wcc[:].bitcast(F32), 0.0)
+        for r in range(4):
+            nc.vector.tensor_copy(out=wcc[32 * r:32 * (r + 1), P * r:P * (r + 1)].bitcast(I32),
+                                  in_=wc1[32 * r:32 * (r + 1), :].bitcast(I32))
 
         att_f = const.tile([P, TILES * HEADS], F32, name="att_f")
-        nc.vector.tensor_copy(out=att_f[:], in_=att_b[:])
+        nc.gpsimd.tensor_scalar(out=att_f[:], in0=att_b[:], scalar1=1.0, scalar2=0.0, op0=ALU.mult, op1=ALU.add)
         att_sum = const.tile([P, NPP * HEADS], F32, name="att_sum")
         nc.vector.tensor_reduce(
             out=att_sum[:].rearrange("p (a h) -> p a h", a=NPP),
             in_=att_f[:].rearrange("p (a j h) -> p a h j", a=NPP, j=N_NEIGH),
             axis=AX.X, op=ALU.add,
         )
+        m_half = const.tile([P, 1], F32, name="m_half")
+        nc.gpsimd.memset(m_half[:], -0.5)
 
+        pwo = ms_pool.tile([P, 4, P], BF16, name="ms")
+        for t in range(4):
+            nc.tensor.transpose(pwo[:, t, :], wo_sb[:, P * t:P * (t + 1)], ident_b[:])
         gwo = const.tile([P, 512], BF16, name="gwo", align_bytes=64)
+        nc.scalar.copy(out=gwo[:].rearrange("p (c t) -> p c t", t=4), in_=pwo[:].rearrange("p t c -> p c t"))
         woc = const.tile([P, P], U32, name="woc", align_bytes=64)
         wos = const.tile([P, P], U8, name="wos", align_bytes=64)
+        nc.vector.quantize_mx(out=woc[:].bitcast(FP8X4), scales=wos[:], in_=gwo[:])
 
         grouped = {}
         codes = {}
         sums = {}
         accs = {}
-        late = {}
         pb = const.tile([P, NPP, D_OUT], BF16, name="pb")
 
         def stage_t(g):
@@ -268,18 +274,19 @@ def tile_transformeraggregator_pb_kernel(
             gq = grouped[g]
             cq = gpool.tile([P, QUAD * 256], U32, name="cq", align_bytes=64)
             sq = gpool.tile([P, QUAD * 256], U8, name="sq", align_bytes=64)
-            for hlf in range(2):
+            pieces = 4 if g == GROUPS - 1 else 2
+            wc = QUAD * 256 // pieces
+            for k in range(pieces):
                 nc.vector.quantize_mx(
-                    out=cq[:, 512 * hlf:512 * (hlf + 1)].bitcast(FP8X4),
-                    scales=sq[:, 512 * hlf:512 * (hlf + 1)],
-                    in_=gq[:, 2048 * hlf:2048 * (hlf + 1)],
+                    out=cq[:, wc * k:wc * (k + 1)].bitcast(FP8X4),
+                    scales=sq[:, wc * k:wc * (k + 1)],
+                    in_=gq[:, 4 * wc * k:4 * wc * (k + 1)],
                 )
             codes[g] = (cq, sq)
 
         def stage_m(g):
             cq, sq = codes[g]
-            cc, cs = cos_codes[g // BATCH]
-            cw = P * (g % BATCH)
+            cc, cs, cw = cos_codes[g]
             mo = mo_pool.tile([P, QUAD, D_OUT], F32, name="mo")
             for r in range(QUAD):
                 for ps in range(2):
@@ -293,7 +300,7 @@ def tile_transformeraggregator_pb_kernel(
                 nc.tensor.matmul_mx(
                     out=mo[:, r, :],
                     lhsT=cc[:, cw:cw + P].bitcast(FP8X4), lhsT_scale=cs[:, cw:cw + P],
-                    rhs=wcc[:, P * r:P * (r + 1)].bitcast(FP8X4), rhs_scale=wcs[:, P * r:P * (r + 1)],
+                    rhs=wcc[:, P * r:P * (r + 1)].bitcast(FP8X4), rhs_scale=wcs[:],
                     start=False, stop=True,
                 )
             sums[g] = mo
@@ -316,8 +323,10 @@ def tile_transformeraggregator_pb_kernel(
                     else:
                         nc.vector.scalar_tensor_tensor(out=acc[:, r, cols], in0=mo[:, r, cols], scalar=w,
                                                        in1=acc[:, r, cols], op0=ALU.mult, op1=ALU.add)
+            if g % GPN == GPN - 1:
+                output_stage(a)
 
-        def out_pool(a):
+        def output_stage(a):
             acc = accs[a]
             red = spool.tile([P, D_OUT], F32, name="red")
             nc.vector.tensor_reduce(out=red[:], in_=acc[:].rearrange("p r c -> p c r"), axis=AX.X, op=ALU.add)
@@ -327,31 +336,22 @@ def tile_transformeraggregator_pb_kernel(
                     out=pb[:, a, cols], in0=wvb[:, cols], scalar=att_sum[:, HEADS * a + h:HEADS * a + h + 1],
                     in1=red[:, cols], op0=ALU.mult, op1=ALU.add,
                 )
-
-        def out_transpose(a):
             ps2 = ms_pool.tile([P, 4, P], BF16, name="ms")
             nc.tensor.transpose(ps2[:, 0, :], pb[:, a, :], ident_b[:])
             for c in range(3):
                 nc.tensor.transpose(ps2[:, 1 + c, :], rootf[:, a, P * c:P * (c + 1)], ident_b[:])
             g2 = spool.tile([P, 512], BF16, name="g2", align_bytes=64)
-            nc.scalar.copy(out=g2[:].rearrange("p (w t) -> p w t", t=4), in_=ps2[:].rearrange("p t w -> p w t"))
-            late[("g2", a)] = g2
-
-        def out_quantise(a):
+            if a == NPP - 1:
+                nc.vector.tensor_copy(out=g2[:].rearrange("p (w t) -> p w t", t=4),
+                                      in_=ps2[:].rearrange("p t w -> p w t"))
+            else:
+                nc.scalar.copy(out=g2[:].rearrange("p (w t) -> p w t", t=4), in_=ps2[:].rearrange("p t w -> p w t"))
             c2 = spool.tile([P, P], U32, name="c2", align_bytes=64)
             s2 = spool.tile([P, P], U8, name="s2", align_bytes=64)
-            nc.vector.quantize_mx(out=c2[:].bitcast(FP8X4), scales=s2[:], in_=late[("g2", a)][:])
-            late[("c2", a)] = (c2, s2)
-
-        def out_matmul(a):
-            c2, s2 = late[("c2", a)]
+            nc.vector.quantize_mx(out=c2[:].bitcast(FP8X4), scales=s2[:], in_=g2[:])
             o2 = ms_pool.tile([P, D_OUT], F32, name="ms")
             nc.tensor.matmul_mx(out=o2[:], lhsT=c2[:].bitcast(FP8X4), lhsT_scale=s2[:],
                                 rhs=woc[:].bitcast(FP8X4), rhs_scale=wos[:], start=True, stop=True)
-            late[("o2", a)] = o2
-
-        def out_stats(a):
-            o2 = late[("o2", a)]
             hid = spool.tile([P, D_OUT], F32, name="hid")
             nc.vector.tensor_tensor(out=hid[:], in0=o2[:], in1=wob[:], op=ALU.add)
             nc.vector.tensor_scalar_max(out=hid[:], in0=hid[:], scalar1=0.0)
@@ -363,63 +363,28 @@ def tile_transformeraggregator_pb_kernel(
             nc.vector.tensor_scalar_add(out=ve[:], in0=mv[:, 1:2], scalar1=LN_EPS)
             rstd = spool.tile([P, 1], F32, name="rstd")
             nc.gpsimd.tensor_tensor(out=rstd[:], in0=ve[:], in1=m_half[:], op=ALU.pow)
-            late[("st", a)] = (hid, mv, rstd)
-
-        def out_norm(a):
-            hid, mv, rstd = late[("st", a)]
             res = spool.tile([P, D_OUT], F32, name="res")
-            nc.vector.tensor_scalar(out=res[:], in0=hid[:], scalar1=mv[:, 0:1], scalar2=rstd[:],
-                                    op0=ALU.subtract, op1=ALU.mult)
-            nc.vector.tensor_tensor(out=res[:], in0=res[:], in1=lng[:], op=ALU.mult)
-            nc.vector.tensor_tensor(out=res[:], in0=res[:], in1=lnb[:], op=ALU.add)
+            nc.vector.scalar_tensor_tensor(out=res[:], in0=hid[:], scalar=mv[:, 0:1], in1=lng[:],
+                                           op0=ALU.subtract, op1=ALU.mult)
+            nc.vector.scalar_tensor_tensor(out=res[:], in0=res[:], scalar=rstd[:], in1=lnb[:],
+                                           op0=ALU.mult, op1=ALU.add)
             nc.sync.dma_start(out=out_v[:, a, :], in_=res[:])
 
-        done_at = [GPN * a + GPN - 1 + 2 for a in range(NPP)]
-
-        for s in range(GROUPS + 7):
+        for s in range(GROUPS + 2):
             if s < GROUPS:
                 stage_t(s)
                 if s + NX < GROUPS:
                     load(s + NX)
-            if s == 1:
-                pwo = ms_pool.tile([P, 4, P], BF16, name="ms")
-                for t in range(4):
-                    nc.tensor.transpose(pwo[:, t, :], wo_sb[:, P * t:P * (t + 1)], ident_b[:])
-                nc.scalar.copy(out=gwo[:].rearrange("p (c t) -> p c t", t=4), in_=pwo[:].rearrange("p t c -> p c t"))
-            if s % BATCH == 2 and s // BATCH + 2 < BATCHES:
-                spread_dt_pe(s // BATCH + 2)
-                spread_dt_out(s // BATCH + 2)
-            for a in range(NPP):
-                if done_at[a] + 1 == s:
-                    out_transpose(a)
             if 1 <= s <= GROUPS:
                 stage_q(s - 1)
-            for a in range(NPP):
-                if done_at[a] + 2 == s:
-                    out_quantise(a)
-            if s == 2:
-                nc.vector.quantize_mx(out=woc[:].bitcast(FP8X4), scales=wos[:], in_=gwo[:])
-            b_next, t_next = s // BATCH + 1, s % BATCH
-            if b_next < BATCHES:
+            b_next, t_next = s // BATCH + EARLY, s % BATCH
+            if b_next < len(COS_BATCHES):
                 if t_next == 0:
                     cos_open(b_next)
-                cos_reduce(b_next, t_next)
-                cos_sin(b_next, t_next)
-            if s % BATCH == 0 and 1 <= s // BATCH < BATCHES:
-                cos_close(s // BATCH)
-            if s % BATCH == 1 and s // BATCH + 2 < BATCHES:
-                repeat_dt(s // BATCH + 2)
+                cos_plane(b_next, t_next)
+            if s % BATCH == 0 and EARLY <= s // BATCH + EARLY - 1 < len(COS_BATCHES):
+                cos_close(s // BATCH + EARLY - 1)
             if 1 <= s <= GROUPS:
                 stage_m(s - 1)
-            for a in range(NPP):
-                if done_at[a] + 2 == s:
-                    out_matmul(a)
-            if 2 <= s < GROUPS + 2:
+            if s >= 2:
                 stage_p(s - 2)
-            for a in range(NPP):
-                if done_at[a] == s:
-                    out_pool(a)
-                if done_at[a] + 3 == s:
-                    out_stats(a)
-                if done_at[a] + 4 == s:
-                    out_norm(a)

@@ -41,6 +41,7 @@ def tile_transformeraggregator_pb_kernel(
 ):
     nc = tc.nc
     with ExitStack() as ctx:
+        ctx.enter_context(tc.manual_schedule())
         const = ctx.enter_context(tc.tile_pool(name="const", bufs=1))
         xpool = ctx.enter_context(tc.tile_pool(name="xpool", bufs=1))
         gpool = ctx.enter_context(tc.tile_pool(name="gpool", bufs=4))
@@ -66,12 +67,12 @@ def tile_transformeraggregator_pb_kernel(
             nc.sync.dma_start(out=x[:, :, 0:D_NODE], in_=node_v[:, QUAD * g:QUAD * (g + 1), :])
             nc.sync.dma_start(out=x[:, :, D_NODE:D_FEAT], in_=edge_v[:, QUAD * g:QUAD * (g + 1), :])
 
+        tb8 = const.tile([P, P], BF16, name="tb8")
+        nc.vector.memset(tb8[:], 0.0)
         nts = const.tile([P, TILES], BF16, name="nts")
         nc.scalar.dma_start(out=nts[:], in_=neighbor_ts.rearrange("(p a) j -> p (a j)", a=NPP))
         rts = const.tile([P, NPP], BF16, name="rts")
         nc.scalar.dma_start(out=rts[:], in_=root_ts.rearrange("(p a) -> p a", a=NPP))
-        tb8 = const.tile([P, P], BF16, name="tb8")
-        nc.vector.memset(tb8[:], 0.0)
         nc.scalar.dma_start(
             out=tb8[0:4, :].rearrange("t (r q) -> t r q", r=4),
             in_=time_w.rearrange("(t q) o -> t o q", t=4).to_broadcast([4, 4, 32]),
@@ -84,15 +85,21 @@ def tile_transformeraggregator_pb_kernel(
             nc.sync.dma_start(out=xq[0][:, r, 0:D_NODE], in_=node_v[:, r, :])
             nc.sync.dma_start(out=xq[0][:, r, D_NODE:D_FEAT], in_=edge_v[:, r, :])
         wvz = const.tile([P, K1], BF16, name="wvz")
-        nc.gpsimd.memset(wvz[:, D_FEAT:K1], 0.0)
         nc.scalar.dma_start(out=wvz[:, 0:D_FEAT], in_=wv_w[:, 0:D_FEAT])
         wcos = const.tile([P, D_TIME], BF16, name="wcos")
         nc.scalar.dma_start(out=wcos[:], in_=wv_w[:, D_FEAT:K1])
         att_b = const.tile([P, TILES * HEADS], BF16, name="att_b")
         nc.scalar.dma_start(out=att_b[:], in_=att.rearrange("(p a) j h -> p (a j h)", a=NPP))
-        for k in range(NX):
+
+        nc.gpsimd.memset(xq[0][:, :, D_FEAT:K1], 0.0)
+        nc.gpsimd.memset(wvz[:, D_FEAT:K1], 0.0)
+        wcc = const.tile([P, 512], U32, name="wcc", align_bytes=64)
+        nc.gpsimd.memset(wcc[:].bitcast(F32), 0.0)
+        for k in range(1, NX):
             nc.gpsimd.memset(xq[k][:, :, D_FEAT:K1], 0.0)
-        for g in range(1, NX):
+        m_half = const.tile([P, 1], F32, name="m_half")
+        nc.gpsimd.memset(m_half[:], -0.5)
+        for g in range(1, 3):
             load(g)
 
         wvb = const.tile([P, D_OUT], BF16, name="wvb")
@@ -107,6 +114,8 @@ def tile_transformeraggregator_pb_kernel(
         nc.sync.dma_start(out=lng[:], in_=ln_g.partition_broadcast(P))
         lnb = const.tile([P, D_OUT], BF16, name="lnb")
         nc.sync.dma_start(out=lnb[:], in_=ln_b.partition_broadcast(P))
+        for g in range(3, NX):
+            load(g)
 
         def transpose_row_tile(words):
             tp = tp_pool.tile([P, 4, P], F32, name="tp")
@@ -131,13 +140,15 @@ def tile_transformeraggregator_pb_kernel(
         dtq = const.tile([P, GROUPS * P], F32, name="dtq")
         TB = QUAD * BATCH
 
-        def spread_dt(b):
+        def repeat_dt(b):
             src = dt_rows[:, TB * b:TB * (b + 1)].unsqueeze(2).to_broadcast([P, TB, 32])
             if b == 0:
                 nc.vector.tensor_copy(out=dt_rep[:, TB * b:TB * (b + 1), :], in_=src)
             else:
                 nc.gpsimd.tensor_scalar(out=dt_rep[:, TB * b:TB * (b + 1), :], in0=src, scalar1=1.0, scalar2=0.0,
                                         op0=ALU.mult, op1=ALU.add)
+
+        def spread_dt(b):
             tpd = ms_pool.tile([P, 4, P], F32, name="ms")
             for q in range(BATCH):
                 g = BATCH * b + q
@@ -146,10 +157,14 @@ def tile_transformeraggregator_pb_kernel(
                 )
             nc.scalar.copy(out=dtq[:, 512 * b:512 * (b + 1)], in_=tpd[:].rearrange("p q w -> p (q w)"))
 
-        spread_dt(0)
+        for b in range(BATCHES):
+            repeat_dt(b)
+        att_f = const.tile([P, TILES * HEADS], F32, name="att_f")
+        nc.gpsimd.tensor_scalar(out=att_f[:], in0=att_b[:], scalar1=1.0, scalar2=0.0, op0=ALU.mult, op1=ALU.add)
 
         ps8 = ms_pool.tile([P, P], BF16, name="ms")
         nc.tensor.transpose(ps8[:], tb8[:], ident_b[:])
+        spread_dt(0)
         a_q = const.tile([P, 4], F32, name="a_q")
         nc.vector.tensor_scalar(out=a_q[:], in0=ps8[:, 0:4], scalar1=1.0 / TWO_PI, scalar2=None, op0=ALU.mult)
         b_q = const.tile([P, 4], F32, name="b_q")
@@ -160,34 +175,28 @@ def tile_transformeraggregator_pb_kernel(
 
         cos_state = {}
 
-        turns = const.tile([P, 4, 512], I32, name="turns")
-
         def cos_open(b):
+            turns = cpool.tile([P, 4, 512], I32, name="turns")
             frac = cpool.tile([P, 4, 512], F32, name="frac")
             planes = cpool.tile([P, 4, 512], BF16, name="planes")
-            cos_state[b] = (frac, planes)
-
-        def cos_turns(b, t):
-            g0, n = COS_BATCHES[b]
-            nc.gpsimd.tensor_scalar(out=turns[:, t, 0:P * n], in0=dtq[:, P * g0:P * (g0 + n)], scalar1=a_q[:, t:t + 1],
-                                    scalar2=b_q[:, t:t + 1], op0=ALU.mult, op1=ALU.add)
+            cos_state[b] = (turns, frac, planes)
 
         def cos_plane(b, t):
             g0, n = COS_BATCHES[b]
-            frac, planes = cos_state[b]
-            nc.vector.scalar_tensor_tensor(out=frac[:, t, 0:P * n], in0=dtq[:, P * g0:P * (g0 + n)],
-                                           scalar=a_q[:, t:t + 1], in1=turns[:, t, 0:P * n],
-                                           op0=ALU.mult, op1=ALU.subtract)
+            turns, frac, planes = cos_state[b]
+            d = dtq[:, P * g0:P * (g0 + n)]
+            nc.vector.tensor_scalar(out=turns[:, t, 0:P * n], in0=d, scalar1=a_q[:, t:t + 1], scalar2=b_q[:, t:t + 1],
+                                    op0=ALU.mult, op1=ALU.add)
+            nc.vector.scalar_tensor_tensor(out=frac[:, t, 0:P * n], in0=d, scalar=a_q[:, t:t + 1],
+                                           in1=turns[:, t, 0:P * n], op0=ALU.mult, op1=ALU.subtract)
             nc.scalar.activation(out=planes[:, t, 0:P * n], in_=frac[:, t, 0:P * n], func=ACT.Sin,
                                  bias=b_2[:, t:t + 1], scale=TWO_PI)
-            if b + 1 < len(COS_BATCHES):
-                cos_turns(b + 1, t)
 
         cos_codes = {}
 
         def cos_close(b):
             g0, n = COS_BATCHES[b]
-            planes = cos_state[b][1]
+            planes = cos_state[b][2]
             cos_g = cpool.tile([P, 2048], BF16, name="cos_g", align_bytes=64)
             nc.vector.tensor_copy(
                 out=cos_g[:, 0:512 * n].rearrange("p (c i t) -> p c t i", i=4, t=4),
@@ -199,23 +208,9 @@ def tile_transformeraggregator_pb_kernel(
             for g in range(g0, g0 + n):
                 cos_codes[g] = (cc, cs, P * (g - g0))
 
-        for t in range(4):
-            cos_turns(0, t)
-        for b in range(1, BATCHES):
-            spread_dt(b)
-        for b in range(EARLY):
-            cos_open(b)
-            for t in range(4):
-                cos_plane(b, t)
-            cos_close(b)
-
         tpw = transpose_row_tile(wvz[:].bitcast(F32))
         gw = const.tile([P, K1], BF16, name="gw", align_bytes=64)
         evacuate(gw[:].bitcast(F32), tpw)
-        wvc = const.tile([P, 256], U32, name="wvc", align_bytes=64)
-        wvs = const.tile([P, 256], U8, name="wvs", align_bytes=64)
-        nc.vector.quantize_mx(out=wvc[:].bitcast(FP8X4), scales=wvs[:], in_=gw[:])
-
         wcr = const.tile([P, 4, 4, 32], BF16, name="wcr")
         nc.vector.tensor_copy(
             out=wcr[:],
@@ -226,49 +221,26 @@ def tile_transformeraggregator_pb_kernel(
             nc.tensor.transpose(pw[:, t, :], wcr[:, t, :, :].rearrange("p r q -> p (r q)"), ident_b[:])
         wcg = const.tile([P, 512], BF16, name="wcg", align_bytes=64)
         nc.scalar.copy(out=wcg[:].rearrange("p (c t) -> p c t", t=4), in_=pw[:].rearrange("p t c -> p c t"))
-        wc1 = const.tile([P, P], U32, name="wc1", align_bytes=64)
-        wcs = const.tile([P, P], U8, name="wcs", align_bytes=64)
-        nc.vector.quantize_mx(out=wc1[:].bitcast(FP8X4), scales=wcs[:], in_=wcg[:])
-        wcc = const.tile([P, 512], U32, name="wcc", align_bytes=64)
-        nc.gpsimd.memset(wcc[:].bitcast(F32), 0.0)
-        for r in range(4):
-            nc.vector.tensor_copy(out=wcc[32 * r:32 * (r + 1), P * r:P * (r + 1)].bitcast(I32),
-                                  in_=wc1[32 * r:32 * (r + 1), :].bitcast(I32))
 
-        att_f = const.tile([P, TILES * HEADS], F32, name="att_f")
-        nc.gpsimd.tensor_scalar(out=att_f[:], in0=att_b[:], scalar1=1.0, scalar2=0.0, op0=ALU.mult, op1=ALU.add)
-        att_sum = const.tile([P, NPP * HEADS], F32, name="att_sum")
-        nc.vector.tensor_reduce(
-            out=att_sum[:].rearrange("p (a h) -> p a h", a=NPP),
-            in_=att_f[:].rearrange("p (a j h) -> p a h j", a=NPP, j=N_NEIGH),
-            axis=AX.X, op=ALU.add,
-        )
-        m_half = const.tile([P, 1], F32, name="m_half")
-        nc.gpsimd.memset(m_half[:], -0.5)
-
-        pwo = ms_pool.tile([P, 4, P], BF16, name="ms")
-        for t in range(4):
-            nc.tensor.transpose(pwo[:, t, :], wo_sb[:, P * t:P * (t + 1)], ident_b[:])
         gwo = const.tile([P, 512], BF16, name="gwo", align_bytes=64)
-        nc.scalar.copy(out=gwo[:].rearrange("p (c t) -> p c t", t=4), in_=pwo[:].rearrange("p t c -> p c t"))
         woc = const.tile([P, P], U32, name="woc", align_bytes=64)
         wos = const.tile([P, P], U8, name="wos", align_bytes=64)
-        nc.vector.quantize_mx(out=woc[:].bitcast(FP8X4), scales=wos[:], in_=gwo[:])
 
         grouped = {}
         codes = {}
         sums = {}
         accs = {}
+        late = {}
         pb = const.tile([P, NPP, D_OUT], BF16, name="pb")
 
-        def stage_t(g):
-            xw = xq[g % NX][:].bitcast(F32)
-            gq = gpool.tile([P, QUAD * K1], BF16, name="gq", align_bytes=64)
-            gqw = gq[:].bitcast(F32)
-            for r in range(QUAD):
-                tp = transpose_row_tile(xw[:, r, :])
-                evacuate(gqw[:, 512 * r:512 * (r + 1)], tp)
-            grouped[g] = gq
+        def piece_t(g, r):
+            if r == 0:
+                gq_new = gpool.tile([P, QUAD * K1], BF16, name="gq", align_bytes=64)
+                grouped[g] = gq_new
+            tp = transpose_row_tile(xq[g % NX][:].bitcast(F32)[:, r, :])
+            evacuate(grouped[g][:].bitcast(F32)[:, 512 * r:512 * (r + 1)], tp)
+            if r == QUAD - 1 and g + NX < GROUPS:
+                load(g + NX)
 
         def stage_q(g):
             gq = grouped[g]
@@ -284,26 +256,27 @@ def tile_transformeraggregator_pb_kernel(
                 )
             codes[g] = (cq, sq)
 
-        def stage_m(g):
+        def piece_m(g, r):
             cq, sq = codes[g]
             cc, cs, cw = cos_codes[g]
-            mo = mo_pool.tile([P, QUAD, D_OUT], F32, name="mo")
-            for r in range(QUAD):
-                for ps in range(2):
-                    s = 256 * r + P * ps
-                    nc.tensor.matmul_mx(
-                        out=mo[:, r, :],
-                        lhsT=cq[:, s:s + P].bitcast(FP8X4), lhsT_scale=sq[:, s:s + P],
-                        rhs=wvc[:, P * ps:P * (ps + 1)].bitcast(FP8X4), rhs_scale=wvs[:, P * ps:P * (ps + 1)],
-                        start=(ps == 0), stop=False,
-                    )
+            if r == 0:
+                mo_new = mo_pool.tile([P, QUAD, D_OUT], F32, name="mo")
+                sums[g] = mo_new
+            mo = sums[g]
+            for ps in range(2):
+                s = 256 * r + P * ps
                 nc.tensor.matmul_mx(
                     out=mo[:, r, :],
-                    lhsT=cc[:, cw:cw + P].bitcast(FP8X4), lhsT_scale=cs[:, cw:cw + P],
-                    rhs=wcc[:, P * r:P * (r + 1)].bitcast(FP8X4), rhs_scale=wcs[:],
-                    start=False, stop=True,
+                    lhsT=cq[:, s:s + P].bitcast(FP8X4), lhsT_scale=sq[:, s:s + P],
+                    rhs=wvc[:, P * ps:P * (ps + 1)].bitcast(FP8X4), rhs_scale=wvs[:, P * ps:P * (ps + 1)],
+                    start=(ps == 0), stop=False,
                 )
-            sums[g] = mo
+            nc.tensor.matmul_mx(
+                out=mo[:, r, :],
+                lhsT=cc[:, cw:cw + P].bitcast(FP8X4), lhsT_scale=cs[:, cw:cw + P],
+                rhs=wcc[:, P * r:P * (r + 1)].bitcast(FP8X4), rhs_scale=wcs[:],
+                start=False, stop=True,
+            )
 
         def stage_p(g):
             mo = sums[g]
@@ -323,10 +296,8 @@ def tile_transformeraggregator_pb_kernel(
                     else:
                         nc.vector.scalar_tensor_tensor(out=acc[:, r, cols], in0=mo[:, r, cols], scalar=w,
                                                        in1=acc[:, r, cols], op0=ALU.mult, op1=ALU.add)
-            if g % GPN == GPN - 1:
-                output_stage(a)
 
-        def output_stage(a):
+        def out_pool(a):
             acc = accs[a]
             red = spool.tile([P, D_OUT], F32, name="red")
             nc.vector.tensor_reduce(out=red[:], in_=acc[:].rearrange("p r c -> p c r"), axis=AX.X, op=ALU.add)
@@ -336,6 +307,8 @@ def tile_transformeraggregator_pb_kernel(
                     out=pb[:, a, cols], in0=wvb[:, cols], scalar=att_sum[:, HEADS * a + h:HEADS * a + h + 1],
                     in1=red[:, cols], op0=ALU.mult, op1=ALU.add,
                 )
+
+        def out_transpose(a):
             ps2 = ms_pool.tile([P, 4, P], BF16, name="ms")
             nc.tensor.transpose(ps2[:, 0, :], pb[:, a, :], ident_b[:])
             for c in range(3):
@@ -346,12 +319,23 @@ def tile_transformeraggregator_pb_kernel(
                                       in_=ps2[:].rearrange("p t w -> p w t"))
             else:
                 nc.scalar.copy(out=g2[:].rearrange("p (w t) -> p w t", t=4), in_=ps2[:].rearrange("p t w -> p w t"))
+            late[("g2", a)] = g2
+
+        def out_quantise(a):
             c2 = spool.tile([P, P], U32, name="c2", align_bytes=64)
             s2 = spool.tile([P, P], U8, name="s2", align_bytes=64)
-            nc.vector.quantize_mx(out=c2[:].bitcast(FP8X4), scales=s2[:], in_=g2[:])
+            nc.vector.quantize_mx(out=c2[:].bitcast(FP8X4), scales=s2[:], in_=late[("g2", a)][:])
+            late[("c2", a)] = (c2, s2)
+
+        def out_matmul(a):
+            c2, s2 = late[("c2", a)]
             o2 = ms_pool.tile([P, D_OUT], F32, name="ms")
             nc.tensor.matmul_mx(out=o2[:], lhsT=c2[:].bitcast(FP8X4), lhsT_scale=s2[:],
                                 rhs=woc[:].bitcast(FP8X4), rhs_scale=wos[:], start=True, stop=True)
+            late[("o2", a)] = o2
+
+        def out_stats(a):
+            o2 = late[("o2", a)]
             hid = spool.tile([P, D_OUT], F32, name="hid")
             nc.vector.tensor_tensor(out=hid[:], in0=o2[:], in1=wob[:], op=ALU.add)
             nc.vector.tensor_scalar_max(out=hid[:], in0=hid[:], scalar1=0.0)
@@ -366,25 +350,88 @@ def tile_transformeraggregator_pb_kernel(
             res = spool.tile([P, D_OUT], F32, name="res")
             nc.vector.scalar_tensor_tensor(out=res[:], in0=hid[:], scalar=mv[:, 0:1], in1=lng[:],
                                            op0=ALU.subtract, op1=ALU.mult)
+            late[("st", a)] = (res, rstd)
+
+        def out_norm(a):
+            res, rstd = late[("st", a)]
             nc.vector.scalar_tensor_tensor(out=res[:], in0=res[:], scalar=rstd[:], in1=lnb[:],
                                            op0=ALU.mult, op1=ALU.add)
             nc.sync.dma_start(out=out_v[:, a, :], in_=res[:])
 
-        for s in range(GROUPS + 2):
-            if s < GROUPS:
-                stage_t(s)
-                if s + NX < GROUPS:
-                    load(s + NX)
-            if 1 <= s <= GROUPS:
-                stage_q(s - 1)
-            b_next, t_next = s // BATCH + EARLY, s % BATCH
-            if b_next < len(COS_BATCHES):
-                if t_next == 0:
-                    cos_open(b_next)
-                cos_plane(b_next, t_next)
-            if s % BATCH == 0 and EARLY <= s // BATCH + EARLY - 1 < len(COS_BATCHES):
-                cos_close(s // BATCH + EARLY - 1)
-            if 1 <= s <= GROUPS:
-                stage_m(s - 1)
-            if s >= 2:
-                stage_p(s - 2)
+        for r in range(QUAD):
+            piece_t(0, r)
+        spread_dt(1)
+        cos_open(0)
+        for t in range(4):
+            cos_plane(0, t)
+        cos_open(1)
+        for t in range(4):
+            cos_plane(1, t)
+        wvc = const.tile([P, 256], U32, name="wvc", align_bytes=64)
+        wvs = const.tile([P, 256], U8, name="wvs", align_bytes=64)
+        nc.vector.quantize_mx(out=wvc[:].bitcast(FP8X4), scales=wvs[:], in_=gw[:])
+        wc1 = const.tile([P, P], U32, name="wc1", align_bytes=64)
+        wcs = const.tile([P, P], U8, name="wcs", align_bytes=64)
+        nc.vector.quantize_mx(out=wc1[:].bitcast(FP8X4), scales=wcs[:], in_=wcg[:])
+        cos_close(0)
+        for r in range(4):
+            nc.vector.tensor_copy(out=wcc[32 * r:32 * (r + 1), P * r:P * (r + 1)].bitcast(I32),
+                                  in_=wc1[32 * r:32 * (r + 1), :].bitcast(I32))
+        cos_open(2)
+        for t in range(4):
+            cos_plane(2, t)
+        cos_close(1)
+        att_sum = const.tile([P, NPP * HEADS], F32, name="att_sum")
+        nc.vector.tensor_reduce(
+            out=att_sum[:].rearrange("p (a h) -> p a h", a=NPP),
+            in_=att_f[:].rearrange("p (a j h) -> p a h j", a=NPP, j=N_NEIGH),
+            axis=AX.X, op=ALU.add,
+        )
+
+        LAG_M, LAG_P = 2, 3
+        done_at = [GPN * a + GPN - 1 + LAG_P for a in range(NPP)]
+
+        for s in range(1, GROUPS + LAG_P + 5):
+            for r in range(QUAD):
+                if s < GROUPS:
+                    piece_t(s, r)
+                if r == 0:
+                    if s - 1 < GROUPS:
+                        stage_q(s - 1)
+                    if s == 1:
+                        cos_close(2)
+                    for a in range(NPP):
+                        if done_at[a] + 2 == s:
+                            out_quantise(a)
+                    if s == 6:
+                        nc.vector.quantize_mx(out=woc[:].bitcast(FP8X4), scales=wos[:], in_=gwo[:])
+                if 0 <= s - LAG_M < GROUPS:
+                    piece_m(s - LAG_M, r)
+            if s == 5:
+                pwo = ms_pool.tile([P, 4, P], BF16, name="ms")
+                for t in range(4):
+                    nc.tensor.transpose(pwo[:, t, :], wo_sb[:, P * t:P * (t + 1)], ident_b[:])
+                nc.scalar.copy(out=gwo[:].rearrange("p (c t) -> p c t", t=4), in_=pwo[:].rearrange("p t c -> p c t"))
+            if s % BATCH == 3 and s // BATCH + 2 < BATCHES:
+                spread_dt(s // BATCH + 2)
+            for a in range(NPP):
+                if done_at[a] + 1 == s:
+                    out_transpose(a)
+                if done_at[a] + 2 == s:
+                    out_matmul(a)
+            k_cos, t_cos = (s - 1) // BATCH, (s - 1) % BATCH
+            if EARLY + k_cos < len(COS_BATCHES):
+                if t_cos == 0:
+                    cos_open(EARLY + k_cos)
+                cos_plane(EARLY + k_cos, t_cos)
+            if t_cos == 0 and 1 <= k_cos and EARLY + k_cos - 1 < len(COS_BATCHES):
+                cos_close(EARLY + k_cos - 1)
+            if 0 <= s - LAG_P < GROUPS:
+                stage_p(s - LAG_P)
+            for a in range(NPP):
+                if done_at[a] == s:
+                    out_pool(a)
+                if done_at[a] + 3 == s:
+                    out_stats(a)
+                if done_at[a] + 4 == s:
+                    out_norm(a)

@@ -49,7 +49,8 @@ def tile_transformeraggregator_pb_kernel(
         spool = ctx.enter_context(tc.tile_pool(name="spool", bufs=2))
         tp_pool = ctx.enter_context(tc.psum_pool(name="tp", bufs=4))
         mo_pool = ctx.enter_context(tc.psum_pool(name="mo", bufs=2))
-        ms_pool = ctx.enter_context(tc.psum_pool(name="ms", bufs=2))
+        ms_pool = ctx.enter_context(tc.psum_pool(name="ms", bufs=1))
+        dm_pool = ctx.enter_context(tc.psum_pool(name="dm", bufs=1))
 
         node_v = neighbor_node_feature.rearrange("(p a) j c -> p (a j) c", a=NPP)
         edge_v = neighbor_edge_feature.rearrange("(p a) j c -> p (a j) c", a=NPP)
@@ -278,6 +279,17 @@ def tile_transformeraggregator_pb_kernel(
                 start=False, stop=True,
             )
 
+        idle_sum = dm_pool.tile([P, 512], F32, name="idle_sum")
+
+        def clock_pass(g):
+            cq, sq = codes[g]
+            nc.tensor.matmul_mx(
+                out=idle_sum[:],
+                lhsT=wvc[:, 0:P].bitcast(FP8X4), lhsT_scale=wvs[:, 0:P],
+                rhs=cq[:, 0:512].bitcast(FP8X4), rhs_scale=sq[:, 0:512],
+                start=True, stop=True,
+            )
+
         def stage_p(g):
             mo = sums[g]
             a = g // GPN
@@ -392,10 +404,11 @@ def tile_transformeraggregator_pb_kernel(
         done_at = [GPN * a + GPN - 1 + LAG_P for a in range(NPP)]
 
         for s in range(1, GROUPS + LAG_P + 5):
-            for r in range(QUAD):
+            for hlf in range(2):
                 if s < GROUPS:
-                    piece_t(s, r)
-                if r == 0:
+                    piece_t(s, 2 * hlf)
+                    piece_t(s, 2 * hlf + 1)
+                if hlf == 0:
                     if s - 1 < GROUPS:
                         stage_q(s - 1)
                     if s == 1:
@@ -405,18 +418,24 @@ def tile_transformeraggregator_pb_kernel(
                             out_quantise(a)
                     if s == 6:
                         nc.vector.quantize_mx(out=woc[:].bitcast(FP8X4), scales=wos[:], in_=gwo[:])
+                else:
+                    if s == 5:
+                        pwo = ms_pool.tile([P, 4, P], BF16, name="ms")
+                        for t in range(4):
+                            nc.tensor.transpose(pwo[:, t, :], wo_sb[:, P * t:P * (t + 1)], ident_b[:])
+                        nc.scalar.copy(out=gwo[:].rearrange("p (c t) -> p c t", t=4),
+                                       in_=pwo[:].rearrange("p t c -> p c t"))
+                    if s % BATCH == 3 and s // BATCH + 2 < BATCHES:
+                        spread_dt(s // BATCH + 2)
+                    for a in range(NPP):
+                        if done_at[a] + 1 == s:
+                            out_transpose(a)
                 if 0 <= s - LAG_M < GROUPS:
-                    piece_m(s - LAG_M, r)
-            if s == 5:
-                pwo = ms_pool.tile([P, 4, P], BF16, name="ms")
-                for t in range(4):
-                    nc.tensor.transpose(pwo[:, t, :], wo_sb[:, P * t:P * (t + 1)], ident_b[:])
-                nc.scalar.copy(out=gwo[:].rearrange("p (c t) -> p c t", t=4), in_=pwo[:].rearrange("p t c -> p c t"))
-            if s % BATCH == 3 and s // BATCH + 2 < BATCHES:
-                spread_dt(s // BATCH + 2)
+                    piece_m(s - LAG_M, 2 * hlf)
+                    piece_m(s - LAG_M, 2 * hlf + 1)
+                    if s < GROUPS:
+                        clock_pass(s - LAG_M)
             for a in range(NPP):
-                if done_at[a] + 1 == s:
-                    out_transpose(a)
                 if done_at[a] + 2 == s:
                     out_matmul(a)
             k_cos, t_cos = (s - 1) // BATCH, (s - 1) % BATCH

@@ -41,7 +41,6 @@ def tile_transformeraggregator_pb_kernel(
 ):
     nc = tc.nc
     with ExitStack() as ctx:
-        ctx.enter_context(tc.manual_schedule())
         const = ctx.enter_context(tc.tile_pool(name="const", bufs=1))
         xpool = ctx.enter_context(tc.tile_pool(name="xpool", bufs=1))
         gpool = ctx.enter_context(tc.tile_pool(name="gpool", bufs=4))
@@ -49,8 +48,7 @@ def tile_transformeraggregator_pb_kernel(
         spool = ctx.enter_context(tc.tile_pool(name="spool", bufs=2))
         tp_pool = ctx.enter_context(tc.psum_pool(name="tp", bufs=4))
         mo_pool = ctx.enter_context(tc.psum_pool(name="mo", bufs=2))
-        ms_pool = ctx.enter_context(tc.psum_pool(name="ms", bufs=1))
-        dm_pool = ctx.enter_context(tc.psum_pool(name="dm", bufs=1))
+        ms_pool = ctx.enter_context(tc.psum_pool(name="ms", bufs=2))
 
         node_v = neighbor_node_feature.rearrange("(p a) j c -> p (a j) c", a=NPP)
         edge_v = neighbor_edge_feature.rearrange("(p a) j c -> p (a j) c", a=NPP)
@@ -68,12 +66,12 @@ def tile_transformeraggregator_pb_kernel(
             nc.sync.dma_start(out=x[:, :, 0:D_NODE], in_=node_v[:, QUAD * g:QUAD * (g + 1), :])
             nc.sync.dma_start(out=x[:, :, D_NODE:D_FEAT], in_=edge_v[:, QUAD * g:QUAD * (g + 1), :])
 
-        tb8 = const.tile([P, P], BF16, name="tb8")
-        nc.vector.memset(tb8[:], 0.0)
         nts = const.tile([P, TILES], BF16, name="nts")
         nc.scalar.dma_start(out=nts[:], in_=neighbor_ts.rearrange("(p a) j -> p (a j)", a=NPP))
         rts = const.tile([P, NPP], BF16, name="rts")
         nc.scalar.dma_start(out=rts[:], in_=root_ts.rearrange("(p a) -> p a", a=NPP))
+        tb8 = const.tile([P, P], BF16, name="tb8")
+        nc.vector.memset(tb8[:], 0.0)
         nc.scalar.dma_start(
             out=tb8[0:4, :].rearrange("t (r q) -> t r q", r=4),
             in_=time_w.rearrange("(t q) o -> t o q", t=4).to_broadcast([4, 4, 32]),
@@ -86,21 +84,15 @@ def tile_transformeraggregator_pb_kernel(
             nc.sync.dma_start(out=xq[0][:, r, 0:D_NODE], in_=node_v[:, r, :])
             nc.sync.dma_start(out=xq[0][:, r, D_NODE:D_FEAT], in_=edge_v[:, r, :])
         wvz = const.tile([P, K1], BF16, name="wvz")
+        nc.gpsimd.memset(wvz[:, D_FEAT:K1], 0.0)
         nc.scalar.dma_start(out=wvz[:, 0:D_FEAT], in_=wv_w[:, 0:D_FEAT])
         wcos = const.tile([P, D_TIME], BF16, name="wcos")
         nc.scalar.dma_start(out=wcos[:], in_=wv_w[:, D_FEAT:K1])
         att_b = const.tile([P, TILES * HEADS], BF16, name="att_b")
         nc.scalar.dma_start(out=att_b[:], in_=att.rearrange("(p a) j h -> p (a j h)", a=NPP))
-
-        nc.gpsimd.memset(xq[0][:, :, D_FEAT:K1], 0.0)
-        nc.gpsimd.memset(wvz[:, D_FEAT:K1], 0.0)
-        wcc = const.tile([P, 512], U32, name="wcc", align_bytes=64)
-        nc.gpsimd.memset(wcc[:].bitcast(F32), 0.0)
-        for k in range(1, NX):
+        for k in range(NX):
             nc.gpsimd.memset(xq[k][:, :, D_FEAT:K1], 0.0)
-        m_half = const.tile([P, 1], F32, name="m_half")
-        nc.gpsimd.memset(m_half[:], -0.5)
-        for g in range(1, 3):
+        for g in range(1, NX):
             load(g)
 
         wvb = const.tile([P, D_OUT], BF16, name="wvb")
@@ -115,8 +107,6 @@ def tile_transformeraggregator_pb_kernel(
         nc.sync.dma_start(out=lng[:], in_=ln_g.partition_broadcast(P))
         lnb = const.tile([P, D_OUT], BF16, name="lnb")
         nc.sync.dma_start(out=lnb[:], in_=ln_b.partition_broadcast(P))
-        for g in range(3, NX):
-            load(g)
 
         def transpose_row_tile(words):
             tp = tp_pool.tile([P, 4, P], F32, name="tp")
@@ -141,15 +131,13 @@ def tile_transformeraggregator_pb_kernel(
         dtq = const.tile([P, GROUPS * P], F32, name="dtq")
         TB = QUAD * BATCH
 
-        def repeat_dt(b):
+        def spread_dt(b):
             src = dt_rows[:, TB * b:TB * (b + 1)].unsqueeze(2).to_broadcast([P, TB, 32])
             if b == 0:
                 nc.vector.tensor_copy(out=dt_rep[:, TB * b:TB * (b + 1), :], in_=src)
             else:
                 nc.gpsimd.tensor_scalar(out=dt_rep[:, TB * b:TB * (b + 1), :], in0=src, scalar1=1.0, scalar2=0.0,
                                         op0=ALU.mult, op1=ALU.add)
-
-        def spread_dt(b):
             tpd = ms_pool.tile([P, 4, P], F32, name="ms")
             for q in range(BATCH):
                 g = BATCH * b + q
@@ -158,14 +146,10 @@ def tile_transformeraggregator_pb_kernel(
                 )
             nc.scalar.copy(out=dtq[:, 512 * b:512 * (b + 1)], in_=tpd[:].rearrange("p q w -> p (q w)"))
 
-        for b in range(BATCHES):
-            repeat_dt(b)
-        att_f = const.tile([P, TILES * HEADS], F32, name="att_f")
-        nc.gpsimd.tensor_scalar(out=att_f[:], in0=att_b[:], scalar1=1.0, scalar2=0.0, op0=ALU.mult, op1=ALU.add)
+        spread_dt(0)
 
         ps8 = ms_pool.tile([P, P], BF16, name="ms")
         nc.tensor.transpose(ps8[:], tb8[:], ident_b[:])
-        spread_dt(0)
         a_q = const.tile([P, 4], F32, name="a_q")
         nc.vector.tensor_scalar(out=a_q[:], in0=ps8[:, 0:4], scalar1=1.0 / TWO_PI, scalar2=None, op0=ALU.mult)
         b_q = const.tile([P, 4], F32, name="b_q")
@@ -176,28 +160,34 @@ def tile_transformeraggregator_pb_kernel(
 
         cos_state = {}
 
+        turns = const.tile([P, 4, 512], I32, name="turns")
+
         def cos_open(b):
-            turns = cpool.tile([P, 4, 512], I32, name="turns")
             frac = cpool.tile([P, 4, 512], F32, name="frac")
             planes = cpool.tile([P, 4, 512], BF16, name="planes")
-            cos_state[b] = (turns, frac, planes)
+            cos_state[b] = (frac, planes)
+
+        def cos_turns(b, t):
+            g0, n = COS_BATCHES[b]
+            nc.vector.tensor_scalar(out=turns[:, t, 0:P * n], in0=dtq[:, P * g0:P * (g0 + n)], scalar1=a_q[:, t:t + 1],
+                                    scalar2=b_q[:, t:t + 1], op0=ALU.mult, op1=ALU.add)
 
         def cos_plane(b, t):
             g0, n = COS_BATCHES[b]
-            turns, frac, planes = cos_state[b]
-            d = dtq[:, P * g0:P * (g0 + n)]
-            nc.vector.tensor_scalar(out=turns[:, t, 0:P * n], in0=d, scalar1=a_q[:, t:t + 1], scalar2=b_q[:, t:t + 1],
-                                    op0=ALU.mult, op1=ALU.add)
-            nc.vector.scalar_tensor_tensor(out=frac[:, t, 0:P * n], in0=d, scalar=a_q[:, t:t + 1],
-                                           in1=turns[:, t, 0:P * n], op0=ALU.mult, op1=ALU.subtract)
+            frac, planes = cos_state[b]
+            nc.vector.scalar_tensor_tensor(out=frac[:, t, 0:P * n], in0=dtq[:, P * g0:P * (g0 + n)],
+                                           scalar=a_q[:, t:t + 1], in1=turns[:, t, 0:P * n],
+                                           op0=ALU.mult, op1=ALU.subtract)
             nc.scalar.activation(out=planes[:, t, 0:P * n], in_=frac[:, t, 0:P * n], func=ACT.Sin,
                                  bias=b_2[:, t:t + 1], scale=TWO_PI)
+            if b + 1 < len(COS_BATCHES):
+                cos_turns(b + 1, t)
 
         cos_codes = {}
 
         def cos_close(b):
             g0, n = COS_BATCHES[b]
-            planes = cos_state[b][2]
+            planes = cos_state[b][1]
             cos_g = cpool.tile([P, 2048], BF16, name="cos_g", align_bytes=64)
             nc.vector.tensor_copy(
                 out=cos_g[:, 0:512 * n].rearrange("p (c i t) -> p c t i", i=4, t=4),
@@ -209,9 +199,23 @@ def tile_transformeraggregator_pb_kernel(
             for g in range(g0, g0 + n):
                 cos_codes[g] = (cc, cs, P * (g - g0))
 
+        for t in range(4):
+            cos_turns(0, t)
+        for b in range(1, BATCHES):
+            spread_dt(b)
+        for b in range(EARLY):
+            cos_open(b)
+            for t in range(4):
+                cos_plane(b, t)
+            cos_close(b)
+
         tpw = transpose_row_tile(wvz[:].bitcast(F32))
         gw = const.tile([P, K1], BF16, name="gw", align_bytes=64)
         evacuate(gw[:].bitcast(F32), tpw)
+        wvc = const.tile([P, 256], U32, name="wvc", align_bytes=64)
+        wvs = const.tile([P, 256], U8, name="wvs", align_bytes=64)
+        nc.vector.quantize_mx(out=wvc[:].bitcast(FP8X4), scales=wvs[:], in_=gw[:])
+
         wcr = const.tile([P, 4, 4, 32], BF16, name="wcr")
         nc.vector.tensor_copy(
             out=wcr[:],
@@ -222,26 +226,49 @@ def tile_transformeraggregator_pb_kernel(
             nc.tensor.transpose(pw[:, t, :], wcr[:, t, :, :].rearrange("p r q -> p (r q)"), ident_b[:])
         wcg = const.tile([P, 512], BF16, name="wcg", align_bytes=64)
         nc.scalar.copy(out=wcg[:].rearrange("p (c t) -> p c t", t=4), in_=pw[:].rearrange("p t c -> p c t"))
+        wc1 = const.tile([P, P], U32, name="wc1", align_bytes=64)
+        wcs = const.tile([P, P], U8, name="wcs", align_bytes=64)
+        nc.vector.quantize_mx(out=wc1[:].bitcast(FP8X4), scales=wcs[:], in_=wcg[:])
+        wcc = const.tile([P, 512], U32, name="wcc", align_bytes=64)
+        nc.gpsimd.memset(wcc[:].bitcast(F32), 0.0)
+        for r in range(4):
+            nc.vector.tensor_copy(out=wcc[32 * r:32 * (r + 1), P * r:P * (r + 1)].bitcast(I32),
+                                  in_=wc1[32 * r:32 * (r + 1), :].bitcast(I32))
 
+        att_f = const.tile([P, TILES * HEADS], F32, name="att_f")
+        nc.gpsimd.tensor_scalar(out=att_f[:], in0=att_b[:], scalar1=1.0, scalar2=0.0, op0=ALU.mult, op1=ALU.add)
+        att_sum = const.tile([P, NPP * HEADS], F32, name="att_sum")
+        nc.vector.tensor_reduce(
+            out=att_sum[:].rearrange("p (a h) -> p a h", a=NPP),
+            in_=att_f[:].rearrange("p (a j h) -> p a h j", a=NPP, j=N_NEIGH),
+            axis=AX.X, op=ALU.add,
+        )
+        m_half = const.tile([P, 1], F32, name="m_half")
+        nc.gpsimd.memset(m_half[:], -0.5)
+
+        pwo = ms_pool.tile([P, 4, P], BF16, name="ms")
+        for t in range(4):
+            nc.tensor.transpose(pwo[:, t, :], wo_sb[:, P * t:P * (t + 1)], ident_b[:])
         gwo = const.tile([P, 512], BF16, name="gwo", align_bytes=64)
+        nc.scalar.copy(out=gwo[:].rearrange("p (c t) -> p c t", t=4), in_=pwo[:].rearrange("p t c -> p c t"))
         woc = const.tile([P, P], U32, name="woc", align_bytes=64)
         wos = const.tile([P, P], U8, name="wos", align_bytes=64)
+        nc.vector.quantize_mx(out=woc[:].bitcast(FP8X4), scales=wos[:], in_=gwo[:])
 
         grouped = {}
         codes = {}
         sums = {}
         accs = {}
-        late = {}
         pb = const.tile([P, NPP, D_OUT], BF16, name="pb")
 
-        def piece_t(g, r):
-            if r == 0:
-                gq_new = gpool.tile([P, QUAD * K1], BF16, name="gq", align_bytes=64)
-                grouped[g] = gq_new
-            tp = transpose_row_tile(xq[g % NX][:].bitcast(F32)[:, r, :])
-            evacuate(grouped[g][:].bitcast(F32)[:, 512 * r:512 * (r + 1)], tp)
-            if r == QUAD - 1 and g + NX < GROUPS:
-                load(g + NX)
+        def stage_t(g):
+            xw = xq[g % NX][:].bitcast(F32)
+            gq = gpool.tile([P, QUAD * K1], BF16, name="gq", align_bytes=64)
+            gqw = gq[:].bitcast(F32)
+            for r in range(QUAD):
+                tp = transpose_row_tile(xw[:, r, :])
+                evacuate(gqw[:, 512 * r:512 * (r + 1)], tp)
+            grouped[g] = gq
 
         def stage_q(g):
             gq = grouped[g]
@@ -257,38 +284,26 @@ def tile_transformeraggregator_pb_kernel(
                 )
             codes[g] = (cq, sq)
 
-        def piece_m(g, r):
+        def stage_m(g):
             cq, sq = codes[g]
             cc, cs, cw = cos_codes[g]
-            if r == 0:
-                mo_new = mo_pool.tile([P, QUAD, D_OUT], F32, name="mo")
-                sums[g] = mo_new
-            mo = sums[g]
-            for ps in range(2):
-                s = 256 * r + P * ps
+            mo = mo_pool.tile([P, QUAD, D_OUT], F32, name="mo")
+            for r in range(QUAD):
+                for ps in range(2):
+                    s = 256 * r + P * ps
+                    nc.tensor.matmul_mx(
+                        out=mo[:, r, :],
+                        lhsT=cq[:, s:s + P].bitcast(FP8X4), lhsT_scale=sq[:, s:s + P],
+                        rhs=wvc[:, P * ps:P * (ps + 1)].bitcast(FP8X4), rhs_scale=wvs[:, P * ps:P * (ps + 1)],
+                        start=(ps == 0), stop=False,
+                    )
                 nc.tensor.matmul_mx(
                     out=mo[:, r, :],
-                    lhsT=cq[:, s:s + P].bitcast(FP8X4), lhsT_scale=sq[:, s:s + P],
-                    rhs=wvc[:, P * ps:P * (ps + 1)].bitcast(FP8X4), rhs_scale=wvs[:, P * ps:P * (ps + 1)],
-                    start=(ps == 0), stop=False,
+                    lhsT=cc[:, cw:cw + P].bitcast(FP8X4), lhsT_scale=cs[:, cw:cw + P],
+                    rhs=wcc[:, P * r:P * (r + 1)].bitcast(FP8X4), rhs_scale=wcs[:],
+                    start=False, stop=True,
                 )
-            nc.tensor.matmul_mx(
-                out=mo[:, r, :],
-                lhsT=cc[:, cw:cw + P].bitcast(FP8X4), lhsT_scale=cs[:, cw:cw + P],
-                rhs=wcc[:, P * r:P * (r + 1)].bitcast(FP8X4), rhs_scale=wcs[:],
-                start=False, stop=True,
-            )
-
-        idle_sum = dm_pool.tile([P, 512], F32, name="idle_sum")
-
-        def clock_pass(g):
-            cq, sq = codes[g]
-            nc.tensor.matmul_mx(
-                out=idle_sum[:],
-                lhsT=wvc[:, 0:P].bitcast(FP8X4), lhsT_scale=wvs[:, 0:P],
-                rhs=cq[:, 0:512].bitcast(FP8X4), rhs_scale=sq[:, 0:512],
-                start=True, stop=True,
-            )
+            sums[g] = mo
 
         def stage_p(g):
             mo = sums[g]
@@ -308,8 +323,10 @@ def tile_transformeraggregator_pb_kernel(
                     else:
                         nc.vector.scalar_tensor_tensor(out=acc[:, r, cols], in0=mo[:, r, cols], scalar=w,
                                                        in1=acc[:, r, cols], op0=ALU.mult, op1=ALU.add)
+            if g % GPN == GPN - 1:
+                output_stage(a)
 
-        def out_pool(a):
+        def output_stage(a):
             acc = accs[a]
             red = spool.tile([P, D_OUT], F32, name="red")
             nc.vector.tensor_reduce(out=red[:], in_=acc[:].rearrange("p r c -> p c r"), axis=AX.X, op=ALU.add)
@@ -319,8 +336,6 @@ def tile_transformeraggregator_pb_kernel(
                     out=pb[:, a, cols], in0=wvb[:, cols], scalar=att_sum[:, HEADS * a + h:HEADS * a + h + 1],
                     in1=red[:, cols], op0=ALU.mult, op1=ALU.add,
                 )
-
-        def out_transpose(a):
             ps2 = ms_pool.tile([P, 4, P], BF16, name="ms")
             nc.tensor.transpose(ps2[:, 0, :], pb[:, a, :], ident_b[:])
             for c in range(3):
@@ -331,23 +346,12 @@ def tile_transformeraggregator_pb_kernel(
                                       in_=ps2[:].rearrange("p t w -> p w t"))
             else:
                 nc.scalar.copy(out=g2[:].rearrange("p (w t) -> p w t", t=4), in_=ps2[:].rearrange("p t w -> p w t"))
-            late[("g2", a)] = g2
-
-        def out_quantise(a):
             c2 = spool.tile([P, P], U32, name="c2", align_bytes=64)
             s2 = spool.tile([P, P], U8, name="s2", align_bytes=64)
-            nc.vector.quantize_mx(out=c2[:].bitcast(FP8X4), scales=s2[:], in_=late[("g2", a)][:])
-            late[("c2", a)] = (c2, s2)
-
-        def out_matmul(a):
-            c2, s2 = late[("c2", a)]
+            nc.vector.quantize_mx(out=c2[:].bitcast(FP8X4), scales=s2[:], in_=g2[:])
             o2 = ms_pool.tile([P, D_OUT], F32, name="ms")
             nc.tensor.matmul_mx(out=o2[:], lhsT=c2[:].bitcast(FP8X4), lhsT_scale=s2[:],
                                 rhs=woc[:].bitcast(FP8X4), rhs_scale=wos[:], start=True, stop=True)
-            late[("o2", a)] = o2
-
-        def out_stats(a):
-            o2 = late[("o2", a)]
             hid = spool.tile([P, D_OUT], F32, name="hid")
             nc.vector.tensor_tensor(out=hid[:], in0=o2[:], in1=wob[:], op=ALU.add)
             nc.vector.tensor_scalar_max(out=hid[:], in0=hid[:], scalar1=0.0)
@@ -362,95 +366,25 @@ def tile_transformeraggregator_pb_kernel(
             res = spool.tile([P, D_OUT], F32, name="res")
             nc.vector.scalar_tensor_tensor(out=res[:], in0=hid[:], scalar=mv[:, 0:1], in1=lng[:],
                                            op0=ALU.subtract, op1=ALU.mult)
-            late[("st", a)] = (res, rstd)
-
-        def out_norm(a):
-            res, rstd = late[("st", a)]
             nc.vector.scalar_tensor_tensor(out=res[:], in0=res[:], scalar=rstd[:], in1=lnb[:],
                                            op0=ALU.mult, op1=ALU.add)
             nc.sync.dma_start(out=out_v[:, a, :], in_=res[:])
 
-        for r in range(QUAD):
-            piece_t(0, r)
-        spread_dt(1)
-        cos_open(0)
-        for t in range(4):
-            cos_plane(0, t)
-        cos_open(1)
-        for t in range(4):
-            cos_plane(1, t)
-        wvc = const.tile([P, 256], U32, name="wvc", align_bytes=64)
-        wvs = const.tile([P, 256], U8, name="wvs", align_bytes=64)
-        nc.vector.quantize_mx(out=wvc[:].bitcast(FP8X4), scales=wvs[:], in_=gw[:])
-        wc1 = const.tile([P, P], U32, name="wc1", align_bytes=64)
-        wcs = const.tile([P, P], U8, name="wcs", align_bytes=64)
-        nc.vector.quantize_mx(out=wc1[:].bitcast(FP8X4), scales=wcs[:], in_=wcg[:])
-        cos_close(0)
-        for r in range(4):
-            nc.vector.tensor_copy(out=wcc[32 * r:32 * (r + 1), P * r:P * (r + 1)].bitcast(I32),
-                                  in_=wc1[32 * r:32 * (r + 1), :].bitcast(I32))
-        cos_open(2)
-        for t in range(4):
-            cos_plane(2, t)
-        cos_close(1)
-        att_sum = const.tile([P, NPP * HEADS], F32, name="att_sum")
-        nc.vector.tensor_reduce(
-            out=att_sum[:].rearrange("p (a h) -> p a h", a=NPP),
-            in_=att_f[:].rearrange("p (a j h) -> p a h j", a=NPP, j=N_NEIGH),
-            axis=AX.X, op=ALU.add,
-        )
-
-        LAG_M, LAG_P = 2, 3
-        done_at = [GPN * a + GPN - 1 + LAG_P for a in range(NPP)]
-
-        for s in range(1, GROUPS + LAG_P + 5):
-            for hlf in range(2):
-                if s < GROUPS:
-                    piece_t(s, 2 * hlf)
-                    piece_t(s, 2 * hlf + 1)
-                if hlf == 0:
-                    if s - 1 < GROUPS:
-                        stage_q(s - 1)
-                    if s == 1:
-                        cos_close(2)
-                    for a in range(NPP):
-                        if done_at[a] + 2 == s:
-                            out_quantise(a)
-                    if s == 6:
-                        nc.vector.quantize_mx(out=woc[:].bitcast(FP8X4), scales=wos[:], in_=gwo[:])
-                else:
-                    if s == 5:
-                        pwo = ms_pool.tile([P, 4, P], BF16, name="ms")
-                        for t in range(4):
-                            nc.tensor.transpose(pwo[:, t, :], wo_sb[:, P * t:P * (t + 1)], ident_b[:])
-                        nc.scalar.copy(out=gwo[:].rearrange("p (c t) -> p c t", t=4),
-                                       in_=pwo[:].rearrange("p t c -> p c t"))
-                    if s % BATCH == 3 and s // BATCH + 2 < BATCHES:
-                        spread_dt(s // BATCH + 2)
-                    for a in range(NPP):
-                        if done_at[a] + 1 == s:
-                            out_transpose(a)
-                if 0 <= s - LAG_M < GROUPS:
-                    piece_m(s - LAG_M, 2 * hlf)
-                    piece_m(s - LAG_M, 2 * hlf + 1)
-                    if s < GROUPS:
-                        clock_pass(s - LAG_M)
-            for a in range(NPP):
-                if done_at[a] + 2 == s:
-                    out_matmul(a)
-            k_cos, t_cos = (s - 1) // BATCH, (s - 1) % BATCH
-            if EARLY + k_cos < len(COS_BATCHES):
-                if t_cos == 0:
-                    cos_open(EARLY + k_cos)
-                cos_plane(EARLY + k_cos, t_cos)
-            if t_cos == 0 and 1 <= k_cos and EARLY + k_cos - 1 < len(COS_BATCHES):
-                cos_close(EARLY + k_cos - 1)
-            if 0 <= s - LAG_P < GROUPS:
-                stage_p(s - LAG_P)
-            for a in range(NPP):
-                if done_at[a] == s:
-                    out_pool(a)
-                if done_at[a] + 3 == s:
-                    out_stats(a)
-                if done_at[a] + 4 == s:
-                    out_norm(a)
+        for s in range(GROUPS + 2):
+            if s < GROUPS:
+                stage_t(s)
+                if s + NX < GROUPS:
+                    load(s + NX)
+            if 1 <= s <= GROUPS:
+                stage_q(s - 1)
+            b_next, t_next = s // BATCH + EARLY, s % BATCH
+            if b_next < len(COS_BATCHES):
+                if t_next == 0:
+                    cos_open(b_next)
+                cos_plane(b_next, t_next)
+            if s % BATCH == 0 and EARLY <= s // BATCH + EARLY - 1 < len(COS_BATCHES):
+                cos_close(s // BATCH + EARLY - 1)
+            if 1 <= s <= GROUPS:
+                stage_m(s - 1)
+            if s >= 2:
+                stage_p(s - 2)

@@ -26,8 +26,6 @@ GROUPS = TILES // QUAD
 GPN = N_NEIGH // QUAD
 BATCH = 4
 BATCHES = GROUPS // BATCH
-COS_BATCHES = [(0, 1), (1, 1), (2, 2), (4, 4), (8, 4), (12, 4), (16, 4)]
-EARLY = 3
 NX = 6
 LN_EPS = 1e-5
 TWO_PI = 2.0 * math.pi
@@ -43,35 +41,25 @@ def tile_transformeraggregator_pb_kernel(
     with ExitStack() as ctx:
         const = ctx.enter_context(tc.tile_pool(name="const", bufs=1))
         xpool = ctx.enter_context(tc.tile_pool(name="xpool", bufs=1))
-        gpool = ctx.enter_context(tc.tile_pool(name="gpool", bufs=4))
+        gpool = ctx.enter_context(tc.tile_pool(name="gpool", bufs=3))
         cpool = ctx.enter_context(tc.tile_pool(name="cpool", bufs=2))
         spool = ctx.enter_context(tc.tile_pool(name="spool", bufs=2))
         tp_pool = ctx.enter_context(tc.psum_pool(name="tp", bufs=4))
         mo_pool = ctx.enter_context(tc.psum_pool(name="mo", bufs=2))
-        ms_pool = ctx.enter_context(tc.psum_pool(name="ms", bufs=2))
+        ms_pool = ctx.enter_context(tc.psum_pool(name="ms", bufs=1))
+        ac_pool = ctx.enter_context(tc.psum_pool(name="ac", bufs=1))
+        ctx.enter_context(tc.manual_schedule())
 
         node_v = neighbor_node_feature.rearrange("(p a) j c -> p (a j) c", a=NPP)
         edge_v = neighbor_edge_feature.rearrange("(p a) j c -> p (a j) c", a=NPP)
         out_v = out.rearrange("(p a) c -> p a c", a=NPP)
 
-        ident_f = const.tile([P, P], F32, name="ident_f")
-        make_identity(nc, ident_f[:])
-        ident_b = const.tile([P, P], BF16, name="ident_b")
-        make_identity(nc, ident_b[:])
-
-        xq = [xpool.tile([P, QUAD, K1], BF16, name="xq%d" % k) for k in range(NX)]
-
-        def load(g):
-            x = xq[g % NX]
-            nc.sync.dma_start(out=x[:, :, 0:D_NODE], in_=node_v[:, QUAD * g:QUAD * (g + 1), :])
-            nc.sync.dma_start(out=x[:, :, D_NODE:D_FEAT], in_=edge_v[:, QUAD * g:QUAD * (g + 1), :])
-
+        tb8 = const.tile([P, P], BF16, name="tb8")
+        nc.vector.memset(tb8[:], 0.0)
         nts = const.tile([P, TILES], BF16, name="nts")
         nc.scalar.dma_start(out=nts[:], in_=neighbor_ts.rearrange("(p a) j -> p (a j)", a=NPP))
         rts = const.tile([P, NPP], BF16, name="rts")
         nc.scalar.dma_start(out=rts[:], in_=root_ts.rearrange("(p a) -> p a", a=NPP))
-        tb8 = const.tile([P, P], BF16, name="tb8")
-        nc.vector.memset(tb8[:], 0.0)
         nc.scalar.dma_start(
             out=tb8[0:4, :].rearrange("t (r q) -> t r q", r=4),
             in_=time_w.rearrange("(t q) o -> t o q", t=4).to_broadcast([4, 4, 32]),
@@ -80,33 +68,53 @@ def tile_transformeraggregator_pb_kernel(
             out=tb8[4:8, :].rearrange("t (r q) -> t r q", r=4),
             in_=time_b.rearrange("(t o q) -> t o q", t=4, o=1).to_broadcast([4, 4, 32]),
         )
+        xq = [xpool.tile([P, QUAD, K1], BF16, name="xq%d" % k) for k in range(NX)]
+
+        def load(g):
+            x = xq[g % NX]
+            nc.sync.dma_start(out=x[:, :, 0:D_NODE], in_=node_v[:, QUAD * g:QUAD * (g + 1), :])
+            nc.sync.dma_start(out=x[:, :, D_NODE:D_FEAT], in_=edge_v[:, QUAD * g:QUAD * (g + 1), :])
+
         for r in range(QUAD):
             nc.sync.dma_start(out=xq[0][:, r, 0:D_NODE], in_=node_v[:, r, :])
             nc.sync.dma_start(out=xq[0][:, r, D_NODE:D_FEAT], in_=edge_v[:, r, :])
         wvz = const.tile([P, K1], BF16, name="wvz")
-        nc.gpsimd.memset(wvz[:, D_FEAT:K1], 0.0)
         nc.scalar.dma_start(out=wvz[:, 0:D_FEAT], in_=wv_w[:, 0:D_FEAT])
         wcos = const.tile([P, D_TIME], BF16, name="wcos")
         nc.scalar.dma_start(out=wcos[:], in_=wv_w[:, D_FEAT:K1])
         att_b = const.tile([P, TILES * HEADS], BF16, name="att_b")
         nc.scalar.dma_start(out=att_b[:], in_=att.rearrange("(p a) j h -> p (a j h)", a=NPP))
-        for k in range(NX):
-            nc.gpsimd.memset(xq[k][:, :, D_FEAT:K1], 0.0)
-        for g in range(1, NX):
-            load(g)
 
         wvb = const.tile([P, D_OUT], BF16, name="wvb")
-        nc.sync.dma_start(out=wvb[:], in_=wv_b.partition_broadcast(P))
+        nc.scalar.dma_start(out=wvb[:], in_=wv_b.partition_broadcast(P))
+
+        ident_f = const.tile([P, P], F32, name="ident_f")
+        make_identity(nc, ident_f[:])
+        ident_b = const.tile([P, P], BF16, name="ident_b")
+        make_identity(nc, ident_b[:])
+        nc.gpsimd.memset(xq[0][:, :, D_FEAT:K1], 0.0)
+        nc.gpsimd.memset(wvz[:, D_FEAT:K1], 0.0)
+        for k in range(1, NX):
+            nc.gpsimd.memset(xq[k][:, :, D_FEAT:K1], 0.0)
+        m_half = const.tile([P, 1], F32, name="m_half")
+        nc.gpsimd.memset(m_half[:], -0.5)
+        for g in range(1, NX - 2):
+            load(g)
         wo_sb = const.tile([P, D_OUT + D_NODE], BF16, name="wo_sb")
         nc.sync.dma_start(out=wo_sb[:], in_=wo_w)
         rootf = const.tile([P, NPP, D_NODE], BF16, name="rootf")
         nc.sync.dma_start(out=rootf[:], in_=root_node_feature.rearrange("(p a) c -> p a c", a=NPP))
+        for g in range(NX - 2, NX):
+            load(g)
         wob = const.tile([P, D_OUT], BF16, name="wob")
         nc.sync.dma_start(out=wob[:], in_=wo_b.partition_broadcast(P))
         lng = const.tile([P, D_OUT], BF16, name="lng")
         nc.sync.dma_start(out=lng[:], in_=ln_g.partition_broadcast(P))
         lnb = const.tile([P, D_OUT], BF16, name="lnb")
         nc.sync.dma_start(out=lnb[:], in_=ln_b.partition_broadcast(P))
+
+        warm = const.tile([P, 1], F32, name="warm")
+        nc.scalar.activation(out=warm[:], in_=ident_f[:, 0:1], func=ACT.Sin)
 
         def transpose_row_tile(words):
             tp = tp_pool.tile([P, 4, P], F32, name="tp")
@@ -121,174 +129,110 @@ def tile_transformeraggregator_pb_kernel(
             )
 
         dt_rows = const.tile([P, TILES], F32, name="dt_rows")
-        nc.vector.tensor_tensor(
-            out=dt_rows[:].rearrange("p (a j) -> p a j", a=NPP),
-            in0=rts[:].unsqueeze(2).to_broadcast([P, NPP, N_NEIGH]),
-            in1=nts[:].rearrange("p (a j) -> p a j", a=NPP),
-            op=ALU.subtract,
-        )
-        dt_rep = const.tile([P, TILES, 32], F32, name="dt_rep")
         dtq = const.tile([P, GROUPS * P], F32, name="dtq")
         TB = QUAD * BATCH
+        dt_reps = {}
 
-        def spread_dt(b):
+        def repeat_dt(b):
+            dt_rep = cpool.tile([P, TB, 32], F32, name="dt_rep", bufs=2)
             src = dt_rows[:, TB * b:TB * (b + 1)].unsqueeze(2).to_broadcast([P, TB, 32])
             if b == 0:
-                nc.vector.tensor_copy(out=dt_rep[:, TB * b:TB * (b + 1), :], in_=src)
+                nc.vector.tensor_copy(out=dt_rep[:], in_=src)
             else:
-                nc.gpsimd.tensor_scalar(out=dt_rep[:, TB * b:TB * (b + 1), :], in0=src, scalar1=1.0, scalar2=0.0,
-                                        op0=ALU.mult, op1=ALU.add)
-            tpd = ms_pool.tile([P, 4, P], F32, name="ms")
+                nc.gpsimd.tensor_scalar(out=dt_rep[:], in0=src, scalar1=1.0, scalar2=0.0, op0=ALU.mult, op1=ALU.add)
+            dt_reps[b] = dt_rep
+
+        def turn_dt(b):
+            tpd = tp_pool.tile([P, 4, P], F32, name="tp")
             for q in range(BATCH):
-                g = BATCH * b + q
                 nc.tensor.transpose(
-                    tpd[:, q, :], dt_rep[:, QUAD * g:QUAD * (g + 1), :].rearrange("p i c -> p (i c)"), ident_f[:]
+                    tpd[:, q, :], dt_reps[b][:, QUAD * q:QUAD * (q + 1), :].rearrange("p i c -> p (i c)"), ident_f[:]
                 )
-            nc.scalar.copy(out=dtq[:, 512 * b:512 * (b + 1)], in_=tpd[:].rearrange("p q w -> p (q w)"))
+            dst, src = dtq[:, 512 * b:512 * (b + 1)], tpd[:].rearrange("p q w -> p (q w)")
+            if b == 0:
+                nc.vector.tensor_copy(out=dst, in_=src)
+            else:
+                nc.scalar.copy(out=dst, in_=src)
 
-        spread_dt(0)
-
-        ps8 = ms_pool.tile([P, P], BF16, name="ms")
-        nc.tensor.transpose(ps8[:], tb8[:], ident_b[:])
         a_q = const.tile([P, 4], F32, name="a_q")
-        nc.vector.tensor_scalar(out=a_q[:], in0=ps8[:, 0:4], scalar1=1.0 / TWO_PI, scalar2=None, op0=ALU.mult)
         b_q = const.tile([P, 4], F32, name="b_q")
-        nc.vector.tensor_scalar(out=b_q[:], in0=ps8[:, 4:8], scalar1=1.0 / TWO_PI, scalar2=0.25,
-                                op0=ALU.mult, op1=ALU.add)
         b_2 = const.tile([P, 4], F32, name="b_2")
-        nc.vector.tensor_scalar(out=b_2[:], in0=ps8[:, 4:8], scalar1=0.5 * math.pi, scalar2=None, op0=ALU.add)
-
-        cos_state = {}
-
-        turns = const.tile([P, 4, 512], I32, name="turns")
-
-        def cos_open(b):
-            frac = cpool.tile([P, 4, 512], F32, name="frac")
-            planes = cpool.tile([P, 4, 512], BF16, name="planes")
-            cos_state[b] = (frac, planes)
-
-        def cos_turns(b, t):
-            g0, n = COS_BATCHES[b]
-            nc.vector.tensor_scalar(out=turns[:, t, 0:P * n], in0=dtq[:, P * g0:P * (g0 + n)], scalar1=a_q[:, t:t + 1],
-                                    scalar2=b_q[:, t:t + 1], op0=ALU.mult, op1=ALU.add)
-
-        def cos_plane(b, t):
-            g0, n = COS_BATCHES[b]
-            frac, planes = cos_state[b]
-            nc.vector.scalar_tensor_tensor(out=frac[:, t, 0:P * n], in0=dtq[:, P * g0:P * (g0 + n)],
-                                           scalar=a_q[:, t:t + 1], in1=turns[:, t, 0:P * n],
-                                           op0=ALU.mult, op1=ALU.subtract)
-            nc.scalar.activation(out=planes[:, t, 0:P * n], in_=frac[:, t, 0:P * n], func=ACT.Sin,
-                                 bias=b_2[:, t:t + 1], scale=TWO_PI)
-            if b + 1 < len(COS_BATCHES):
-                cos_turns(b + 1, t)
-
+        turns = {}
+        fracs = {}
+        planes = {}
         cos_codes = {}
 
-        def cos_close(b):
-            g0, n = COS_BATCHES[b]
-            planes = cos_state[b][1]
-            cos_g = cpool.tile([P, 2048], BF16, name="cos_g", align_bytes=64)
+        def cos_turns(b, t):
+            tn = cpool.tile([P, 512], I32, name="turns", bufs=3)
+            nc.vector.tensor_scalar(out=tn[:], in0=dtq[:, 512 * b:512 * (b + 1)], scalar1=a_q[:, t:t + 1],
+                                    scalar2=b_q[:, t:t + 1], op0=ALU.mult, op1=ALU.add)
+            turns[b, t] = tn
+
+        def cos_frac(b, t):
+            fr = cpool.tile([P, 512], F32, name="frac", bufs=3)
+            nc.vector.scalar_tensor_tensor(out=fr[:], in0=dtq[:, 512 * b:512 * (b + 1)], scalar=a_q[:, t:t + 1],
+                                           in1=turns[b, t][:], op0=ALU.mult, op1=ALU.subtract)
+            fracs[b, t] = fr
+
+        def cos_sine(b, t):
+            if t == 0:
+                pl_new = cpool.tile([P, 4, 512], BF16, name="planes")
+                planes[b] = pl_new
+            nc.scalar.activation(out=planes[b][:, t, :], in_=fracs[b, t][:], func=ACT.Sin,
+                                 bias=b_2[:, t:t + 1], scale=TWO_PI)
+
+        cos_groups = {}
+
+        def cos_gather(g):
+            b, q = g // BATCH, g % BATCH
+            cos_g = cpool.tile([P, 512], BF16, name="cos_g", align_bytes=64)
             nc.vector.tensor_copy(
-                out=cos_g[:, 0:512 * n].rearrange("p (c i t) -> p c t i", i=4, t=4),
-                in_=planes[:, :, 0:P * n].rearrange("p t (c i) -> p c t i", i=4),
+                out=cos_g[:].rearrange("p (c i t) -> p c t i", i=4, t=4),
+                in_=planes[b][:, :, P * q:P * (q + 1)].rearrange("p t (c i) -> p c t i", i=4),
             )
-            cc = cpool.tile([P, 512], U32, name="cc", align_bytes=64, bufs=4)
-            cs = cpool.tile([P, 512], U8, name="cs", align_bytes=64, bufs=4)
-            nc.vector.quantize_mx(out=cc[:, 0:P * n].bitcast(FP8X4), scales=cs[:, 0:P * n], in_=cos_g[:, 0:512 * n])
-            for g in range(g0, g0 + n):
-                cos_codes[g] = (cc, cs, P * (g - g0))
+            cos_groups[g] = cos_g
 
-        for t in range(4):
-            cos_turns(0, t)
-        for b in range(1, BATCHES):
-            spread_dt(b)
-        for b in range(EARLY):
-            cos_open(b)
-            for t in range(4):
-                cos_plane(b, t)
-            cos_close(b)
-
-        tpw = transpose_row_tile(wvz[:].bitcast(F32))
-        gw = const.tile([P, K1], BF16, name="gw", align_bytes=64)
-        evacuate(gw[:].bitcast(F32), tpw)
-        wvc = const.tile([P, 256], U32, name="wvc", align_bytes=64)
-        wvs = const.tile([P, 256], U8, name="wvs", align_bytes=64)
-        nc.vector.quantize_mx(out=wvc[:].bitcast(FP8X4), scales=wvs[:], in_=gw[:])
-
-        wcr = const.tile([P, 4, 4, 32], BF16, name="wcr")
-        nc.vector.tensor_copy(
-            out=wcr[:],
-            in_=wcos[:].rearrange("p (t q) -> p t q", t=4).unsqueeze(2).to_broadcast([P, 4, 4, 32]),
-        )
-        pw = ms_pool.tile([P, 4, P], BF16, name="ms")
-        for t in range(4):
-            nc.tensor.transpose(pw[:, t, :], wcr[:, t, :, :].rearrange("p r q -> p (r q)"), ident_b[:])
-        wcg = const.tile([P, 512], BF16, name="wcg", align_bytes=64)
-        nc.scalar.copy(out=wcg[:].rearrange("p (c t) -> p c t", t=4), in_=pw[:].rearrange("p t c -> p c t"))
-        wc1 = const.tile([P, P], U32, name="wc1", align_bytes=64)
-        wcs = const.tile([P, P], U8, name="wcs", align_bytes=64)
-        nc.vector.quantize_mx(out=wc1[:].bitcast(FP8X4), scales=wcs[:], in_=wcg[:])
-        wcc = const.tile([P, 512], U32, name="wcc", align_bytes=64)
-        nc.gpsimd.memset(wcc[:].bitcast(F32), 0.0)
-        for r in range(4):
-            nc.vector.tensor_copy(out=wcc[32 * r:32 * (r + 1), P * r:P * (r + 1)].bitcast(I32),
-                                  in_=wc1[32 * r:32 * (r + 1), :].bitcast(I32))
-
-        att_f = const.tile([P, TILES * HEADS], F32, name="att_f")
-        nc.gpsimd.tensor_scalar(out=att_f[:], in0=att_b[:], scalar1=1.0, scalar2=0.0, op0=ALU.mult, op1=ALU.add)
-        att_sum = const.tile([P, NPP * HEADS], F32, name="att_sum")
-        nc.vector.tensor_reduce(
-            out=att_sum[:].rearrange("p (a h) -> p a h", a=NPP),
-            in_=att_f[:].rearrange("p (a j h) -> p a h j", a=NPP, j=N_NEIGH),
-            axis=AX.X, op=ALU.add,
-        )
-        m_half = const.tile([P, 1], F32, name="m_half")
-        nc.gpsimd.memset(m_half[:], -0.5)
-
-        pwo = ms_pool.tile([P, 4, P], BF16, name="ms")
-        for t in range(4):
-            nc.tensor.transpose(pwo[:, t, :], wo_sb[:, P * t:P * (t + 1)], ident_b[:])
-        gwo = const.tile([P, 512], BF16, name="gwo", align_bytes=64)
-        nc.scalar.copy(out=gwo[:].rearrange("p (c t) -> p c t", t=4), in_=pwo[:].rearrange("p t c -> p c t"))
-        woc = const.tile([P, P], U32, name="woc", align_bytes=64)
-        wos = const.tile([P, P], U8, name="wos", align_bytes=64)
-        nc.vector.quantize_mx(out=woc[:].bitcast(FP8X4), scales=wos[:], in_=gwo[:])
+        def cos_quantize(g):
+            cc = cpool.tile([P, P], U32, name="cc", align_bytes=64, bufs=3)
+            cs = cpool.tile([P, P], U8, name="cs", align_bytes=64, bufs=3)
+            nc.vector.quantize_mx(out=cc[:].bitcast(FP8X4), scales=cs[:], in_=cos_groups[g][:])
+            cos_codes[g] = (cc, cs)
 
         grouped = {}
         codes = {}
         sums = {}
+        prods = {}
         accs = {}
-        pb = const.tile([P, NPP, D_OUT], BF16, name="pb")
+        g2s = {}
 
-        def stage_t(g):
-            xw = xq[g % NX][:].bitcast(F32)
-            gq = gpool.tile([P, QUAD * K1], BF16, name="gq", align_bytes=64)
-            gqw = gq[:].bitcast(F32)
-            for r in range(QUAD):
-                tp = transpose_row_tile(xw[:, r, :])
-                evacuate(gqw[:, 512 * r:512 * (r + 1)], tp)
-            grouped[g] = gq
+        def stage_t(g, r):
+            if r == 0:
+                gq_new = gpool.tile([P, QUAD * K1], BF16, name="gq", align_bytes=64)
+                grouped[g] = gq_new
+            tp = transpose_row_tile(xq[g % NX][:].bitcast(F32)[:, r, :])
+            evacuate(grouped[g][:].bitcast(F32)[:, 512 * r:512 * (r + 1)], tp)
 
-        def stage_q(g):
-            gq = grouped[g]
-            cq = gpool.tile([P, QUAD * 256], U32, name="cq", align_bytes=64)
-            sq = gpool.tile([P, QUAD * 256], U8, name="sq", align_bytes=64)
-            pieces = 4 if g == GROUPS - 1 else 2
-            wc = QUAD * 256 // pieces
-            for k in range(pieces):
-                nc.vector.quantize_mx(
-                    out=cq[:, wc * k:wc * (k + 1)].bitcast(FP8X4),
-                    scales=sq[:, wc * k:wc * (k + 1)],
-                    in_=gq[:, 4 * wc * k:4 * wc * (k + 1)],
-                )
-            codes[g] = (cq, sq)
-
-        def stage_m(g):
+        def stage_q(g, k, pieces=2):
+            if k == 0:
+                cq_new = gpool.tile([P, QUAD * 256], U32, name="cq", align_bytes=64)
+                sq_new = gpool.tile([P, QUAD * 256], U8, name="sq", align_bytes=64)
+                codes[g] = (cq_new, sq_new)
             cq, sq = codes[g]
-            cc, cs, cw = cos_codes[g]
-            mo = mo_pool.tile([P, QUAD, D_OUT], F32, name="mo")
-            for r in range(QUAD):
+            wc = QUAD * 256 // pieces
+            nc.vector.quantize_mx(
+                out=cq[:, wc * k:wc * (k + 1)].bitcast(FP8X4),
+                scales=sq[:, wc * k:wc * (k + 1)],
+                in_=grouped[g][:, 4 * wc * k:4 * wc * (k + 1)],
+            )
+
+        def stage_m(g, rows=range(QUAD)):
+            cq, sq = codes[g]
+            cc, cs = cos_codes[g]
+            if rows[0] == 0:
+                mo_new = mo_pool.tile([P, QUAD, D_OUT], F32, name="mo")
+                sums[g] = mo_new
+            mo = sums[g]
+            for r in rows:
                 for ps in range(2):
                     s = 256 * r + P * ps
                     nc.tensor.matmul_mx(
@@ -299,66 +243,81 @@ def tile_transformeraggregator_pb_kernel(
                     )
                 nc.tensor.matmul_mx(
                     out=mo[:, r, :],
-                    lhsT=cc[:, cw:cw + P].bitcast(FP8X4), lhsT_scale=cs[:, cw:cw + P],
+                    lhsT=cc[:].bitcast(FP8X4), lhsT_scale=cs[:],
                     rhs=wcc[:, P * r:P * (r + 1)].bitcast(FP8X4), rhs_scale=wcs[:],
                     start=False, stop=True,
                 )
-            sums[g] = mo
 
         def stage_p(g):
-            mo = sums[g]
+            prod = gpool.tile([P, QUAD * D_OUT], F32, name="prod")
+            nc.vector.tensor_tensor(
+                out=prod[:].rearrange("p (s c) -> p s c", c=D_HEAD),
+                in0=sums[g][:].rearrange("p r (h c) -> p (r h) c", h=HEADS),
+                in1=att_b[:, QUAD * HEADS * g:QUAD * HEADS * (g + 1)].unsqueeze(2).to_broadcast(
+                    [P, QUAD * HEADS, D_HEAD]),
+                op=ALU.mult,
+            )
+            prods[g] = prod
+
+        def stage_s(g):
             a = g // GPN
             if g % GPN == 0:
-                acc_new = spool.tile([P, QUAD, D_OUT], F32, name="acc")
+                acc_new = ac_pool.tile([P, P], F32, name="acc")
                 accs[a] = acc_new
-            acc = accs[a]
+                nc.tensor.matmul(acc_new[:], lhsT=bias_rows[:, a, :], rhs=ident_f[:], is_transpose=True,
+                                 start=True, stop=False)
             for r in range(QUAD):
-                i = QUAD * g + r
-                for h in range(HEADS):
-                    cols = slice(D_HEAD * h, D_HEAD * (h + 1))
-                    w = att_f[:, HEADS * i + h:HEADS * i + h + 1]
-                    if g % GPN == 0:
-                        nc.vector.tensor_scalar(out=acc[:, r, cols], in0=mo[:, r, cols], scalar1=w, scalar2=None,
-                                                op0=ALU.mult)
-                    else:
-                        nc.vector.scalar_tensor_tensor(out=acc[:, r, cols], in0=mo[:, r, cols], scalar=w,
-                                                       in1=acc[:, r, cols], op0=ALU.mult, op1=ALU.add)
-            if g % GPN == GPN - 1:
-                output_stage(a)
+                nc.tensor.matmul(accs[a][:], lhsT=prods[g][:, D_OUT * r:D_OUT * (r + 1)], rhs=ident_f[:],
+                                 is_transpose=True, start=False, stop=(g % GPN == GPN - 1 and r == QUAD - 1))
 
-        def output_stage(a):
-            acc = accs[a]
-            red = spool.tile([P, D_OUT], F32, name="red")
-            nc.vector.tensor_reduce(out=red[:], in_=acc[:].rearrange("p r c -> p c r"), axis=AX.X, op=ALU.add)
-            for h in range(HEADS):
-                cols = slice(D_HEAD * h, D_HEAD * (h + 1))
-                nc.vector.scalar_tensor_tensor(
-                    out=pb[:, a, cols], in0=wvb[:, cols], scalar=att_sum[:, HEADS * a + h:HEADS * a + h + 1],
-                    in1=red[:, cols], op0=ALU.mult, op1=ALU.add,
-                )
-            ps2 = ms_pool.tile([P, 4, P], BF16, name="ms")
-            nc.tensor.transpose(ps2[:, 0, :], pb[:, a, :], ident_b[:])
+        def root_stage(a):
+            ps2 = tp_pool.tile([P, 3, P], BF16, name="tp")
             for c in range(3):
-                nc.tensor.transpose(ps2[:, 1 + c, :], rootf[:, a, P * c:P * (c + 1)], ident_b[:])
-            g2 = spool.tile([P, 512], BF16, name="g2", align_bytes=64)
-            if a == NPP - 1:
-                nc.vector.tensor_copy(out=g2[:].rearrange("p (w t) -> p w t", t=4),
-                                      in_=ps2[:].rearrange("p t w -> p w t"))
-            else:
-                nc.scalar.copy(out=g2[:].rearrange("p (w t) -> p w t", t=4), in_=ps2[:].rearrange("p t w -> p w t"))
+                nc.tensor.transpose(ps2[:, c, :], rootf[:, a, P * c:P * (c + 1)], ident_b[:])
+            g2 = const.tile([P, P, 4], BF16, name="g2_%d" % a, align_bytes=64)
+            nc.scalar.copy(out=g2[:, :, 1:4], in_=ps2[:].rearrange("p t w -> p w t"))
+            g2s[a] = g2
+
+        outs = {}
+
+        def out_a(a):
+            nc.scalar.copy(out=g2s[a][:, :, 0], in_=accs[a][:])
+
+        def out_b(a):
             c2 = spool.tile([P, P], U32, name="c2", align_bytes=64)
             s2 = spool.tile([P, P], U8, name="s2", align_bytes=64)
-            nc.vector.quantize_mx(out=c2[:].bitcast(FP8X4), scales=s2[:], in_=g2[:])
+            nc.vector.quantize_mx(out=c2[:].bitcast(FP8X4), scales=s2[:], in_=g2s[a][:].rearrange("p w t -> p (w t)"))
+            outs[a] = [c2, s2]
+
+        def out_c(a):
+            c2, s2 = outs[a]
             o2 = ms_pool.tile([P, D_OUT], F32, name="ms")
             nc.tensor.matmul_mx(out=o2[:], lhsT=c2[:].bitcast(FP8X4), lhsT_scale=s2[:],
                                 rhs=woc[:].bitcast(FP8X4), rhs_scale=wos[:], start=True, stop=True)
+            outs[a] = [o2]
+
+        def out_d(a):
             hid = spool.tile([P, D_OUT], F32, name="hid")
-            nc.vector.tensor_tensor(out=hid[:], in0=o2[:], in1=wob[:], op=ALU.add)
+            nc.vector.tensor_tensor(out=hid[:], in0=outs[a][0][:], in1=wob[:], op=ALU.add)
+            outs[a] = [hid]
+
+        def out_e(a):
+            hid = outs[a][0]
             nc.vector.tensor_scalar_max(out=hid[:], in0=hid[:], scalar1=0.0)
+
+        def out_f(a):
+            hid = outs[a][0]
             stats = spool.tile([P, 6], F32, name="stats")
             nc.vector.bn_stats(out=stats[:], in_=hid[:])
+            outs[a].append(stats)
+
+        def out_g(a):
             mv = spool.tile([P, 2], F32, name="mv")
-            nc.vector.bn_aggr(out=mv[:], in_=stats[:])
+            nc.vector.bn_aggr(out=mv[:], in_=outs[a][1][:])
+            outs[a].append(mv)
+
+        def out_h(a):
+            hid, stats, mv = outs[a]
             ve = spool.tile([P, 1], F32, name="ve")
             nc.vector.tensor_scalar_add(out=ve[:], in0=mv[:, 1:2], scalar1=LN_EPS)
             rstd = spool.tile([P, 1], F32, name="rstd")
@@ -366,25 +325,174 @@ def tile_transformeraggregator_pb_kernel(
             res = spool.tile([P, D_OUT], F32, name="res")
             nc.vector.scalar_tensor_tensor(out=res[:], in0=hid[:], scalar=mv[:, 0:1], in1=lng[:],
                                            op0=ALU.subtract, op1=ALU.mult)
+            outs[a] = [res, rstd]
+
+        def out_i(a):
+            res, rstd = outs[a]
             nc.vector.scalar_tensor_tensor(out=res[:], in0=res[:], scalar=rstd[:], in1=lnb[:],
                                            op0=ALU.mult, op1=ALU.add)
             nc.sync.dma_start(out=out_v[:, a, :], in_=res[:])
 
-        for s in range(GROUPS + 2):
-            if s < GROUPS:
-                stage_t(s)
-                if s + NX < GROUPS:
-                    load(s + NX)
-            if 1 <= s <= GROUPS:
-                stage_q(s - 1)
-            b_next, t_next = s // BATCH + EARLY, s % BATCH
-            if b_next < len(COS_BATCHES):
-                if t_next == 0:
-                    cos_open(b_next)
-                cos_plane(b_next, t_next)
-            if s % BATCH == 0 and EARLY <= s // BATCH + EARLY - 1 < len(COS_BATCHES):
-                cos_close(s // BATCH + EARLY - 1)
-            if 1 <= s <= GROUPS:
-                stage_m(s - 1)
+        nc.vector.tensor_tensor(
+            out=dt_rows[:].rearrange("p (a j) -> p a j", a=NPP),
+            in0=rts[:].unsqueeze(2).to_broadcast([P, NPP, N_NEIGH]),
+            in1=nts[:].rearrange("p (a j) -> p a j", a=NPP),
+            op=ALU.subtract,
+        )
+        repeat_dt(0)
+        repeat_dt(1)
+        turn_dt(0)
+        ps8 = ac_pool.tile([P, P], BF16, name="acc")
+        nc.tensor.transpose(ps8[:], tb8[:], ident_b[:])
+        nc.vector.tensor_scalar(out=a_q[:], in0=ps8[:, 0:4], scalar1=1.0 / TWO_PI, scalar2=None, op0=ALU.mult)
+        nc.vector.tensor_scalar(out=b_q[:], in0=ps8[:, 4:8], scalar1=1.0 / TWO_PI, scalar2=0.25,
+                                op0=ALU.mult, op1=ALU.add)
+        nc.vector.tensor_scalar(out=b_2[:], in0=ps8[:, 4:8], scalar1=0.5 * math.pi, scalar2=None, op0=ALU.add)
+        cos_turns(0, 0)
+        cos_turns(0, 1)
+        cos_frac(0, 0)
+        cos_turns(0, 2)
+        cos_frac(0, 1)
+        cos_turns(0, 3)
+        cos_frac(0, 2)
+        stage_t(0, 0)
+        stage_t(0, 1)
+        cos_sine(0, 0)
+        stage_t(0, 2)
+        cos_sine(0, 1)
+        stage_t(0, 3)
+        cos_frac(0, 3)
+        cos_sine(0, 2)
+        cos_sine(0, 3)
+
+        wvc = const.tile([P, 256], U32, name="wvc", align_bytes=64)
+        wvs = const.tile([P, 256], U8, name="wvs", align_bytes=64)
+        gw = const.tile([P, K1], BF16, name="gw", align_bytes=64)
+        wcr = const.tile([P, 4, 4, 32], BF16, name="wcr")
+        wcg = const.tile([P, 512], BF16, name="wcg", align_bytes=64)
+        wc1 = const.tile([P, P], U32, name="wc1", align_bytes=64)
+        wcs = const.tile([P, P], U8, name="wcs", align_bytes=64)
+        wcc = const.tile([P, 512], U32, name="wcc", align_bytes=64)
+        nc.gpsimd.memset(wcc[:].bitcast(F32), 0.0)
+        nc.vector.tensor_copy(
+            out=wcr[:],
+            in_=wcos[:].rearrange("p (t q) -> p t q", t=4).unsqueeze(2).to_broadcast([P, 4, 4, 32]),
+        )
+        stage_q(0, 0)
+        tpw = transpose_row_tile(wvz[:].bitcast(F32))
+        evacuate(gw[:].bitcast(F32), tpw)
+        pw = mo_pool.tile([P, 4, P], BF16, name="mo")
+        for t in range(4):
+            nc.tensor.transpose(pw[:, t, :], wcr[:, t, :, :].rearrange("p r q -> p (r q)"), ident_b[:])
+        nc.scalar.copy(out=wcg[:].rearrange("p (c t) -> p c t", t=4), in_=pw[:].rearrange("p t c -> p c t"))
+        turn_dt(1)
+        stage_q(0, 1)
+        nc.vector.quantize_mx(out=wvc[:].bitcast(FP8X4), scales=wvs[:], in_=gw[:])
+        att_sum = const.tile([P, NPP * HEADS], F32, name="att_sum")
+        nc.vector.tensor_reduce(
+            out=att_sum[:].rearrange("p (a h) -> p a h", a=NPP),
+            in_=att_b[:].rearrange("p (a j h) -> p a h j", a=NPP, j=N_NEIGH),
+            axis=AX.X, op=ALU.add,
+        )
+        nc.vector.quantize_mx(out=wc1[:].bitcast(FP8X4), scales=wcs[:], in_=wcg[:])
+        cos_turns(1, 0)
+        for r in range(4):
+            nc.vector.tensor_copy(out=wcc[32 * r:32 * (r + 1), P * r:P * (r + 1)].bitcast(I32),
+                                  in_=wc1[32 * r:32 * (r + 1), :].bitcast(I32))
+        bias_rows = const.tile([P, NPP, D_OUT], F32, name="bias_rows")
+
+        def bias_stage():
+            for a in range(NPP):
+                nc.gpsimd.tensor_tensor(
+                    out=bias_rows[:, a, :].rearrange("p (h c) -> p h c", h=HEADS),
+                    in0=wvb[:].rearrange("p (h c) -> p h c", h=HEADS),
+                    in1=att_sum[:, HEADS * a:HEADS * (a + 1)].unsqueeze(2).to_broadcast([P, HEADS, D_HEAD]),
+                    op=ALU.mult,
+                )
+
+        woc = const.tile([P, P], U32, name="woc", align_bytes=64)
+        wos = const.tile([P, P], U8, name="wos", align_bytes=64)
+        gwo = const.tile([P, 512], BF16, name="gwo", align_bytes=64)
+
+        def wo_stage():
+            pwo = tp_pool.tile([P, 4, P], BF16, name="tp")
+            for t in range(4):
+                nc.tensor.transpose(pwo[:, t, :], wo_sb[:, P * t:P * (t + 1)], ident_b[:])
+            nc.scalar.copy(out=gwo[:].rearrange("p (c t) -> p c t", t=4), in_=pwo[:].rearrange("p t c -> p c t"))
+
+        def wo_quantize():
+            nc.vector.quantize_mx(out=woc[:].bitcast(FP8X4), scales=wos[:], in_=gwo[:])
+
+        extra = {1: [(bias_stage,)]}
+        for b in range(2, BATCHES):
+            extra.setdefault(4 * b - 7, []).append((repeat_dt, b))
+            extra.setdefault(4 * b - 6, []).append((turn_dt, b))
+        extra.setdefault(5, []).append((wo_stage,))
+        for a in range(NPP):
+            extra.setdefault(7 + a, []).append((root_stage, a))
+        woven = {}
+        for a in range(NPP - 1):
+            s0 = GPN * (a + 1) + 4
+            woven.setdefault(s0, []).extend([None, None, None, None, (out_b, a), (out_c, a)])
+            woven.setdefault(s0 + 1, []).extend([(out_d, a), (out_e, a), (out_f, a), (out_g, a), (out_h, a), (out_i, a)])
+        woven.setdefault(6, []).append((wo_quantize,))
+        for s in range(1, GROUPS):
+            pooled = (s - 4) // GPN - 1 if s >= GPN + 4 and (s - 4) % GPN == 0 else None
+            for r in range(QUAD):
+                stage_t(s, r)
+                if r == 1 and pooled is not None:
+                    out_a(pooled)
+            if s + NX - 1 < GROUPS:
+                load(s + NX - 1)
+            if s >= 4:
+                stage_s(s - 4)
+            for job in extra.get(s, ()):
+                job[0](*job[1:])
+            jobs = []
+            if s > 1:
+                jobs.append((stage_q, s - 1, 0))
+            if s + 3 < GROUPS:
+                jobs.append((cos_frac, (s + 3) // 4, (s + 3) % 4))
+            jobs.append((cos_gather, s - 1))
+            if s > 1:
+                jobs.append((stage_q, s - 1, 1))
+            jobs.append((cos_quantize, s - 1))
+            if s >= 3:
+                jobs.append((stage_p, s - 3))
+            if s + 4 < GROUPS:
+                jobs.append((cos_turns, (s + 4) // 4, (s + 4) % 4))
+            pieces = woven.get(s, [])
+            for k in range(max(len(jobs), len(pieces))):
+                if k < len(jobs):
+                    jobs[k][0](*jobs[k][1:])
+                    if jobs[k][0] == cos_frac:
+                        cos_sine((s + 3) // 4, (s + 3) % 4)
+                if k < len(pieces) and pieces[k]:
+                    pieces[k][0](*pieces[k][1:])
             if s >= 2:
-                stage_p(s - 2)
+                stage_m(s - 2)
+
+        last = GROUPS - 1
+        cos_gather(last)
+        stage_q(last, 0, 4)
+        out_d(NPP - 2)
+        cos_quantize(last)
+        out_e(NPP - 2)
+        stage_p(last - 2)
+        stage_q(last, 1, 4)
+        out_f(NPP - 2)
+        stage_s(last - 3)
+        stage_m(last - 1)
+        stage_s(last - 2)
+        stage_q(last, 2, 4)
+        out_g(NPP - 2)
+        stage_q(last, 3, 4)
+        out_h(NPP - 2)
+        stage_p(last - 1)
+        stage_m(last)
+        out_i(NPP - 2)
+        stage_s(last - 1)
+        stage_p(last)
+        stage_s(last)
+        for piece in (out_a, out_b, out_c, out_d, out_e, out_f, out_g, out_h, out_i):
+            piece(NPP - 1)

@@ -26,6 +26,8 @@ GROUPS = TILES // QUAD
 GPN = N_NEIGH // QUAD
 BATCH = 4
 BATCHES = GROUPS // BATCH
+PLAIN = (0,)
+PAIR = 2
 NX = 6
 LN_EPS = 1e-5
 TWO_PI = 2.0 * math.pi
@@ -45,8 +47,7 @@ def tile_transformeraggregator_pb_kernel(
         cpool = ctx.enter_context(tc.tile_pool(name="cpool", bufs=2))
         spool = ctx.enter_context(tc.tile_pool(name="spool", bufs=2))
         tp_pool = ctx.enter_context(tc.psum_pool(name="tp", bufs=4))
-        mo_pool = ctx.enter_context(tc.psum_pool(name="mo", bufs=2))
-        ms_pool = ctx.enter_context(tc.psum_pool(name="ms", bufs=1))
+        mo_pool = ctx.enter_context(tc.psum_pool(name="mo", bufs=3))
         ac_pool = ctx.enter_context(tc.psum_pool(name="ac", bufs=1))
         ctx.enter_context(tc.manual_schedule())
 
@@ -54,6 +55,8 @@ def tile_transformeraggregator_pb_kernel(
         edge_v = neighbor_edge_feature.rearrange("(p a) j c -> p (a j) c", a=NPP)
         out_v = out.rearrange("(p a) c -> p a c", a=NPP)
 
+        warm = const.tile([P, 1], F32, name="warm")
+        nc.vector.memset(warm[:], 0.0)
         tb8 = const.tile([P, P], BF16, name="tb8")
         nc.vector.memset(tb8[:], 0.0)
         nts = const.tile([P, TILES], BF16, name="nts")
@@ -68,25 +71,30 @@ def tile_transformeraggregator_pb_kernel(
             out=tb8[4:8, :].rearrange("t (r q) -> t r q", r=4),
             in_=time_b.rearrange("(t o q) -> t o q", t=4, o=1).to_broadcast([4, 4, 32]),
         )
+        warm_out = const.tile([P, 1], F32, name="warm_out")
+        nc.scalar.activation(out=warm_out[:], in_=warm[:], func=ACT.Sin)
+
         xq = [xpool.tile([P, QUAD, K1], BF16, name="xq%d" % k) for k in range(NX)]
 
-        def load(g):
+        def load(g, rows=slice(0, QUAD)):
             x = xq[g % NX]
-            nc.sync.dma_start(out=x[:, :, 0:D_NODE], in_=node_v[:, QUAD * g:QUAD * (g + 1), :])
-            nc.sync.dma_start(out=x[:, :, D_NODE:D_FEAT], in_=edge_v[:, QUAD * g:QUAD * (g + 1), :])
+            tiles = slice(QUAD * g + rows.start, QUAD * g + rows.stop)
+            nc.sync.dma_start(out=x[:, rows, 0:D_NODE], in_=node_v[:, tiles, :])
+            nc.sync.dma_start(out=x[:, rows, D_NODE:D_FEAT], in_=edge_v[:, tiles, :])
 
-        for r in range(QUAD):
-            nc.sync.dma_start(out=xq[0][:, r, 0:D_NODE], in_=node_v[:, r, :])
-            nc.sync.dma_start(out=xq[0][:, r, D_NODE:D_FEAT], in_=edge_v[:, r, :])
+        load(0, slice(0, 1))
+        load(0, slice(1, 2))
+        load(0, slice(2, 4))
         wvz = const.tile([P, K1], BF16, name="wvz")
-        nc.scalar.dma_start(out=wvz[:, 0:D_FEAT], in_=wv_w[:, 0:D_FEAT])
+        nc.sync.dma_start(out=wvz[:, 0:D_FEAT], in_=wv_w[:, 0:D_FEAT])
         wcos = const.tile([P, D_TIME], BF16, name="wcos")
-        nc.scalar.dma_start(out=wcos[:], in_=wv_w[:, D_FEAT:K1])
+        nc.sync.dma_start(out=wcos[:], in_=wv_w[:, D_FEAT:K1])
+        load(1)
         att_b = const.tile([P, TILES * HEADS], BF16, name="att_b")
-        nc.scalar.dma_start(out=att_b[:], in_=att.rearrange("(p a) j h -> p (a j h)", a=NPP))
-
+        nc.sync.dma_start(out=att_b[:], in_=att.rearrange("(p a) j h -> p (a j h)", a=NPP))
+        load(2)
         wvb = const.tile([P, D_OUT], BF16, name="wvb")
-        nc.scalar.dma_start(out=wvb[:], in_=wv_b.partition_broadcast(P))
+        nc.sync.dma_start(out=wvb[:], in_=wv_b.partition_broadcast(P))
 
         ident_f = const.tile([P, P], F32, name="ident_f")
         make_identity(nc, ident_f[:])
@@ -98,23 +106,19 @@ def tile_transformeraggregator_pb_kernel(
             nc.gpsimd.memset(xq[k][:, :, D_FEAT:K1], 0.0)
         m_half = const.tile([P, 1], F32, name="m_half")
         nc.gpsimd.memset(m_half[:], -0.5)
-        for g in range(1, NX - 2):
-            load(g)
+        load(3)
         wo_sb = const.tile([P, D_OUT + D_NODE], BF16, name="wo_sb")
         nc.sync.dma_start(out=wo_sb[:], in_=wo_w)
         rootf = const.tile([P, NPP, D_NODE], BF16, name="rootf")
         nc.sync.dma_start(out=rootf[:], in_=root_node_feature.rearrange("(p a) c -> p a c", a=NPP))
-        for g in range(NX - 2, NX):
-            load(g)
+        load(4)
+        load(5)
         wob = const.tile([P, D_OUT], BF16, name="wob")
         nc.sync.dma_start(out=wob[:], in_=wo_b.partition_broadcast(P))
         lng = const.tile([P, D_OUT], BF16, name="lng")
         nc.sync.dma_start(out=lng[:], in_=ln_g.partition_broadcast(P))
         lnb = const.tile([P, D_OUT], BF16, name="lnb")
         nc.sync.dma_start(out=lnb[:], in_=ln_b.partition_broadcast(P))
-
-        warm = const.tile([P, 1], F32, name="warm")
-        nc.scalar.activation(out=warm[:], in_=ident_f[:, 0:1], func=ACT.Sin)
 
         def transpose_row_tile(words):
             tp = tp_pool.tile([P, 4, P], F32, name="tp")
@@ -163,14 +167,16 @@ def tile_transformeraggregator_pb_kernel(
         cos_codes = {}
 
         def cos_turns(b, t):
+            cols = slice(512 * b, 512 * (b + 1))
             tn = cpool.tile([P, 512], I32, name="turns", bufs=3)
-            nc.vector.tensor_scalar(out=tn[:], in0=dtq[:, 512 * b:512 * (b + 1)], scalar1=a_q[:, t:t + 1],
+            nc.vector.tensor_scalar(out=tn[:], in0=dtq[:, cols], scalar1=a_q[:, t:t + 1],
                                     scalar2=b_q[:, t:t + 1], op0=ALU.mult, op1=ALU.add)
             turns[b, t] = tn
 
         def cos_frac(b, t):
+            cols = slice(512 * b, 512 * (b + 1))
             fr = cpool.tile([P, 512], F32, name="frac", bufs=3)
-            nc.vector.scalar_tensor_tensor(out=fr[:], in0=dtq[:, 512 * b:512 * (b + 1)], scalar=a_q[:, t:t + 1],
+            nc.vector.scalar_tensor_tensor(out=fr[:], in0=dtq[:, cols], scalar=a_q[:, t:t + 1],
                                            in1=turns[b, t][:], op0=ALU.mult, op1=ALU.subtract)
             fracs[b, t] = fr
 
@@ -184,19 +190,20 @@ def tile_transformeraggregator_pb_kernel(
         cos_groups = {}
 
         def cos_gather(g):
-            b, q = g // BATCH, g % BATCH
-            cos_g = cpool.tile([P, 512], BF16, name="cos_g", align_bytes=64)
+            b, c0 = g // BATCH, P * (g % BATCH)
+            cos_g = cpool.tile([P, PAIR * 512], BF16, name="cos_g", align_bytes=64)
             nc.vector.tensor_copy(
                 out=cos_g[:].rearrange("p (c i t) -> p c t i", i=4, t=4),
-                in_=planes[b][:, :, P * q:P * (q + 1)].rearrange("p t (c i) -> p c t i", i=4),
+                in_=planes[b][:, :, c0:c0 + PAIR * P].rearrange("p t (c i) -> p c t i", i=4),
             )
             cos_groups[g] = cos_g
 
         def cos_quantize(g):
-            cc = cpool.tile([P, P], U32, name="cc", align_bytes=64, bufs=3)
-            cs = cpool.tile([P, P], U8, name="cs", align_bytes=64, bufs=3)
+            cc = cpool.tile([P, PAIR * P], U32, name="cc", align_bytes=64, bufs=3)
+            cs = cpool.tile([P, PAIR * P], U8, name="cs", align_bytes=64, bufs=3)
             nc.vector.quantize_mx(out=cc[:].bitcast(FP8X4), scales=cs[:], in_=cos_groups[g][:])
-            cos_codes[g] = (cc, cs)
+            for k in range(PAIR):
+                cos_codes[g + k] = (cc[:, P * k:P * (k + 1)], cs[:, P * k:P * (k + 1)])
 
         grouped = {}
         codes = {}
@@ -212,10 +219,10 @@ def tile_transformeraggregator_pb_kernel(
             tp = transpose_row_tile(xq[g % NX][:].bitcast(F32)[:, r, :])
             evacuate(grouped[g][:].bitcast(F32)[:, 512 * r:512 * (r + 1)], tp)
 
-        def stage_q(g, k, pieces=2):
+        def stage_q(g, k=0, pieces=1):
             if k == 0:
-                cq_new = gpool.tile([P, QUAD * 256], U32, name="cq", align_bytes=64)
-                sq_new = gpool.tile([P, QUAD * 256], U8, name="sq", align_bytes=64)
+                cq_new = gpool.tile([P, QUAD * 256], U32, name="cq", align_bytes=64, bufs=4)
+                sq_new = gpool.tile([P, QUAD * 256], U8, name="sq", align_bytes=64, bufs=4)
                 codes[g] = (cq_new, sq_new)
             cq, sq = codes[g]
             wc = QUAD * 256 // pieces
@@ -225,13 +232,20 @@ def tile_transformeraggregator_pb_kernel(
                 in_=grouped[g][:, 4 * wc * k:4 * wc * (k + 1)],
             )
 
-        def stage_m(g, rows=range(QUAD)):
+        def stage_m(g, rows=range(QUAD), cos=True):
             cq, sq = codes[g]
             cc, cs = cos_codes[g]
-            if rows[0] == 0:
+            if cos:
                 mo_new = mo_pool.tile([P, QUAD, D_OUT], F32, name="mo")
                 sums[g] = mo_new
             mo = sums[g]
+            if cos:
+                nc.tensor.matmul_mx(
+                    out=mo[:].rearrange("p r c -> p (r c)"),
+                    lhsT=cc.bitcast(FP8X4), lhsT_scale=cs,
+                    rhs=wcc[:].bitcast(FP8X4), rhs_scale=wcs4[:],
+                    start=True, stop=False,
+                )
             for r in rows:
                 for ps in range(2):
                     s = 256 * r + P * ps
@@ -239,17 +253,11 @@ def tile_transformeraggregator_pb_kernel(
                         out=mo[:, r, :],
                         lhsT=cq[:, s:s + P].bitcast(FP8X4), lhsT_scale=sq[:, s:s + P],
                         rhs=wvc[:, P * ps:P * (ps + 1)].bitcast(FP8X4), rhs_scale=wvs[:, P * ps:P * (ps + 1)],
-                        start=(ps == 0), stop=False,
+                        start=False, stop=(r == QUAD - 1 and ps == 1),
                     )
-                nc.tensor.matmul_mx(
-                    out=mo[:, r, :],
-                    lhsT=cc[:].bitcast(FP8X4), lhsT_scale=cs[:],
-                    rhs=wcc[:, P * r:P * (r + 1)].bitcast(FP8X4), rhs_scale=wcs[:],
-                    start=False, stop=True,
-                )
 
         def stage_p(g):
-            prod = gpool.tile([P, QUAD * D_OUT], F32, name="prod")
+            prod = gpool.tile([P, QUAD * D_OUT], F32, name="prod", bufs=4)
             nc.vector.tensor_tensor(
                 out=prod[:].rearrange("p (s c) -> p s c", c=D_HEAD),
                 in0=sums[g][:].rearrange("p r (h c) -> p (r h) c", h=HEADS),
@@ -259,16 +267,17 @@ def tile_transformeraggregator_pb_kernel(
             )
             prods[g] = prod
 
-        def stage_s(g):
+        def stage_s(g, rows=range(QUAD)):
             a = g // GPN
-            if g % GPN == 0:
+            if g % GPN == 0 and rows[0] == 0:
                 acc_new = ac_pool.tile([P, P], F32, name="acc")
                 accs[a] = acc_new
                 nc.tensor.matmul(acc_new[:], lhsT=bias_rows[:, a, :], rhs=ident_f[:], is_transpose=True,
                                  start=True, stop=False)
-            for r in range(QUAD):
+            for r in rows:
                 nc.tensor.matmul(accs[a][:], lhsT=prods[g][:, D_OUT * r:D_OUT * (r + 1)], rhs=ident_f[:],
-                                 is_transpose=True, start=False, stop=(g % GPN == GPN - 1 and r == QUAD - 1))
+                                 is_transpose=r not in PLAIN, start=False,
+                                 stop=(g % GPN == GPN - 1 and r == QUAD - 1))
 
         def root_stage(a):
             ps2 = tp_pool.tile([P, 3, P], BF16, name="tp")
@@ -291,7 +300,7 @@ def tile_transformeraggregator_pb_kernel(
 
         def out_c(a):
             c2, s2 = outs[a]
-            o2 = ms_pool.tile([P, D_OUT], F32, name="ms")
+            o2 = mo_pool.tile([P, D_OUT], F32, name="mo")
             nc.tensor.matmul_mx(out=o2[:], lhsT=c2[:].bitcast(FP8X4), lhsT_scale=s2[:],
                                 rhs=woc[:].bitcast(FP8X4), rhs_scale=wos[:], start=True, stop=True)
             outs[a] = [o2]
@@ -372,13 +381,14 @@ def tile_transformeraggregator_pb_kernel(
         wcg = const.tile([P, 512], BF16, name="wcg", align_bytes=64)
         wc1 = const.tile([P, P], U32, name="wc1", align_bytes=64)
         wcs = const.tile([P, P], U8, name="wcs", align_bytes=64)
+        nc.gpsimd.memset(wcs[:].bitcast(I32), 0)
+        wcs4 = const.tile([P, 512], U8, name="wcs4", align_bytes=64)
         wcc = const.tile([P, 512], U32, name="wcc", align_bytes=64)
         nc.gpsimd.memset(wcc[:].bitcast(F32), 0.0)
         nc.vector.tensor_copy(
             out=wcr[:],
             in_=wcos[:].rearrange("p (t q) -> p t q", t=4).unsqueeze(2).to_broadcast([P, 4, 4, 32]),
         )
-        stage_q(0, 0)
         tpw = transpose_row_tile(wvz[:].bitcast(F32))
         evacuate(gw[:].bitcast(F32), tpw)
         pw = mo_pool.tile([P, 4, P], BF16, name="mo")
@@ -386,7 +396,7 @@ def tile_transformeraggregator_pb_kernel(
             nc.tensor.transpose(pw[:, t, :], wcr[:, t, :, :].rearrange("p r q -> p (r q)"), ident_b[:])
         nc.scalar.copy(out=wcg[:].rearrange("p (c t) -> p c t", t=4), in_=pw[:].rearrange("p t c -> p c t"))
         turn_dt(1)
-        stage_q(0, 1)
+        stage_q(0)
         nc.vector.quantize_mx(out=wvc[:].bitcast(FP8X4), scales=wvs[:], in_=gw[:])
         att_sum = const.tile([P, NPP * HEADS], F32, name="att_sum")
         nc.vector.tensor_reduce(
@@ -396,9 +406,15 @@ def tile_transformeraggregator_pb_kernel(
         )
         nc.vector.quantize_mx(out=wc1[:].bitcast(FP8X4), scales=wcs[:], in_=wcg[:])
         cos_turns(1, 0)
+        cos_turns(1, 1)
+        cos_frac(1, 0)
         for r in range(4):
             nc.vector.tensor_copy(out=wcc[32 * r:32 * (r + 1), P * r:P * (r + 1)].bitcast(I32),
                                   in_=wc1[32 * r:32 * (r + 1), :].bitcast(I32))
+        nc.vector.tensor_copy(
+            out=wcs4[:].bitcast(I32).rearrange("p (r c) -> p r c", r=4),
+            in_=wcs[:].bitcast(I32).unsqueeze(1).to_broadcast([P, 4, P // 4]),
+        )
         bias_rows = const.tile([P, NPP, D_OUT], F32, name="bias_rows")
 
         def bias_stage():
@@ -431,68 +447,82 @@ def tile_transformeraggregator_pb_kernel(
         for a in range(NPP):
             extra.setdefault(7 + a, []).append((root_stage, a))
         woven = {}
+        sums_first = {}
         for a in range(NPP - 1):
-            s0 = GPN * (a + 1) + 4
-            woven.setdefault(s0, []).extend([None, None, None, None, (out_b, a), (out_c, a)])
-            woven.setdefault(s0 + 1, []).extend([(out_d, a), (out_e, a), (out_f, a), (out_g, a), (out_h, a), (out_i, a)])
+            s0 = GPN * (a + 1) + 6
+            woven.setdefault(s0, []).extend([None, None, None, (out_b, a)])
+            sums_first[s0 + 1] = a
+            woven.setdefault(s0 + 2, []).extend([(out_d, a), (out_e, a), (out_f, a), (out_g, a), (out_h, a), (out_i, a)])
         woven.setdefault(6, []).append((wo_quantize,))
         for s in range(1, GROUPS):
-            pooled = (s - 4) // GPN - 1 if s >= GPN + 4 and (s - 4) % GPN == 0 else None
-            for r in range(QUAD):
-                stage_t(s, r)
-                if r == 1 and pooled is not None:
-                    out_a(pooled)
+            pooled = (s - 6) // GPN - 1 if s >= GPN + 6 and (s - 6) % GPN == 0 else None
+            if pooled is not None:
+                out_a(pooled)
+            stage_t(s, 0)
+            stage_t(s, 1)
+            if s >= 6 and pooled is None:
+                stage_s(s - 6, range(0, 1))
+            stage_t(s, 2)
+            stage_t(s, 3)
+            if s + 3 < GROUPS:
+                cos_sine((s + 3) // 4, (s + 3) % 4)
             if s + NX - 1 < GROUPS:
                 load(s + NX - 1)
-            if s >= 4:
-                stage_s(s - 4)
             for job in extra.get(s, ()):
                 job[0](*job[1:])
+            if s >= 6:
+                stage_s(s - 6, range(1 if pooled is None else 0, 4))
+            if s in sums_first:
+                out_c(sums_first[s])
+            if s >= 3:
+                stage_m(s - 3, range(0, 4), True)
             jobs = []
             if s > 1:
-                jobs.append((stage_q, s - 1, 0))
-            if s + 3 < GROUPS:
-                jobs.append((cos_frac, (s + 3) // 4, (s + 3) % 4))
-            jobs.append((cos_gather, s - 1))
-            if s > 1:
-                jobs.append((stage_q, s - 1, 1))
-            jobs.append((cos_quantize, s - 1))
-            if s >= 3:
-                jobs.append((stage_p, s - 3))
+                jobs.append((stage_q, s - 1))
+            if s % 2:
+                jobs.append((cos_gather, s - 1))
             if s + 4 < GROUPS:
-                jobs.append((cos_turns, (s + 4) // 4, (s + 4) % 4))
+                jobs.append((cos_frac, (s + 4) // 4, (s + 4) % 4))
+            if s % 2:
+                jobs.append((cos_quantize, s - 1))
+            if s >= 4:
+                jobs.append((stage_p, s - 4))
+            if s + 5 < GROUPS:
+                jobs.append((cos_turns, (s + 5) // 4, (s + 5) % 4))
             pieces = woven.get(s, [])
             for k in range(max(len(jobs), len(pieces))):
                 if k < len(jobs):
                     jobs[k][0](*jobs[k][1:])
-                    if jobs[k][0] == cos_frac:
-                        cos_sine((s + 3) // 4, (s + 3) % 4)
                 if k < len(pieces) and pieces[k]:
                     pieces[k][0](*pieces[k][1:])
-            if s >= 2:
-                stage_m(s - 2)
 
         last = GROUPS - 1
-        cos_gather(last)
+        prev = NPP - 2
         stage_q(last, 0, 4)
-        out_d(NPP - 2)
-        cos_quantize(last)
-        out_e(NPP - 2)
-        stage_p(last - 2)
+        stage_s(last - 5)
+        stage_m(last - 2)
         stage_q(last, 1, 4)
-        out_f(NPP - 2)
-        stage_s(last - 3)
-        stage_m(last - 1)
-        stage_s(last - 2)
+        stage_p(last - 3)
+        out_a(prev)
+        stage_s(last - 4)
         stage_q(last, 2, 4)
-        out_g(NPP - 2)
+        stage_m(last - 1)
+        out_b(prev)
+        stage_p(last - 2)
         stage_q(last, 3, 4)
-        out_h(NPP - 2)
+        stage_s(last - 3)
         stage_p(last - 1)
         stage_m(last)
-        out_i(NPP - 2)
+        out_c(prev)
+        stage_s(last - 2)
+        out_d(prev)
+        out_e(prev)
         stage_s(last - 1)
+        out_f(prev)
         stage_p(last)
+        out_g(prev)
         stage_s(last)
+        out_h(prev)
+        out_i(prev)
         for piece in (out_a, out_b, out_c, out_d, out_e, out_f, out_g, out_h, out_i):
             piece(NPP - 1)

@@ -26,7 +26,7 @@ GROUPS = TILES // QUAD
 GPN = N_NEIGH // QUAD
 BATCH = 4
 BATCHES = GROUPS // BATCH
-PLAIN = (0,)
+SHARED = range(0, 20, 2)
 PAIR = 2
 NX = 6
 LN_EPS = 1e-5
@@ -138,7 +138,7 @@ def tile_transformeraggregator_pb_kernel(
         dt_reps = {}
 
         def repeat_dt(b):
-            dt_rep = cpool.tile([P, TB, 32], F32, name="dt_rep", bufs=2)
+            dt_rep = cpool.tile([P, TB, 32], F32, name="dt_rep", bufs=3)
             src = dt_rows[:, TB * b:TB * (b + 1)].unsqueeze(2).to_broadcast([P, TB, 32])
             if b == 0:
                 nc.vector.tensor_copy(out=dt_rep[:], in_=src)
@@ -160,43 +160,37 @@ def tile_transformeraggregator_pb_kernel(
 
         a_q = const.tile([P, 4], F32, name="a_q")
         b_q = const.tile([P, 4], F32, name="b_q")
-        b_2 = const.tile([P, 4], F32, name="b_2")
+        angles = {}
         turns = {}
-        fracs = {}
-        planes = {}
+        cos_groups = {}
         cos_codes = {}
 
-        def cos_turns(b, t):
-            cols = slice(512 * b, 512 * (b + 1))
-            tn = cpool.tile([P, 512], I32, name="turns", bufs=3)
-            nc.vector.tensor_scalar(out=tn[:], in0=dtq[:, cols], scalar1=a_q[:, t:t + 1],
+        def cos_angle(b, t):
+            if t == 0:
+                an_new = cpool.tile([P, 4, 512], F32, name="angle", bufs=3)
+                angles[b] = an_new
+            nc.vector.tensor_scalar(out=angles[b][:, t, :], in0=dtq[:, 512 * b:512 * (b + 1)], scalar1=a_q[:, t:t + 1],
                                     scalar2=b_q[:, t:t + 1], op0=ALU.mult, op1=ALU.add)
+
+        def cos_turns(b, t):
+            tn = cpool.tile([P, 2, 512], I32, name="turns")
+            nc.vector.tensor_copy(out=tn[:], in_=angles[b][:, t:t + 2, :])
             turns[b, t] = tn
 
         def cos_frac(b, t):
-            cols = slice(512 * b, 512 * (b + 1))
-            fr = cpool.tile([P, 512], F32, name="frac", bufs=3)
-            nc.vector.scalar_tensor_tensor(out=fr[:], in0=dtq[:, cols], scalar=a_q[:, t:t + 1],
-                                           in1=turns[b, t][:], op0=ALU.mult, op1=ALU.subtract)
-            fracs[b, t] = fr
+            part = angles[b][:, t:t + 2, :]
+            nc.vector.tensor_tensor(out=part, in0=part, in1=turns[b, t][:], op=ALU.subtract)
 
-        def cos_sine(b, t):
-            if t == 0:
-                pl_new = cpool.tile([P, 4, 512], BF16, name="planes")
-                planes[b] = pl_new
-            nc.scalar.activation(out=planes[b][:, t, :], in_=fracs[b, t][:], func=ACT.Sin,
-                                 bias=b_2[:, t:t + 1], scale=TWO_PI)
-
-        cos_groups = {}
-
-        def cos_gather(g):
-            b, c0 = g // BATCH, P * (g % BATCH)
-            cos_g = cpool.tile([P, PAIR * 512], BF16, name="cos_g", align_bytes=64)
-            nc.vector.tensor_copy(
-                out=cos_g[:].rearrange("p (c i t) -> p c t i", i=4, t=4),
-                in_=planes[b][:, :, c0:c0 + PAIR * P].rearrange("p t (c i) -> p c t i", i=4),
+        def cos_sine(g):
+            b, c0, k = g // BATCH, P * (g % BATCH), g % PAIR
+            if k == 0:
+                cg_new = cpool.tile([P, PAIR * 512], BF16, name="cos_g", align_bytes=64)
+                cos_groups[g] = cg_new
+            nc.scalar.activation(
+                out=cos_groups[g - k][:, 512 * k:512 * (k + 1)].rearrange("p (c i t) -> p c t i", i=4, t=4),
+                in_=angles[b][:, :, c0:c0 + P].rearrange("p t (c i) -> p c t i", i=4),
+                func=ACT.Sin, scale=TWO_PI,
             )
-            cos_groups[g] = cos_g
 
         def cos_quantize(g):
             cc = cpool.tile([P, PAIR * P], U32, name="cc", align_bytes=64, bufs=3)
@@ -256,7 +250,27 @@ def tile_transformeraggregator_pb_kernel(
                         start=False, stop=(r == QUAD - 1 and ps == 1),
                     )
 
+        def weigh_half(g):
+            prod = gpool.tile([P, QUAD * D_OUT], F32, name="prod", bufs=4)
+            prods[g] = prod
+            for i in range(2 * HEADS):
+                w = QUAD * HEADS * g + i
+                nc.scalar.activation(
+                    out=prod[:, D_HEAD * i:D_HEAD * (i + 1)],
+                    in_=sums[g][:, i // HEADS, D_HEAD * (i % HEADS):D_HEAD * (i % HEADS + 1)],
+                    func=ACT.Copy, scale=att_f[:, w:w + 1],
+                )
+
         def stage_p(g):
+            if g in SHARED:
+                for i in range(2 * HEADS):
+                    part = prods[g][:, D_HEAD * i:D_HEAD * (i + 1)]
+                    w = QUAD * HEADS * g + 2 * HEADS + i
+                    nc.vector.scalar_tensor_tensor(
+                        out=part, in0=sums[g][:, 2 + i // HEADS, D_HEAD * (i % HEADS):D_HEAD * (i % HEADS + 1)],
+                        scalar=att_f[:, w:w + 1], in1=part, op0=ALU.mult, op1=ALU.add,
+                    )
+                return
             prod = gpool.tile([P, QUAD * D_OUT], F32, name="prod", bufs=4)
             nc.vector.tensor_tensor(
                 out=prod[:].rearrange("p (s c) -> p s c", c=D_HEAD),
@@ -274,10 +288,10 @@ def tile_transformeraggregator_pb_kernel(
                 accs[a] = acc_new
                 nc.tensor.matmul(acc_new[:], lhsT=bias_rows[:, a, :], rhs=ident_f[:], is_transpose=True,
                                  start=True, stop=False)
-            for r in rows:
+            for r in range(2) if g in SHARED else rows:
                 nc.tensor.matmul(accs[a][:], lhsT=prods[g][:, D_OUT * r:D_OUT * (r + 1)], rhs=ident_f[:],
-                                 is_transpose=r not in PLAIN, start=False,
-                                 stop=(g % GPN == GPN - 1 and r == QUAD - 1))
+                                 is_transpose=True, start=False,
+                                 stop=(g % GPN == GPN - 1 and r == (1 if g in SHARED else QUAD - 1)))
 
         def root_stage(a):
             ps2 = tp_pool.tile([P, 3, P], BF16, name="tp")
@@ -348,31 +362,25 @@ def tile_transformeraggregator_pb_kernel(
             in1=nts[:].rearrange("p (a j) -> p a j", a=NPP),
             op=ALU.subtract,
         )
-        repeat_dt(0)
-        repeat_dt(1)
+        for b in range(3):
+            repeat_dt(b)
         turn_dt(0)
         ps8 = ac_pool.tile([P, P], BF16, name="acc")
         nc.tensor.transpose(ps8[:], tb8[:], ident_b[:])
         nc.vector.tensor_scalar(out=a_q[:], in0=ps8[:, 0:4], scalar1=1.0 / TWO_PI, scalar2=None, op0=ALU.mult)
         nc.vector.tensor_scalar(out=b_q[:], in0=ps8[:, 4:8], scalar1=1.0 / TWO_PI, scalar2=0.25,
                                 op0=ALU.mult, op1=ALU.add)
-        nc.vector.tensor_scalar(out=b_2[:], in0=ps8[:, 4:8], scalar1=0.5 * math.pi, scalar2=None, op0=ALU.add)
-        cos_turns(0, 0)
-        cos_turns(0, 1)
-        cos_frac(0, 0)
-        cos_turns(0, 2)
-        cos_frac(0, 1)
-        cos_turns(0, 3)
-        cos_frac(0, 2)
+        for t in range(4):
+            cos_angle(0, t)
         stage_t(0, 0)
         stage_t(0, 1)
-        cos_sine(0, 0)
+        cos_turns(0, 0)
+        cos_turns(0, 2)
+        cos_frac(0, 0)
+        cos_frac(0, 2)
         stage_t(0, 2)
-        cos_sine(0, 1)
         stage_t(0, 3)
-        cos_frac(0, 3)
-        cos_sine(0, 2)
-        cos_sine(0, 3)
+        turn_dt(1)
 
         wvc = const.tile([P, 256], U32, name="wvc", align_bytes=64)
         wvs = const.tile([P, 256], U8, name="wvs", align_bytes=64)
@@ -389,15 +397,21 @@ def tile_transformeraggregator_pb_kernel(
             out=wcr[:],
             in_=wcos[:].rearrange("p (t q) -> p t q", t=4).unsqueeze(2).to_broadcast([P, 4, 4, 32]),
         )
+        stage_q(0)
         tpw = transpose_row_tile(wvz[:].bitcast(F32))
         evacuate(gw[:].bitcast(F32), tpw)
+        cos_sine(0)
         pw = mo_pool.tile([P, 4, P], BF16, name="mo")
         for t in range(4):
             nc.tensor.transpose(pw[:, t, :], wcr[:, t, :, :].rearrange("p r q -> p (r q)"), ident_b[:])
         nc.scalar.copy(out=wcg[:].rearrange("p (c t) -> p c t", t=4), in_=pw[:].rearrange("p t c -> p c t"))
-        turn_dt(1)
-        stage_q(0)
+        cos_sine(1)
+        turn_dt(2)
+        for t in range(4):
+            cos_angle(1, t)
         nc.vector.quantize_mx(out=wvc[:].bitcast(FP8X4), scales=wvs[:], in_=gw[:])
+        att_f = const.tile([P, TILES * HEADS], F32, name="att_f")
+        nc.gpsimd.tensor_scalar(out=att_f[:], in0=att_b[:], scalar1=1.0, scalar2=0.0, op0=ALU.mult, op1=ALU.add)
         att_sum = const.tile([P, NPP * HEADS], F32, name="att_sum")
         nc.vector.tensor_reduce(
             out=att_sum[:].rearrange("p (a h) -> p a h", a=NPP),
@@ -406,8 +420,6 @@ def tile_transformeraggregator_pb_kernel(
         )
         nc.vector.quantize_mx(out=wc1[:].bitcast(FP8X4), scales=wcs[:], in_=wcg[:])
         cos_turns(1, 0)
-        cos_turns(1, 1)
-        cos_frac(1, 0)
         for r in range(4):
             nc.vector.tensor_copy(out=wcc[32 * r:32 * (r + 1), P * r:P * (r + 1)].bitcast(I32),
                                   in_=wc1[32 * r:32 * (r + 1), :].bitcast(I32))
@@ -415,6 +427,7 @@ def tile_transformeraggregator_pb_kernel(
             out=wcs4[:].bitcast(I32).rearrange("p (r c) -> p r c", r=4),
             in_=wcs[:].bitcast(I32).unsqueeze(1).to_broadcast([P, 4, P // 4]),
         )
+        cos_frac(1, 0)
         bias_rows = const.tile([P, NPP, D_OUT], F32, name="bias_rows")
 
         def bias_stage():
@@ -440,55 +453,57 @@ def tile_transformeraggregator_pb_kernel(
             nc.vector.quantize_mx(out=woc[:].bitcast(FP8X4), scales=wos[:], in_=gwo[:])
 
         extra = {1: [(bias_stage,)]}
-        for b in range(2, BATCHES):
-            extra.setdefault(4 * b - 7, []).append((repeat_dt, b))
-            extra.setdefault(4 * b - 6, []).append((turn_dt, b))
+        for b in range(3, BATCHES):
+            extra.setdefault(4 * b - 10, []).append((repeat_dt, b))
+            extra.setdefault(4 * b - 8, []).append((turn_dt, b))
         extra.setdefault(5, []).append((wo_stage,))
         for a in range(NPP):
             extra.setdefault(7 + a, []).append((root_stage, a))
         woven = {}
         sums_first = {}
         for a in range(NPP - 1):
-            s0 = GPN * (a + 1) + 6
+            s0 = GPN * (a + 1) + 4
             woven.setdefault(s0, []).extend([None, None, None, (out_b, a)])
             sums_first[s0 + 1] = a
             woven.setdefault(s0 + 2, []).extend([(out_d, a), (out_e, a), (out_f, a), (out_g, a), (out_h, a), (out_i, a)])
         woven.setdefault(6, []).append((wo_quantize,))
         for s in range(1, GROUPS):
-            pooled = (s - 6) // GPN - 1 if s >= GPN + 6 and (s - 6) % GPN == 0 else None
+            pooled = (s - 4) // GPN - 1 if s >= GPN + 4 and (s - 4) % GPN == 0 else None
             if pooled is not None:
                 out_a(pooled)
             stage_t(s, 0)
+            if s - 3 in SHARED:
+                weigh_half(s - 3)
             stage_t(s, 1)
-            if s >= 6 and pooled is None:
-                stage_s(s - 6, range(0, 1))
             stage_t(s, 2)
             stage_t(s, 3)
-            if s + 3 < GROUPS:
-                cos_sine((s + 3) // 4, (s + 3) % 4)
+            if s + 1 < GROUPS:
+                cos_sine(s + 1)
             if s + NX - 1 < GROUPS:
                 load(s + NX - 1)
             for job in extra.get(s, ()):
                 job[0](*job[1:])
-            if s >= 6:
-                stage_s(s - 6, range(1 if pooled is None else 0, 4))
+            if s >= 4:
+                stage_s(s - 4, range(0, 4))
             if s in sums_first:
                 out_c(sums_first[s])
-            if s >= 3:
-                stage_m(s - 3, range(0, 4), True)
+            if s >= 2:
+                stage_m(s - 2, range(0, 4), True)
             jobs = []
+            if s % 2 == 0 and (s + 4 - s % 4) // 4 < BATCHES:
+                jobs.append((cos_frac, (s + 4 - s % 4) // 4, s % 4))
             if s > 1:
-                jobs.append((stage_q, s - 1))
-            if s % 2:
-                jobs.append((cos_gather, s - 1))
-            if s + 4 < GROUPS:
-                jobs.append((cos_frac, (s + 4) // 4, (s + 4) % 4))
+                jobs.append((stage_q, s - 1, 0, 2))
+            if s + 7 < GROUPS:
+                jobs.append((cos_angle, (s + 7) // 4, (s + 7) % 4))
+            if s > 1:
+                jobs.append((stage_q, s - 1, 1, 2))
             if s % 2:
                 jobs.append((cos_quantize, s - 1))
-            if s >= 4:
-                jobs.append((stage_p, s - 4))
-            if s + 5 < GROUPS:
-                jobs.append((cos_turns, (s + 5) // 4, (s + 5) % 4))
+            if s >= 3:
+                jobs.append((stage_p, s - 3))
+            if s % 2 and (s + 3) // 4 + s % 4 // 3 < BATCHES:
+                jobs.append((cos_turns, (s + 3) // 4 + s % 4 // 3, (s + 1) % 4))
             pieces = woven.get(s, [])
             for k in range(max(len(jobs), len(pieces))):
                 if k < len(jobs):
@@ -499,30 +514,30 @@ def tile_transformeraggregator_pb_kernel(
         last = GROUPS - 1
         prev = NPP - 2
         stage_q(last, 0, 4)
-        stage_s(last - 5)
-        stage_m(last - 2)
-        stage_q(last, 1, 4)
-        stage_p(last - 3)
-        out_a(prev)
-        stage_s(last - 4)
-        stage_q(last, 2, 4)
-        stage_m(last - 1)
-        out_b(prev)
-        stage_p(last - 2)
-        stage_q(last, 3, 4)
         stage_s(last - 3)
+        stage_q(last, 1, 4)
+        if last - 2 in SHARED:
+            weigh_half(last - 2)
+        stage_p(last - 2)
+        stage_m(last - 1)
+        stage_q(last, 2, 4)
+        out_c(prev)
+        stage_q(last, 3, 4)
+        stage_s(last - 2)
+        if last - 1 in SHARED:
+            weigh_half(last - 1)
         stage_p(last - 1)
         stage_m(last)
-        out_c(prev)
-        stage_s(last - 2)
         out_d(prev)
         out_e(prev)
         stage_s(last - 1)
         out_f(prev)
-        stage_p(last)
         out_g(prev)
-        stage_s(last)
+        if last in SHARED:
+            weigh_half(last)
+        stage_p(last)
         out_h(prev)
+        stage_s(last)
         out_i(prev)
         for piece in (out_a, out_b, out_c, out_d, out_e, out_f, out_g, out_h, out_i):
             piece(NPP - 1)

@@ -138,7 +138,7 @@ def tile_transformeraggregator_pb_kernel(
         dt_reps = {}
 
         def repeat_dt(b):
-            dt_rep = cpool.tile([P, TB, 32], F32, name="dt_rep", bufs=3)
+            dt_rep = cpool.tile([P, TB, 32], F32, name="dt_rep", bufs=2)
             src = dt_rows[:, TB * b:TB * (b + 1)].unsqueeze(2).to_broadcast([P, TB, 32])
             if b == 0:
                 nc.vector.tensor_copy(out=dt_rep[:], in_=src)
@@ -160,37 +160,43 @@ def tile_transformeraggregator_pb_kernel(
 
         a_q = const.tile([P, 4], F32, name="a_q")
         b_q = const.tile([P, 4], F32, name="b_q")
-        angles = {}
+        b_2 = const.tile([P, 4], F32, name="b_2")
         turns = {}
-        cos_groups = {}
+        fracs = {}
+        planes = {}
         cos_codes = {}
 
-        def cos_angle(b, t):
-            if t == 0:
-                an_new = cpool.tile([P, 4, 512], F32, name="angle", bufs=3)
-                angles[b] = an_new
-            nc.vector.tensor_scalar(out=angles[b][:, t, :], in0=dtq[:, 512 * b:512 * (b + 1)], scalar1=a_q[:, t:t + 1],
-                                    scalar2=b_q[:, t:t + 1], op0=ALU.mult, op1=ALU.add)
-
         def cos_turns(b, t):
-            tn = cpool.tile([P, 2, 512], I32, name="turns")
-            nc.vector.tensor_copy(out=tn[:], in_=angles[b][:, t:t + 2, :])
+            cols = slice(512 * b, 512 * (b + 1))
+            tn = cpool.tile([P, 512], I32, name="turns", bufs=3)
+            nc.vector.tensor_scalar(out=tn[:], in0=dtq[:, cols], scalar1=a_q[:, t:t + 1],
+                                    scalar2=b_q[:, t:t + 1], op0=ALU.mult, op1=ALU.add)
             turns[b, t] = tn
 
         def cos_frac(b, t):
-            part = angles[b][:, t:t + 2, :]
-            nc.vector.tensor_tensor(out=part, in0=part, in1=turns[b, t][:], op=ALU.subtract)
+            cols = slice(512 * b, 512 * (b + 1))
+            fr = cpool.tile([P, 512], F32, name="frac", bufs=3)
+            nc.vector.scalar_tensor_tensor(out=fr[:], in0=dtq[:, cols], scalar=a_q[:, t:t + 1],
+                                           in1=turns[b, t][:], op0=ALU.mult, op1=ALU.subtract)
+            fracs[b, t] = fr
 
-        def cos_sine(g):
-            b, c0, k = g // BATCH, P * (g % BATCH), g % PAIR
-            if k == 0:
-                cg_new = cpool.tile([P, PAIR * 512], BF16, name="cos_g", align_bytes=64)
-                cos_groups[g] = cg_new
-            nc.scalar.activation(
-                out=cos_groups[g - k][:, 512 * k:512 * (k + 1)].rearrange("p (c i t) -> p c t i", i=4, t=4),
-                in_=angles[b][:, :, c0:c0 + P].rearrange("p t (c i) -> p c t i", i=4),
-                func=ACT.Sin, scale=TWO_PI,
+        def cos_sine(b, t):
+            if t == 0:
+                pl_new = cpool.tile([P, 4, 512], BF16, name="planes")
+                planes[b] = pl_new
+            nc.scalar.activation(out=planes[b][:, t, :], in_=fracs[b, t][:], func=ACT.Sin,
+                                 bias=b_2[:, t:t + 1], scale=TWO_PI)
+
+        cos_groups = {}
+
+        def cos_gather(g):
+            b, c0 = g // BATCH, P * (g % BATCH)
+            cos_g = cpool.tile([P, PAIR * 512], BF16, name="cos_g", align_bytes=64)
+            nc.vector.tensor_copy(
+                out=cos_g[:].rearrange("p (c i t) -> p c t i", i=4, t=4),
+                in_=planes[b][:, :, c0:c0 + PAIR * P].rearrange("p t (c i) -> p c t i", i=4),
             )
+            cos_groups[g] = cos_g
 
         def cos_quantize(g):
             cc = cpool.tile([P, PAIR * P], U32, name="cc", align_bytes=64, bufs=3)
@@ -362,25 +368,31 @@ def tile_transformeraggregator_pb_kernel(
             in1=nts[:].rearrange("p (a j) -> p a j", a=NPP),
             op=ALU.subtract,
         )
-        for b in range(3):
-            repeat_dt(b)
+        repeat_dt(0)
+        repeat_dt(1)
         turn_dt(0)
         ps8 = ac_pool.tile([P, P], BF16, name="acc")
         nc.tensor.transpose(ps8[:], tb8[:], ident_b[:])
         nc.vector.tensor_scalar(out=a_q[:], in0=ps8[:, 0:4], scalar1=1.0 / TWO_PI, scalar2=None, op0=ALU.mult)
         nc.vector.tensor_scalar(out=b_q[:], in0=ps8[:, 4:8], scalar1=1.0 / TWO_PI, scalar2=0.25,
                                 op0=ALU.mult, op1=ALU.add)
-        for t in range(4):
-            cos_angle(0, t)
+        nc.vector.tensor_scalar(out=b_2[:], in0=ps8[:, 4:8], scalar1=0.5 * math.pi, scalar2=None, op0=ALU.add)
+        cos_turns(0, 0)
+        cos_turns(0, 1)
+        cos_frac(0, 0)
+        cos_turns(0, 2)
+        cos_frac(0, 1)
+        cos_turns(0, 3)
+        cos_frac(0, 2)
         stage_t(0, 0)
         stage_t(0, 1)
-        cos_turns(0, 0)
-        cos_turns(0, 2)
-        cos_frac(0, 0)
-        cos_frac(0, 2)
+        cos_sine(0, 0)
         stage_t(0, 2)
+        cos_sine(0, 1)
         stage_t(0, 3)
-        turn_dt(1)
+        cos_frac(0, 3)
+        cos_sine(0, 2)
+        cos_sine(0, 3)
 
         wvc = const.tile([P, 256], U32, name="wvc", align_bytes=64)
         wvs = const.tile([P, 256], U8, name="wvs", align_bytes=64)
@@ -397,18 +409,14 @@ def tile_transformeraggregator_pb_kernel(
             out=wcr[:],
             in_=wcos[:].rearrange("p (t q) -> p t q", t=4).unsqueeze(2).to_broadcast([P, 4, 4, 32]),
         )
-        stage_q(0)
         tpw = transpose_row_tile(wvz[:].bitcast(F32))
         evacuate(gw[:].bitcast(F32), tpw)
-        cos_sine(0)
         pw = mo_pool.tile([P, 4, P], BF16, name="mo")
         for t in range(4):
             nc.tensor.transpose(pw[:, t, :], wcr[:, t, :, :].rearrange("p r q -> p (r q)"), ident_b[:])
         nc.scalar.copy(out=wcg[:].rearrange("p (c t) -> p c t", t=4), in_=pw[:].rearrange("p t c -> p c t"))
-        cos_sine(1)
-        turn_dt(2)
-        for t in range(4):
-            cos_angle(1, t)
+        turn_dt(1)
+        stage_q(0)
         nc.vector.quantize_mx(out=wvc[:].bitcast(FP8X4), scales=wvs[:], in_=gw[:])
         att_f = const.tile([P, TILES * HEADS], F32, name="att_f")
         nc.gpsimd.tensor_scalar(out=att_f[:], in0=att_b[:], scalar1=1.0, scalar2=0.0, op0=ALU.mult, op1=ALU.add)
@@ -420,6 +428,8 @@ def tile_transformeraggregator_pb_kernel(
         )
         nc.vector.quantize_mx(out=wc1[:].bitcast(FP8X4), scales=wcs[:], in_=wcg[:])
         cos_turns(1, 0)
+        cos_turns(1, 1)
+        cos_frac(1, 0)
         for r in range(4):
             nc.vector.tensor_copy(out=wcc[32 * r:32 * (r + 1), P * r:P * (r + 1)].bitcast(I32),
                                   in_=wc1[32 * r:32 * (r + 1), :].bitcast(I32))
@@ -427,7 +437,6 @@ def tile_transformeraggregator_pb_kernel(
             out=wcs4[:].bitcast(I32).rearrange("p (r c) -> p r c", r=4),
             in_=wcs[:].bitcast(I32).unsqueeze(1).to_broadcast([P, 4, P // 4]),
         )
-        cos_frac(1, 0)
         bias_rows = const.tile([P, NPP, D_OUT], F32, name="bias_rows")
 
         def bias_stage():
@@ -453,9 +462,9 @@ def tile_transformeraggregator_pb_kernel(
             nc.vector.quantize_mx(out=woc[:].bitcast(FP8X4), scales=wos[:], in_=gwo[:])
 
         extra = {1: [(bias_stage,)]}
-        for b in range(3, BATCHES):
-            extra.setdefault(4 * b - 10, []).append((repeat_dt, b))
-            extra.setdefault(4 * b - 8, []).append((turn_dt, b))
+        for b in range(2, BATCHES):
+            extra.setdefault(4 * b - 7, []).append((repeat_dt, b))
+            extra.setdefault(4 * b - 6, []).append((turn_dt, b))
         extra.setdefault(5, []).append((wo_stage,))
         for a in range(NPP):
             extra.setdefault(7 + a, []).append((root_stage, a))
@@ -477,8 +486,8 @@ def tile_transformeraggregator_pb_kernel(
             stage_t(s, 1)
             stage_t(s, 2)
             stage_t(s, 3)
-            if s + 1 < GROUPS:
-                cos_sine(s + 1)
+            if s + 3 < GROUPS:
+                cos_sine((s + 3) // 4, (s + 3) % 4)
             if s + NX - 1 < GROUPS:
                 load(s + NX - 1)
             for job in extra.get(s, ()):
@@ -490,20 +499,20 @@ def tile_transformeraggregator_pb_kernel(
             if s >= 2:
                 stage_m(s - 2, range(0, 4), True)
             jobs = []
-            if s % 2 == 0 and (s + 4 - s % 4) // 4 < BATCHES:
-                jobs.append((cos_frac, (s + 4 - s % 4) // 4, s % 4))
             if s > 1:
                 jobs.append((stage_q, s - 1, 0, 2))
-            if s + 7 < GROUPS:
-                jobs.append((cos_angle, (s + 7) // 4, (s + 7) % 4))
+            if s % 2:
+                jobs.append((cos_gather, s - 1))
+            if s + 4 < GROUPS:
+                jobs.append((cos_frac, (s + 4) // 4, (s + 4) % 4))
             if s > 1:
                 jobs.append((stage_q, s - 1, 1, 2))
             if s % 2:
                 jobs.append((cos_quantize, s - 1))
             if s >= 3:
                 jobs.append((stage_p, s - 3))
-            if s % 2 and (s + 3) // 4 + s % 4 // 3 < BATCHES:
-                jobs.append((cos_turns, (s + 3) // 4 + s % 4 // 3, (s + 1) % 4))
+            if s + 5 < GROUPS:
+                jobs.append((cos_turns, (s + 5) // 4, (s + 5) % 4))
             pieces = woven.get(s, [])
             for k in range(max(len(jobs), len(pieces))):
                 if k < len(jobs):

@@ -92,9 +92,15 @@ def tile_transformeraggregator_pb_kernel(
         load(1)
         att_b = const.tile([P, TILES * HEADS], BF16, name="att_b")
         nc.sync.dma_start(out=att_b[:], in_=att.rearrange("(p a) j h -> p (a j h)", a=NPP))
+        vec_row = const.tile([P, 4 * D_OUT], BF16, name="vec_row")
+        nc.vector.memset(vec_row[:], 0.0)
+        for k, vec in enumerate((wv_b, wo_b, ln_g, ln_b)):
+            nc.sync.dma_start(out=vec_row[0:1, D_OUT * k:D_OUT * (k + 1)], in_=vec.rearrange("(o c) -> o c", o=1))
+        ones = const.tile([P, P], BF16, name="ones")
+        nc.vector.memset(ones[:], 1.0)
+        vecs = const.tile([P, 4 * D_OUT], F32, name="vecs")
+        wvb, wob, lng, lnb = [vecs[:, D_OUT * k:D_OUT * (k + 1)] for k in range(4)]
         load(2)
-        wvb = const.tile([P, D_OUT], BF16, name="wvb")
-        nc.sync.dma_start(out=wvb[:], in_=wv_b.partition_broadcast(P))
 
         ident_f = const.tile([P, P], F32, name="ident_f")
         make_identity(nc, ident_f[:])
@@ -113,12 +119,6 @@ def tile_transformeraggregator_pb_kernel(
         nc.sync.dma_start(out=rootf[:], in_=root_node_feature.rearrange("(p a) c -> p a c", a=NPP))
         load(4)
         load(5)
-        wob = const.tile([P, D_OUT], BF16, name="wob")
-        nc.sync.dma_start(out=wob[:], in_=wo_b.partition_broadcast(P))
-        lng = const.tile([P, D_OUT], BF16, name="lng")
-        nc.sync.dma_start(out=lng[:], in_=ln_g.partition_broadcast(P))
-        lnb = const.tile([P, D_OUT], BF16, name="lnb")
-        nc.sync.dma_start(out=lnb[:], in_=ln_b.partition_broadcast(P))
 
         def transpose_row_tile(words):
             tp = tp_pool.tile([P, 4, P], F32, name="tp")
@@ -327,7 +327,7 @@ def tile_transformeraggregator_pb_kernel(
 
         def out_d(a):
             hid = spool.tile([P, D_OUT], F32, name="hid")
-            nc.vector.tensor_tensor(out=hid[:], in0=outs[a][0][:], in1=wob[:], op=ALU.add)
+            nc.vector.tensor_tensor(out=hid[:], in0=outs[a][0][:], in1=wob, op=ALU.add)
             outs[a] = [hid]
 
         def out_e(a):
@@ -352,15 +352,20 @@ def tile_transformeraggregator_pb_kernel(
             rstd = spool.tile([P, 1], F32, name="rstd")
             nc.gpsimd.tensor_tensor(out=rstd[:], in0=ve[:], in1=m_half[:], op=ALU.pow)
             res = spool.tile([P, D_OUT], F32, name="res")
-            nc.vector.scalar_tensor_tensor(out=res[:], in0=hid[:], scalar=mv[:, 0:1], in1=lng[:],
+            nc.vector.scalar_tensor_tensor(out=res[:], in0=hid[:], scalar=mv[:, 0:1], in1=lng,
                                            op0=ALU.subtract, op1=ALU.mult)
             outs[a] = [res, rstd]
 
         def out_i(a):
             res, rstd = outs[a]
-            nc.vector.scalar_tensor_tensor(out=res[:], in0=res[:], scalar=rstd[:], in1=lnb[:],
+            nc.vector.scalar_tensor_tensor(out=res[:], in0=res[:], scalar=rstd[:], in1=lnb,
                                            op0=ALU.mult, op1=ALU.add)
             nc.sync.dma_start(out=out_v[:, a, :], in_=res[:])
+
+        def spread_vectors():
+            tp = tp_pool.tile([P, 4 * D_OUT], F32, name="tp")
+            nc.tensor.matmul(tp[:], lhsT=ones[:], rhs=vec_row[:], start=True, stop=True)
+            nc.scalar.copy(out=vecs[:], in_=tp[:])
 
         nc.vector.tensor_tensor(
             out=dt_rows[:].rearrange("p (a j) -> p a j", a=NPP),
@@ -443,7 +448,7 @@ def tile_transformeraggregator_pb_kernel(
             for a in range(NPP):
                 nc.gpsimd.tensor_tensor(
                     out=bias_rows[:, a, :].rearrange("p (h c) -> p h c", h=HEADS),
-                    in0=wvb[:].rearrange("p (h c) -> p h c", h=HEADS),
+                    in0=wvb.rearrange("p (h c) -> p h c", h=HEADS),
                     in1=att_sum[:, HEADS * a:HEADS * (a + 1)].unsqueeze(2).to_broadcast([P, HEADS, D_HEAD]),
                     op=ALU.mult,
                 )
@@ -461,7 +466,7 @@ def tile_transformeraggregator_pb_kernel(
         def wo_quantize():
             nc.vector.quantize_mx(out=woc[:].bitcast(FP8X4), scales=wos[:], in_=gwo[:])
 
-        extra = {1: [(bias_stage,)]}
+        extra = {1: [(spread_vectors,)], 2: [(bias_stage,)]}
         for b in range(2, BATCHES):
             extra.setdefault(4 * b - 7, []).append((repeat_dt, b))
             extra.setdefault(4 * b - 6, []).append((turn_dt, b))

import math
from contextlib import ExitStack

import concourse.mybir as mybir
from concourse.masks import make_identity

F32 = mybir.dt.float32
BF16 = mybir.dt.bfloat16
I32 = mybir.dt.int32
U32 = mybir.dt.uint32
U8 = mybir.dt.uint8
FP8X4 = mybir.dt.float8_e4m3fn_x4
ALU = mybir.AluOpType
ACT = mybir.ActivationFunctionType
AX = mybir.AxisListType

P = 128
N_NODES, N_NEIGH, D_NODE, D_EDGE, D_TIME, HEADS, D_OUT = 512, 20, 384, 512, 128, 2, 128
D_HEAD = D_OUT // HEADS
K1 = D_NODE + D_EDGE + D_TIME
D_FEAT = D_NODE + D_EDGE
NPP = N_NODES // P
TILES = NPP * N_NEIGH
QUAD = 4
GROUPS = TILES // QUAD
GPN = N_NEIGH // QUAD
BATCH = 4
BATCHES = GROUPS // BATCH
SHARED = range(0, 20, 2)
PAIR = 2
NX = 6
LN_EPS = 1e-5
TWO_PI = 2.0 * math.pi

FLOPS = 2 * N_NODES * N_NEIGH * K1 * D_OUT + 2 * N_NODES * (D_OUT + D_NODE) * D_OUT


def tile_transformeraggregator_pb_kernel(
    tc, att, root_node_feature, root_ts, neighbor_ts, neighbor_node_feature, neighbor_edge_feature,
    time_w, time_b, wv_w, wv_b, wo_w, wo_b, ln_g, ln_b, out,
):
    nc = tc.nc
    with ExitStack() as ctx:
        const = ctx.enter_context(tc.tile_pool(name="const", bufs=1))
        xpool = ctx.enter_context(tc.tile_pool(name="xpool", bufs=1))
        gpool = ctx.enter_context(tc.tile_pool(name="gpool", bufs=3))
        cpool = ctx.enter_context(tc.tile_pool(name="cpool", bufs=2))
        spool = ctx.enter_context(tc.tile_pool(name="spool", bufs=2))
        tp_pool = ctx.enter_context(tc.psum_pool(name="tp", bufs=4))
        mo_pool = ctx.enter_context(tc.psum_pool(name="mo", bufs=3))
        ac_pool = ctx.enter_context(tc.psum_pool(name="ac", bufs=1))
        ctx.enter_context(tc.manual_schedule())

        node_v = neighbor_node_feature.rearrange("(p a) j c -> p (a j) c", a=NPP)
        edge_v = neighbor_edge_feature.rearrange("(p a) j c -> p (a j) c", a=NPP)
        out_v = out.rearrange("(p a) c -> p a c", a=NPP)

        warm = const.tile([P, 1], F32, name="warm")
        nc.vector.memset(warm[:], 0.0)
        tb8 = const.tile([P, P], BF16, name="tb8")
        nc.vector.memset(tb8[:], 0.0)
        nts = const.tile([P, TILES], BF16, name="nts")
        nc.scalar.dma_start(out=nts[:], in_=neighbor_ts.rearrange("(p a) j -> p (a j)", a=NPP))
        rts = const.tile([P, NPP], BF16, name="rts")
        nc.scalar.dma_start(out=rts[:], in_=root_ts.rearrange("(p a) -> p a", a=NPP))
        nc.scalar.dma_start(
            out=tb8[0:4, :].rearrange("t (r q) -> t r q", r=4),
            in_=time_w.rearrange("(t q) o -> t o q", t=4).to_broadcast([4, 4, 32]),
        )
        nc.scalar.dma_start(
            out=tb8[4:8, :].rearrange("t (r q) -> t r q", r=4),
            in_=time_b.rearrange("(t o q) -> t o q", t=4, o=1).to_broadcast([4, 4, 32]),
        )
        warm_out = const.tile([P, 1], F32, name="warm_out")
        nc.scalar.activation(out=warm_out[:], in_=warm[:], func=ACT.Sin)

        xq = [xpool.tile([P, QUAD, K1], BF16, name="xq%d" % k) for k in range(NX)]

        def load(g, rows=slice(0, QUAD)):
            x = xq[g % NX]
            tiles = slice(QUAD * g + rows.start, QUAD * g + rows.stop)
            nc.sync.dma_start(out=x[:, rows, 0:D_NODE], in_=node_v[:, tiles, :])
            nc.sync.dma_start(out=x[:, rows, D_NODE:D_FEAT], in_=edge_v[:, tiles, :])

        load(0, slice(0, 1))
        load(0, slice(1, 2))
        load(0, slice(2, 4))
        wvz = const.tile([P, K1], BF16, name="wvz")
        nc.sync.dma_start(out=wvz[:, 0:D_FEAT], in_=wv_w[:, 0:D_FEAT])
        wcos = const.tile([P, D_TIME], BF16, name="wcos")
        nc.sync.dma_start(out=wcos[:], in_=wv_w[:, D_FEAT:K1])
        load(1)
        att_b = const.tile([P, TILES * HEADS], BF16, name="att_b")
        nc.sync.dma_start(out=att_b[:], in_=att.rearrange("(p a) j h -> p (a j h)", a=NPP))
        vec_row = const.tile([P, 4 * D_OUT], BF16, name="vec_row")
        nc.vector.memset(vec_row[:], 0.0)
        for k, vec in enumerate((wv_b, wo_b, ln_g, ln_b)):
            nc.sync.dma_start(out=vec_row[0:1, D_OUT * k:D_OUT * (k + 1)], in_=vec.rearrange("(o c) -> o c", o=1))
        ones = const.tile([P, P], BF16, name="ones")
        nc.vector.memset(ones[:], 1.0)
        vecs = const.tile([P, 4 * D_OUT], F32, name="vecs")
        wvb, wob, lng, lnb = [vecs[:, D_OUT * k:D_OUT * (k + 1)] for k in range(4)]
        load(2)

        ident_f = const.tile([P, P], F32, name="ident_f")
        make_identity(nc, ident_f[:])
        ident_b = const.tile([P, P], BF16, name="ident_b")
        make_identity(nc, ident_b[:])
        nc.gpsimd.memset(xq[0][:, :, D_FEAT:K1], 0.0)
        nc.gpsimd.memset(wvz[:, D_FEAT:K1], 0.0)
        for k in range(1, NX):
            nc.gpsimd.memset(xq[k][:, :, D_FEAT:K1], 0.0)
        m_half = const.tile([P, 1], F32, name="m_half")
        nc.gpsimd.memset(m_half[:], -0.5)
        load(3)
        wo_sb = const.tile([P, D_OUT + D_NODE], BF16, name="wo_sb")
        nc.sync.dma_start(out=wo_sb[:], in_=wo_w)
        rootf = const.tile([P, NPP, D_NODE], BF16, name="rootf")
        nc.sync.dma_start(out=rootf[:], in_=root_node_feature.rearrange("(p a) c -> p a c", a=NPP))
        load(4)
        load(5)

        def transpose_row_tile(words):
            tp = tp_pool.tile([P, 4, P], F32, name="tp")
            for c in range(4):
                nc.tensor.transpose(tp[:, c, :], words[:, P * c:P * (c + 1)], ident_f[:])
            return tp

        def evacuate(dst_words, tp):
            nc.scalar.copy(
                out=dst_words.rearrange("p (g w u) -> p g w u", g=2, u=2),
                in_=tp[:].rearrange("p (g u) w -> p g w u", g=2),
            )

        dt_rows = const.tile([P, TILES], F32, name="dt_rows")
        dtq = const.tile([P, GROUPS * P], F32, name="dtq")
        TB = QUAD * BATCH
        dt_reps = {}

        def repeat_dt(b):
            dt_rep = cpool.tile([P, TB, 32], F32, name="dt_rep", bufs=2)
            src = dt_rows[:, TB * b:TB * (b + 1)].unsqueeze(2).to_broadcast([P, TB, 32])
            if b == 0:
                nc.vector.tensor_copy(out=dt_rep[:], in_=src)
            else:
                nc.gpsimd.tensor_scalar(out=dt_rep[:], in0=src, scalar1=1.0, scalar2=0.0, op0=ALU.mult, op1=ALU.add)
            dt_reps[b] = dt_rep

        def turn_dt(b):
            tpd = tp_pool.tile([P, 4, P], F32, name="tp")
            for q in range(BATCH):
                nc.tensor.transpose(
                    tpd[:, q, :], dt_reps[b][:, QUAD * q:QUAD * (q + 1), :].rearrange("p i c -> p (i c)"), ident_f[:]
                )
            dst, src = dtq[:, 512 * b:512 * (b + 1)], tpd[:].rearrange("p q w -> p (q w)")
            if b == 0:
                nc.vector.tensor_copy(out=dst, in_=src)
            else:
                nc.scalar.copy(out=dst, in_=src)

        a_q = const.tile([P, 4], F32, name="a_q")
        b_q = const.tile([P, 4], F32, name="b_q")
        b_2 = const.tile([P, 4], F32, name="b_2")
        turns = {}
        fracs = {}
        planes = {}
        cos_codes = {}

        def cos_turns(b, t):
            cols = slice(512 * b, 512 * (b + 1))
            tn = cpool.tile([P, 512], I32, name="turns", bufs=3)
            nc.vector.tensor_scalar(out=tn[:], in0=dtq[:, cols], scalar1=a_q[:, t:t + 1],
                                    scalar2=b_q[:, t:t + 1], op0=ALU.mult, op1=ALU.add)
            turns[b, t] = tn

        def cos_frac(b, t):
            cols = slice(512 * b, 512 * (b + 1))
            fr = cpool.tile([P, 512], F32, name="frac", bufs=3)
            nc.vector.scalar_tensor_tensor(out=fr[:], in0=dtq[:, cols], scalar=a_q[:, t:t + 1],
                                           in1=turns[b, t][:], op0=ALU.mult, op1=ALU.subtract)
            fracs[b, t] = fr

        def cos_sine(b, t):
            if t == 0:
                pl_new = cpool.tile([P, 4, 512], BF16, name="planes")
                planes[b] = pl_new
            nc.scalar.activation(out=planes[b][:, t, :], in_=fracs[b, t][:], func=ACT.Sin,
                                 bias=b_2[:, t:t + 1], scale=TWO_PI)

        cos_groups = {}

        def cos_gather(g):
            b, c0 = g // BATCH, P * (g % BATCH)
            cos_g = cpool.tile([P, PAIR * 512], BF16, name="cos_g", align_bytes=64)
            nc.vector.tensor_copy(
                out=cos_g[:].rearrange("p (c i t) -> p c t i", i=4, t=4),
                in_=planes[b][:, :, c0:c0 + PAIR * P].rearrange("p t (c i) -> p c t i", i=4),
            )
            cos_groups[g] = cos_g

        def cos_quantize(g):
            cc = cpool.tile([P, PAIR * P], U32, name="cc", align_bytes=64, bufs=3)
            cs = cpool.tile([P, PAIR * P], U8, name="cs", align_bytes=64, bufs=3)
            nc.vector.quantize_mx(out=cc[:].bitcast(FP8X4), scales=cs[:], in_=cos_groups[g][:])
            for k in range(PAIR):
                cos_codes[g + k] = (cc[:, P * k:P * (k + 1)], cs[:, P * k:P * (k + 1)])

        grouped = {}
        codes = {}
        sums = {}
        prods = {}
        accs = {}
        g2s = {}

        def stage_t(g, r):
            if r == 0:
                gq_new = gpool.tile([P, QUAD * K1], BF16, name="gq", align_bytes=64)
                grouped[g] = gq_new
            tp = transpose_row_tile(xq[g % NX][:].bitcast(F32)[:, r, :])
            evacuate(grouped[g][:].bitcast(F32)[:, 512 * r:512 * (r + 1)], tp)

        def stage_q(g, k=0, pieces=1):
            if k == 0:
                cq_new = gpool.tile([P, QUAD * 256], U32, name="cq", align_bytes=64, bufs=4)
                sq_new = gpool.tile([P, QUAD * 256], U8, name="sq", align_bytes=64, bufs=4)
                codes[g] = (cq_new, sq_new)
            cq, sq = codes[g]
            wc = QUAD * 256 // pieces
            nc.vector.quantize_mx(
                out=cq[:, wc * k:wc * (k + 1)].bitcast(FP8X4),
                scales=sq[:, wc * k:wc * (k + 1)],
                in_=grouped[g][:, 4 * wc * k:4 * wc * (k + 1)],
            )

        def stage_m(g, rows=range(QUAD), cos=True):
            cq, sq = codes[g]
            cc, cs = cos_codes[g]
            if cos:
                mo_new = mo_pool.tile([P, QUAD, D_OUT], F32, name="mo")
                sums[g] = mo_new
            mo = sums[g]
            if cos:
                nc.tensor.matmul_mx(
                    out=mo[:].rearrange("p r c -> p (r c)"),
                    lhsT=cc.bitcast(FP8X4), lhsT_scale=cs,
                    rhs=wcc[:].bitcast(FP8X4), rhs_scale=wcs4[:],
                    start=True, stop=False,
                )
            for r in rows:
                for ps in range(2):
                    s = 256 * r + P * ps
                    nc.tensor.matmul_mx(
                        out=mo[:, r, :],
                        lhsT=cq[:, s:s + P].bitcast(FP8X4), lhsT_scale=sq[:, s:s + P],
                        rhs=wvc[:, P * ps:P * (ps + 1)].bitcast(FP8X4), rhs_scale=wvs[:, P * ps:P * (ps + 1)],
                        start=False, stop=(r == QUAD - 1 and ps == 1),
                    )

        def weigh_half(g):
            prod = gpool.tile([P, QUAD * D_OUT], F32, name="prod", bufs=4)
            prods[g] = prod
            for i in range(2 * HEADS):
                w = QUAD * HEADS * g + i
                nc.scalar.activation(
                    out=prod[:, D_HEAD * i:D_HEAD * (i + 1)],
                    in_=sums[g][:, i // HEADS, D_HEAD * (i % HEADS):D_HEAD * (i % HEADS + 1)],
                    func=ACT.Copy, scale=att_f[:, w:w + 1],
                )

        def stage_p(g):
            if g in SHARED:
                for i in range(2 * HEADS):
                    part = prods[g][:, D_HEAD * i:D_HEAD * (i + 1)]
                    w = QUAD * HEADS * g + 2 * HEADS + i
                    nc.vector.scalar_tensor_tensor(
                        out=part, in0=sums[g][:, 2 + i // HEADS, D_HEAD * (i % HEADS):D_HEAD * (i % HEADS + 1)],
                        scalar=att_f[:, w:w + 1], in1=part, op0=ALU.mult, op1=ALU.add,
                    )
                return
            prod = gpool.tile([P, QUAD * D_OUT], F32, name="prod", bufs=4)
            nc.vector.tensor_tensor(
                out=prod[:].rearrange("p (s c) -> p s c", c=D_HEAD),
                in0=sums[g][:].rearrange("p r (h c) -> p (r h) c", h=HEADS),
                in1=att_b[:, QUAD * HEADS * g:QUAD * HEADS * (g + 1)].unsqueeze(2).to_broadcast(
                    [P, QUAD * HEADS, D_HEAD]),
                op=ALU.mult,
            )
            prods[g] = prod

        def stage_s(g, rows=range(QUAD)):
            a = g // GPN
            if g % GPN == 0 and rows[0] == 0:
                acc_new = ac_pool.tile([P, P], F32, name="acc")
                accs[a] = acc_new
                nc.tensor.matmul(acc_new[:], lhsT=bias_rows[:, a, :], rhs=ident_f[:], is_transpose=True,
                                 start=True, stop=False)
            for r in range(2) if g in SHARED else rows:
                nc.tensor.matmul(accs[a][:], lhsT=prods[g][:, D_OUT * r:D_OUT * (r + 1)], rhs=ident_f[:],
                                 is_transpose=True, start=False,
                                 stop=(g % GPN == GPN - 1 and r == (1 if g in SHARED else QUAD - 1)))

        def root_stage(a):
            ps2 = tp_pool.tile([P, 3, P], BF16, name="tp")
            for c in range(3):
                nc.tensor.transpose(ps2[:, c, :], rootf[:, a, P * c:P * (c + 1)], ident_b[:])
            g2 = const.tile([P, P, 4], BF16, name="g2_%d" % a, align_bytes=64)
            nc.scalar.copy(out=g2[:, :, 1:4], in_=ps2[:].rearrange("p t w -> p w t"))
            g2s[a] = g2

        outs = {}

        def out_a(a):
            nc.scalar.copy(out=g2s[a][:, :, 0], in_=accs[a][:])

        def out_b(a):
            c2 = spool.tile([P, P], U32, name="c2", align_bytes=64)
            s2 = spool.tile([P, P], U8, name="s2", align_bytes=64)
            nc.vector.quantize_mx(out=c2[:].bitcast(FP8X4), scales=s2[:], in_=g2s[a][:].rearrange("p w t -> p (w t)"))
            outs[a] = [c2, s2]

        def out_c(a):
            c2, s2 = outs[a]
            o2 = mo_pool.tile([P, D_OUT], F32, name="mo")
            nc.tensor.matmul_mx(out=o2[:], lhsT=c2[:].bitcast(FP8X4), lhsT_scale=s2[:],
                                rhs=woc[:].bitcast(FP8X4), rhs_scale=wos[:], start=True, stop=True)
            outs[a] = [o2]

        def out_d(a):
            hid = spool.tile([P, D_OUT], F32, name="hid")
            nc.vector.tensor_tensor(out=hid[:], in0=outs[a][0][:], in1=wob, op=ALU.add)
            outs[a] = [hid]

        def out_e(a):
            hid = outs[a][0]
            nc.vector.tensor_scalar_max(out=hid[:], in0=hid[:], scalar1=0.0)

        def out_f(a):
            hid = outs[a][0]
            stats = spool.tile([P, 6], F32, name="stats")
            nc.vector.bn_stats(out=stats[:], in_=hid[:])
            outs[a].append(stats)

        def out_g(a):
            mv = spool.tile([P, 2], F32, name="mv")
            nc.vector.bn_aggr(out=mv[:], in_=outs[a][1][:])
            outs[a].append(mv)

        def out_h(a):
            hid, stats, mv = outs[a]
            ve = spool.tile([P, 1], F32, name="ve")
            nc.vector.tensor_scalar_add(out=ve[:], in0=mv[:, 1:2], scalar1=LN_EPS)
            rstd = spool.tile([P, 1], F32, name="rstd")
            nc.gpsimd.tensor_tensor(out=rstd[:], in0=ve[:], in1=m_half[:], op=ALU.pow)
            res = spool.tile([P, D_OUT], F32, name="res")
            nc.vector.scalar_tensor_tensor(out=res[:], in0=hid[:], scalar=mv[:, 0:1], in1=lng,
                                           op0=ALU.subtract, op1=ALU.mult)
            outs[a] = [res, rstd]

        def out_i(a):
            res, rstd = outs[a]
            nc.vector.scalar_tensor_tensor(out=res[:], in0=res[:], scalar=rstd[:], in1=lnb,
                                           op0=ALU.mult, op1=ALU.add)
            nc.sync.dma_start(out=out_v[:, a, :], in_=res[:])

        def spread_vectors():
            tp = tp_pool.tile([P, 4 * D_OUT], F32, name="tp")
            nc.tensor.matmul(tp[:], lhsT=ones[:], rhs=vec_row[:], start=True, stop=True)
            nc.scalar.copy(out=vecs[:], in_=tp[:])

        nc.vector.tensor_tensor(
            out=dt_rows[:].rearrange("p (a j) -> p a j", a=NPP),
            in0=rts[:].unsqueeze(2).to_broadcast([P, NPP, N_NEIGH]),
            in1=nts[:].rearrange("p (a j) -> p a j", a=NPP),
            op=ALU.subtract,
        )
        repeat_dt(0)
        repeat_dt(1)
        turn_dt(0)
        ps8 = ac_pool.tile([P, P], BF16, name="acc")
        nc.tensor.transpose(ps8[:], tb8[:], ident_b[:])
        nc.vector.tensor_scalar(out=a_q[:], in0=ps8[:, 0:4], scalar1=1.0 / TWO_PI, scalar2=None, op0=ALU.mult)
        nc.vector.tensor_scalar(out=b_q[:], in0=ps8[:, 4:8], scalar1=1.0 / TWO_PI, scalar2=0.25,
                                op0=ALU.mult, op1=ALU.add)
        nc.vector.tensor_scalar(out=b_2[:], in0=ps8[:, 4:8], scalar1=0.5 * math.pi, scalar2=None, op0=ALU.add)
        cos_turns(0, 0)
        cos_turns(0, 1)
        cos_frac(0, 0)
        cos_turns(0, 2)
        cos_frac(0, 1)
        cos_turns(0, 3)
        cos_frac(0, 2)
        stage_t(0, 0)
        stage_t(0, 1)
        cos_sine(0, 0)
        stage_t(0, 2)
        cos_sine(0, 1)
        stage_t(0, 3)
        cos_frac(0, 3)
        cos_sine(0, 2)
        cos_sine(0, 3)

        wvc = const.tile([P, 256], U32, name="wvc", align_bytes=64)
        wvs = const.tile([P, 256], U8, name="wvs", align_bytes=64)
        gw = const.tile([P, K1], BF16, name="gw", align_bytes=64)
        wcr = const.tile([P, 4, 4, 32], BF16, name="wcr")
        wcg = const.tile([P, 512], BF16, name="wcg", align_bytes=64)
        wc1 = const.tile([P, P], U32, name="wc1", align_bytes=64)
        wcs = const.tile([P, P], U8, name="wcs", align_bytes=64)
        nc.gpsimd.memset(wcs[:].bitcast(I32), 0)
        wcs4 = const.tile([P, 512], U8, name="wcs4", align_bytes=64)
        wcc = const.tile([P, 512], U32, name="wcc", align_bytes=64)
        nc.gpsimd.memset(wcc[:].bitcast(F32), 0.0)
        nc.vector.tensor_copy(
            out=wcr[:],
            in_=wcos[:].rearrange("p (t q) -> p t q", t=4).unsqueeze(2).to_broadcast([P, 4, 4, 32]),
        )
        tpw = transpose_row_tile(wvz[:].bitcast(F32))
        evacuate(gw[:].bitcast(F32), tpw)
        pw = mo_pool.tile([P, 4, P], BF16, name="mo")
        for t in range(4):
            nc.tensor.transpose(pw[:, t, :], wcr[:, t, :, :].rearrange("p r q -> p (r q)"), ident_b[:])
        nc.scalar.copy(out=wcg[:].rearrange("p (c t) -> p c t", t=4), in_=pw[:].rearrange("p t c -> p c t"))
        turn_dt(1)
        stage_q(0)
        nc.vector.quantize_mx(out=wvc[:].bitcast(FP8X4), scales=wvs[:], in_=gw[:])
        att_f = const.tile([P, TILES * HEADS], F32, name="att_f")
        nc.gpsimd.tensor_scalar(out=att_f[:], in0=att_b[:], scalar1=1.0, scalar2=0.0, op0=ALU.mult, op1=ALU.add)
        att_sum = const.tile([P, NPP * HEADS], F32, name="att_sum")
        nc.vector.tensor_reduce(
            out=att_sum[:].rearrange("p (a h) -> p a h", a=NPP),
            in_=att_b[:].rearrange("p (a j h) -> p a h j", a=NPP, j=N_NEIGH),
            axis=AX.X, op=ALU.add,
        )
        nc.vector.quantize_mx(out=wc1[:].bitcast(FP8X4), scales=wcs[:], in_=wcg[:])
        cos_turns(1, 0)
        cos_turns(1, 1)
        cos_frac(1, 0)
        for r in range(4):
            nc.vector.tensor_copy(out=wcc[32 * r:32 * (r + 1), P * r:P * (r + 1)].bitcast(I32),
                                  in_=wc1[32 * r:32 * (r + 1), :].bitcast(I32))
        nc.vector.tensor_copy(
            out=wcs4[:].bitcast(I32).rearrange("p (r c) -> p r c", r=4),
            in_=wcs[:].bitcast(I32).unsqueeze(1).to_broadcast([P, 4, P // 4]),
        )
        bias_rows = const.tile([P, NPP, D_OUT], F32, name="bias_rows")

        def bias_stage():
            for a in range(NPP):
                nc.gpsimd.tensor_tensor(
                    out=bias_rows[:, a, :].rearrange("p (h c) -> p h c", h=HEADS),
                    in0=wvb.rearrange("p (h c) -> p h c", h=HEADS),
                    in1=att_sum[:, HEADS * a:HEADS * (a + 1)].unsqueeze(2).to_broadcast([P, HEADS, D_HEAD]),
                    op=ALU.mult,
                )

        woc = const.tile([P, P], U32, name="woc", align_bytes=64)
        wos = const.tile([P, P], U8, name="wos", align_bytes=64)
        gwo = const.tile([P, 512], BF16, name="gwo", align_bytes=64)

        def wo_stage():
            pwo = tp_pool.tile([P, 4, P], BF16, name="tp")
            for t in range(4):
                nc.tensor.transpose(pwo[:, t, :], wo_sb[:, P * t:P * (t + 1)], ident_b[:])
            nc.scalar.copy(out=gwo[:].rearrange("p (c t) -> p c t", t=4), in_=pwo[:].rearrange("p t c -> p c t"))

        def wo_quantize():
            nc.vector.quantize_mx(out=woc[:].bitcast(FP8X4), scales=wos[:], in_=gwo[:])

        extra = {1: [(spread_vectors,)], 2: [(bias_stage,)]}
        for b in range(2, BATCHES):
            extra.setdefault(4 * b - 7, []).append((repeat_dt, b))
            extra.setdefault(4 * b - 6, []).append((turn_dt, b))
        extra.setdefault(5, []).append((wo_stage,))
        for a in range(NPP):
            extra.setdefault(7 + a, []).append((root_stage, a))
        woven = {}
        sums_first = {}
        for a in range(NPP - 1):
            s0 = GPN * (a + 1) + 4
            woven.setdefault(s0, []).extend([None, None, None, (out_b, a)])
            sums_first[s0 + 1] = a
            woven.setdefault(s0 + 2, []).extend([(out_d, a), (out_e, a), (out_f, a), (out_g, a), (out_h, a), (out_i, a)])
        woven.setdefault(6, []).append((wo_quantize,))
        for s in range(1, GROUPS):
            pooled = (s - 4) // GPN - 1 if s >= GPN + 4 and (s - 4) % GPN == 0 else None
            if pooled is not None:
                out_a(pooled)
            stage_t(s, 0)
            if s - 3 in SHARED:
                weigh_half(s - 3)
            stage_t(s, 1)
            stage_t(s, 2)
            stage_t(s, 3)
            if s + 3 < GROUPS:
                cos_sine((s + 3) // 4, (s + 3) % 4)
            if s + NX - 1 < GROUPS:
                load(s + NX - 1)
            for job in extra.get(s, ()):
                job[0](*job[1:])
            if s >= 4:
                stage_s(s - 4, range(0, 4))
            if s in sums_first:
                out_c(sums_first[s])
            if s >= 2:
                stage_m(s - 2, range(0, 4), True)
            jobs = []
            if s > 1:
                jobs.append((stage_q, s - 1, 0, 2))
            if s % 2:
                jobs.append((cos_gather, s - 1))
            if s + 4 < GROUPS:
                jobs.append((cos_frac, (s + 4) // 4, (s + 4) % 4))
            if s > 1:
                jobs.append((stage_q, s - 1, 1, 2))
            if s % 2:
                jobs.append((cos_quantize, s - 1))
            if s >= 3:
                jobs.append((stage_p, s - 3))
            if s + 5 < GROUPS:
                jobs.append((cos_turns, (s + 5) // 4, (s + 5) % 4))
            pieces = woven.get(s, [])
            for k in range(max(len(jobs), len(pieces))):
                if k < len(jobs):
                    jobs[k][0](*jobs[k][1:])
                if k < len(pieces) and pieces[k]:
                    pieces[k][0](*pieces[k][1:])

        last = GROUPS - 1
        prev = NPP - 2
        stage_q(last, 0, 4)
        stage_s(last - 3)
        stage_q(last, 1, 4)
        if last - 2 in SHARED:
            weigh_half(last - 2)
        stage_p(last - 2)
        stage_m(last - 1)
        stage_q(last, 2, 4)
        out_c(prev)
        stage_q(last, 3, 4)
        stage_s(last - 2)
        if last - 1 in SHARED:
            weigh_half(last - 1)
        stage_p(last - 1)
        stage_m(last)
        out_d(prev)
        out_e(prev)
        stage_s(last - 1)
        out_f(prev)
        out_g(prev)
        if last in SHARED:
            weigh_half(last)
        stage_p(last)
        out_h(prev)
        stage_s(last)
        out_i(prev)
        for piece in (out_a, out_b, out_c, out_d, out_e, out_f, out_g, out_h, out_i):
            piece(NPP - 1)
